import numpy as np
import ml_dtypes


def mxq(x, axis, fmt="e4m3"):
    dtype, down = {"e4m3": (ml_dtypes.float8_e4m3fn, 7), "e5m2": (ml_dtypes.float8_e5m2, 14)}[fmt]
    v = np.moveaxis(np.asarray(x, np.float32).astype(ml_dtypes.bfloat16).astype(np.float64), axis, -1)
    blocks = v.reshape(v.shape[:-1] + (-1, 32))
    amax = np.abs(blocks).max(-1, keepdims=True)
    byte = np.maximum(np.where(amax > 0, np.frexp(amax)[1] - 1 + 127, 0) - down, 1)
    scale = np.exp2(byte - 127.0)
    codes = (blocks / scale).astype(np.float32).astype(dtype).astype(np.float64)
    return np.moveaxis((codes * scale).reshape(v.shape), -1, axis)


WIDE = False


def mx_kscale(k):
    if not WIDE:
        return np.ones(k)
    levels = np.array([10, -10, 5, -5, 0])
    a = np.random.permutation(np.resize(levels, k // 512 * 4)).reshape(k // 512, 4)
    idx = np.arange(k)
    return np.exp2(a[idx // 512, idx % 128 // 32])


BF16 = ml_dtypes.bfloat16


def bf(x):
    return np.asarray(x, np.float32).astype(BF16)


def f64(x):
    return np.asarray(x).astype(np.float64)


B, I, H = 4096, 512, 512
EPS = 1e-5


def ln(v):
    mu = v.mean(-1, keepdims=True)
    var = np.square(v - mu).mean(-1, keepdims=True)
    return (v - mu) / np.sqrt(var + EPS)


def sigmoid(v):
    return 1.0 / (1.0 + np.exp(-v))


def setup_inputs():
    s = mx_kscale(I)
    return {"x": bf(np.random.standard_normal((B, I)) * s),
            "h": bf(np.random.standard_normal((B, H))),
            "r": bf(sigmoid(np.sqrt(2.0) * np.random.standard_normal((B, H)))),
            "z": bf(sigmoid(np.sqrt(2.0) * np.random.standard_normal((B, H)))),
            "W_in": bf(np.random.standard_normal((H, I)) / np.sqrt(I) / s),
            "b_in": bf(np.random.standard_normal(H) * 0.5),
            "W_hn": bf(np.random.standard_normal((H, H)) / np.sqrt(H)),
            "b_hn": bf(np.random.standard_normal(H) * 0.5)}


def reference(x, h, r, z, W_in, b_in, W_hn, b_hn):
    h = f64(h)
    r, z = f64(r), f64(z)
    i_n = ln((mxq(f64(x), 1, "e4m3") @ mxq(f64(W_in), 1, "e4m3").T) + f64(b_in))
    h_n = ln((mxq(h, 1, "e4m3") @ mxq(f64(W_hn), 1, "e4m3").T) + f64(b_hn))
    n = np.tanh(i_n + r * h_n)
    return (1.0 - z) * n + z * h

@@ -1,0 +1,277 @@
+from contextlib import ExitStack
+
+import concourse.mybir as mybir
+from concourse.masks import make_identity
+
+F32 = mybir.dt.float32
+BF16 = mybir.dt.bfloat16
+U32 = mybir.dt.uint32
+U8 = mybir.dt.uint8
+FP8X4 = mybir.dt.float8_e4m3fn_x4
+ALU = mybir.AluOpType
+ACT = mybir.ActivationFunctionType
+
+P = 128
+B = 4096
+K = 512
+H = 512
+NT = B // P
+GT = 4
+NG = NT // GT
+GW = GT * H
+EPS = 1e-5
+
+FLOPS = 2 * 2 * B * K * H
+
+GP9 = False
+PIN = False
+
+
+def tile_layernormgrucell_pb_t_kernel(tc, x, h, r, z, W_in, b_in, W_hn, b_hn, out):
+    nc = tc.nc
+    xv = x.rearrange("(p t) k -> p (t k)", t=NT)
+    hv = h.rearrange("(p t) k -> p (t k)", t=NT)
+    rv = r.rearrange("(p t) k -> p (t k)", t=NT)
+    zv = z.rearrange("(p t) k -> p (t k)", t=NT)
+    ov = out.rearrange("(p t) k -> p (t k)", t=NT)
+
+    with ExitStack() as ctx:
+        const = ctx.enter_context(tc.tile_pool(name="const", bufs=1))
+        xp = ctx.enter_context(tc.tile_pool(name="xp", bufs=3))
+        hp = ctx.enter_context(tc.tile_pool(name="hp", bufs=5))
+        rp = ctx.enter_context(tc.tile_pool(name="rp", bufs=4))
+        zp = ctx.enter_context(tc.tile_pool(name="zp", bufs=5))
+        gp = ctx.enter_context(tc.tile_pool(name="gp", bufs=2))
+        cp = ctx.enter_context(tc.tile_pool(name="cp", bufs=2))
+        up = ctx.enter_context(tc.tile_pool(name="up", bufs=2))
+        npool = ctx.enter_context(tc.tile_pool(name="npool", bufs=2))
+        op = ctx.enter_context(tc.tile_pool(name="op", bufs=2))
+        sp = ctx.enter_context(tc.tile_pool(name="sp", bufs=3))
+        jp = ctx.enter_context(tc.tile_pool(name="jp", bufs=2))
+        pti = ctx.enter_context(tc.psum_pool(name="pti", bufs=4))
+        pac = ctx.enter_context(tc.psum_pool(name="pac", bufs=4))
+        if PIN:
+            ctx.enter_context(tc.manual_schedule())
+
+        st = {}
+
+        def load(g):
+            cols = slice(g * GW, (g + 1) * GW)
+            x_sb = xp.tile([P, GW], BF16)
+            nc.sync.dma_start(out=x_sb[:], in_=xv[:, cols])
+            h_sb = hp.tile([P, GW], BF16)
+            nc.sync.dma_start(out=h_sb[:], in_=hv[:, cols])
+            r_sb = rp.tile([P, GW], BF16)
+            nc.sync.dma_start(out=r_sb[:], in_=rv[:, cols])
+            z_sb = zp.tile([P, GW], BF16)
+            nc.sync.dma_start(out=z_sb[:], in_=zv[:, cols])
+            st[("x", g)] = x_sb
+            st[("h", g)] = h_sb
+            st[("r", g)] = r_sb
+            st[("z", g)] = z_sb
+
+        ident = const.tile([P, P], F32)
+        make_identity(nc, ident[:])
+        mhalf = const.tile([P, 2 * GT], F32)
+        nc.gpsimd.memset(mhalf[:], -0.5)
+
+        w_raw = []
+        for i, w in enumerate((W_in, W_hn)):
+            w_sb = const.tile([P, 4 * K], BF16, name="w_sb%d" % i)
+            nc.sync.dma_start(
+                out=w_sb[:].rearrange("p (a k) -> p a k", a=4),
+                in_=w.rearrange("(a p) k -> p a k", p=P),
+            )
+            w_raw.append(w_sb)
+            if i == 0:
+                load(0)
+        bias = []
+        for i, b in enumerate((b_in, b_hn)):
+            b_sb = const.tile([P, H], BF16, name="b_sb%d" % i)
+            nc.gpsimd.dma_start(out=b_sb[:], in_=b.partition_broadcast(P))
+            bias.append(b_sb)
+
+        w_codes = []
+        w_scales = []
+        for i in range(2):
+            wf = w_raw[i][:].bitcast(F32)
+            wg = const.tile([P, 4 * H], BF16, name="wg%d" % i, align_bytes=64)
+            wgf = wg[:].bitcast(F32)
+            for hb in range(2):
+                wt = pti.tile([P, 512], F32, tag="ti")
+                for u in range(2):
+                    for jl in range(2):
+                        a = 2 * hb + jl
+                        nc.tensor.transpose(
+                            wt[:, u * 256 + jl * P : u * 256 + (jl + 1) * P],
+                            wf[:, a * 256 + u * P : a * 256 + (u + 1) * P],
+                            ident[:],
+                        )
+                nc.vector.tensor_copy(
+                    out=wgf[:, hb * 512 : (hb + 1) * 512].rearrange("p (n u) -> p n u", u=2),
+                    in_=wt[:].rearrange("p (u n) -> p n u", u=2),
+                )
+            wc = const.tile([P, H], U32, name="wc%d" % i, align_bytes=64)
+            ws = const.tile([P, H], U8, name="ws%d" % i, align_bytes=64)
+            nc.vector.quantize_mx(out=wc[:].bitcast(FP8X4), scales=ws[:], in_=wg[:])
+            w_codes.append(wc)
+            w_scales.append(ws)
+
+        def stage_b(g):
+            xf = st[("x", g)][:].bitcast(F32)
+            hf = st[("h", g)][:].bitcast(F32)
+            grp = gp.tile([P, 2 * GT * 512], BF16, align_bytes=64)
+            grpv = grp[:].bitcast(F32).rearrange("p (o t i u) -> p o t i u", o=2, t=GT, u=2)
+            for t in range(GT):
+                ti = pti.tile([P, 512], F32, tag="ti")
+                for o, src in enumerate((xf, hf)):
+                    for u in range(2):
+                        nc.tensor.transpose(
+                            ti[:, (o * 2 + u) * P : (o * 2 + u + 1) * P],
+                            src[:, t * 256 + u * P : t * 256 + (u + 1) * P],
+                            ident[:],
+                        )
+                nc.scalar.copy(
+                    out=grpv[:, :, t],
+                    in_=ti[:].rearrange("p (o u i) -> p o i u", o=2, u=2),
+                )
+            st[("grp", g)] = grp
+
+        def stage_q(g):
+            codes = cp.tile([P, 2 * GT * P], U32, align_bytes=64)
+            scl = cp.tile([P, 2 * GT * P], U8, align_bytes=64)
+            nc.vector.quantize_mx(out=codes[:].bitcast(FP8X4), scales=scl[:], in_=st[("grp", g)][:])
+            st[("codes", g)] = codes
+            st[("scl", g)] = scl
+
+        def stage_mx(g):
+            codes = st[("codes", g)]
+            scl = st[("scl", g)]
+            u1 = up.tile([P, GW], F32)
+            u2 = up.tile([P, GW], F32)
+            sums = sp.tile([P, 2 * GT], F32)
+            for t in range(GT):
+                for o, u_sb in enumerate((u1, u2)):
+                    c = (o * GT + t) * P
+                    acc = pac.tile([P, H], F32, tag="acc")
+                    nc.tensor.matmul_mx(
+                        out=acc[:],
+                        lhsT=codes[:, c : c + P].bitcast(FP8X4),
+                        lhsT_scale=scl[:, c : c + P],
+                        rhs=w_codes[o][:].bitcast(FP8X4),
+                        rhs_scale=w_scales[o][:],
+                        start=True,
+                        stop=True,
+                    )
+                    nc.vector.scalar_tensor_tensor(
+                        out=u_sb[:, t * H : (t + 1) * H],
+                        in0=acc[:],
+                        scalar=1.0,
+                        in1=bias[o][:],
+                        op0=ALU.mult,
+                        op1=ALU.add,
+                        accum_out=sums[:, o * GT + t : o * GT + t + 1],
+                    )
+            st[("u1", g)] = u1
+            st[("u2", g)] = u2
+            st[("sums", g)] = sums
+
+        def stage_stats(g):
+            negmu = sp.tile([P, 2 * GT], F32)
+            nc.scalar.mul(out=negmu[:], in_=st[("sums", g)][:], mul=-1.0 / H)
+            ssq = sp.tile([P, 2 * GT], F32)
+            for t in range(GT):
+                for o, key in enumerate(("u1", "u2")):
+                    c = o * GT + t
+                    junk = jp.tile([P, H], BF16)
+                    nc.scalar.activation(
+                        out=junk[:],
+                        in_=st[(key, g)][:, t * H : (t + 1) * H],
+                        func=ACT.Square,
+                        bias=negmu[:, c : c + 1],
+                        scale=1.0,
+                        accum_out=ssq[:, c : c + 1],
+                    )
+            tv = sp.tile([P, 2 * GT], F32)
+            nc.gpsimd.tensor_scalar(
+                out=tv[:], in0=ssq[:], scalar1=1.0 / H, scalar2=EPS, op0=ALU.mult, op1=ALU.add
+            )
+            rstd = sp.tile([P, 2 * GT], F32)
+            nc.gpsimd.tensor_tensor(out=rstd[:], in0=tv[:], in1=mhalf[:], op=ALU.pow)
+            c1 = sp.tile([P, GT], F32)
+            nc.gpsimd.tensor_tensor(out=c1[:], in0=negmu[:, 0:GT], in1=rstd[:, 0:GT], op=ALU.mult)
+            std1 = sp.tile([P, GT], F32)
+            nc.gpsimd.tensor_tensor(out=std1[:], in0=tv[:, 0:GT], in1=rstd[:, 0:GT], op=ALU.mult)
+            q = sp.tile([P, GT], F32)
+            nc.gpsimd.tensor_tensor(out=q[:], in0=std1[:], in1=rstd[:, GT : 2 * GT], op=ALU.mult)
+            st[("negmu", g)] = negmu
+            st[("rstd", g)] = rstd
+            st[("c1", g)] = c1
+            st[("q", g)] = q
+
+        def stage_d(g):
+            u1 = st[("u1", g)]
+            u2 = st[("u2", g)]
+            r_sb = st[("r", g)]
+            negmu = st[("negmu", g)]
+            n_sb = npool.tile([P, GW], F32)
+            for t in range(GT):
+                cs = slice(t * H, (t + 1) * H)
+                nc.vector.scalar_tensor_tensor(
+                    out=u2[:, cs],
+                    in0=u2[:, cs],
+                    scalar=negmu[:, GT + t : GT + t + 1],
+                    in1=r_sb[:, cs],
+                    op0=ALU.add,
+                    op1=ALU.mult,
+                )
+                nc.vector.scalar_tensor_tensor(
+                    out=u2[:, cs],
+                    in0=u2[:, cs],
+                    scalar=st[("q", g)][:, t : t + 1],
+                    in1=u1[:, cs],
+                    op0=ALU.mult,
+                    op1=ALU.add,
+                )
+                nc.scalar.activation(
+                    out=n_sb[:, cs],
+                    in_=u2[:, cs],
+                    func=ACT.Tanh,
+                    bias=st[("c1", g)][:, t : t + 1],
+                    scale=st[("rstd", g)][:, t : t + 1],
+                )
+            st[("n", g)] = n_sb
+
+        def stage_e(g):
+            z_sb = st[("z", g)]
+            h_sb = st[("h", g)]
+            n_sb = st[("n", g)]
+            zh = op.tile([P, GW], F32)
+            eng = nc.gpsimd if GP9 else nc.vector
+            eng.tensor_tensor(out=zh[:], in0=z_sb[:], in1=h_sb[:], op=ALU.mult)
+            nc.vector.scalar_tensor_tensor(
+                out=n_sb[:],
+                in0=z_sb[:],
+                scalar=1.0,
+                in1=n_sb[:],
+                op0=ALU.subtract,
+                op1=ALU.mult,
+            )
+            nc.vector.tensor_tensor(out=zh[:], in0=zh[:], in1=n_sb[:], op=ALU.subtract)
+            nc.sync.dma_start(out=ov[:, g * GW : (g + 1) * GW], in_=zh[:])
+
+        for s in range(NG + 3):
+            if s + 1 < NG:
+                load(s + 1)
+            if s < NG:
+                stage_b(s)
+            if 0 <= s - 1 < NG:
+                stage_mx(s - 1)
+            if s < NG:
+                stage_q(s)
+            if 0 <= s - 1 < NG:
+                stage_stats(s - 1)
+            if 0 <= s - 2 < NG:
+                stage_d(s - 2)
+            if 0 <= s - 3 < NG:
+                stage_e(s - 3)

@@ -23,7 +23,7 @@ EPS = 1e-5
 
 FLOPS = 2 * 2 * B * K * H
 
-GP9 = False
+GP9 = True
 PIN = False
 
 
@@ -45,7 +45,7 @@ def tile_layernormgrucell_pb_t_kernel(tc, x, h, r, z, W_in, b_in, W_hn, b_hn, ou
         cp = ctx.enter_context(tc.tile_pool(name="cp", bufs=2))
         up = ctx.enter_context(tc.tile_pool(name="up", bufs=2))
         npool = ctx.enter_context(tc.tile_pool(name="npool", bufs=2))
-        op = ctx.enter_context(tc.tile_pool(name="op", bufs=2))
+        op = ctx.enter_context(tc.tile_pool(name="op", bufs=3))
         sp = ctx.enter_context(tc.tile_pool(name="sp", bufs=3))
         jp = ctx.enter_context(tc.tile_pool(name="jp", bufs=2))
         pti = ctx.enter_context(tc.psum_pool(name="pti", bufs=4))
@@ -242,13 +242,20 @@ def tile_layernormgrucell_pb_t_kernel(tc, x, h, r, z, W_in, b_in, W_hn, b_hn, ou
                 )
             st[("n", g)] = n_sb
 
-        def stage_e(g):
+        def stage_zh(g):
             z_sb = st[("z", g)]
             h_sb = st[("h", g)]
-            n_sb = st[("n", g)]
             zh = op.tile([P, GW], F32)
             eng = nc.gpsimd if GP9 else nc.vector
-            eng.tensor_tensor(out=zh[:], in0=z_sb[:], in1=h_sb[:], op=ALU.mult)
+            for t in range(GT):
+                cs = slice(t * H, (t + 1) * H)
+                eng.tensor_tensor(out=zh[:, cs], in0=z_sb[:, cs], in1=h_sb[:, cs], op=ALU.mult)
+            st[("zh", g)] = zh
+
+        def stage_e(g):
+            z_sb = st[("z", g)]
+            n_sb = st[("n", g)]
+            zh = st[("zh", g)]
             nc.vector.scalar_tensor_tensor(
                 out=n_sb[:],
                 in0=z_sb[:],
@@ -272,6 +279,7 @@ def tile_layernormgrucell_pb_t_kernel(tc, x, h, r, z, W_in, b_in, W_hn, b_hn, ou
             if 0 <= s - 1 < NG:
                 stage_stats(s - 1)
             if 0 <= s - 2 < NG:
+                stage_zh(s - 2)
                 stage_d(s - 2)
             if 0 <= s - 3 < NG:
                 stage_e(s - 3)

@@ -19,81 +19,82 @@ NT = B // P
 GT = 4
 NG = NT // GT
 GW = GT * H
+HW = GW // 2
 EPS = 1e-5
 
 FLOPS = 2 * 2 * B * K * H
 
-GP9 = True
-PIN = False
+G9 = True
 
 
 def tile_layernormgrucell_pb_t_kernel(tc, x, h, r, z, W_in, b_in, W_hn, b_hn, out):
     nc = tc.nc
-    xv = x.rearrange("(p t) k -> p (t k)", t=NT)
-    hv = h.rearrange("(p t) k -> p (t k)", t=NT)
-    rv = r.rearrange("(p t) k -> p (t k)", t=NT)
-    zv = z.rearrange("(p t) k -> p (t k)", t=NT)
+    views = {
+        "x": x.rearrange("(p t) k -> p (t k)", t=NT),
+        "h": h.rearrange("(p t) k -> p (t k)", t=NT),
+        "r": r.rearrange("(p t) k -> p (t k)", t=NT),
+        "z": z.rearrange("(p t) k -> p (t k)", t=NT),
+    }
     ov = out.rearrange("(p t) k -> p (t k)", t=NT)
 
     with ExitStack() as ctx:
         const = ctx.enter_context(tc.tile_pool(name="const", bufs=1))
-        xp = ctx.enter_context(tc.tile_pool(name="xp", bufs=3))
-        hp = ctx.enter_context(tc.tile_pool(name="hp", bufs=5))
-        rp = ctx.enter_context(tc.tile_pool(name="rp", bufs=4))
-        zp = ctx.enter_context(tc.tile_pool(name="zp", bufs=5))
+        pools = {
+            "x": ctx.enter_context(tc.tile_pool(name="xp", bufs=3)),
+            "h": ctx.enter_context(tc.tile_pool(name="hp", bufs=5)),
+            "r": ctx.enter_context(tc.tile_pool(name="rp", bufs=3)),
+            "z": ctx.enter_context(tc.tile_pool(name="zp", bufs=2)),
+        }
         gp = ctx.enter_context(tc.tile_pool(name="gp", bufs=2))
         cp = ctx.enter_context(tc.tile_pool(name="cp", bufs=2))
         up = ctx.enter_context(tc.tile_pool(name="up", bufs=2))
         npool = ctx.enter_context(tc.tile_pool(name="npool", bufs=2))
-        op = ctx.enter_context(tc.tile_pool(name="op", bufs=3))
         sp = ctx.enter_context(tc.tile_pool(name="sp", bufs=3))
         jp = ctx.enter_context(tc.tile_pool(name="jp", bufs=2))
         pti = ctx.enter_context(tc.psum_pool(name="pti", bufs=4))
         pac = ctx.enter_context(tc.psum_pool(name="pac", bufs=4))
-        if PIN:
-            ctx.enter_context(tc.manual_schedule())
+        ctx.enter_context(tc.manual_schedule())
 
         st = {}
 
-        def load(g):
-            cols = slice(g * GW, (g + 1) * GW)
-            x_sb = xp.tile([P, GW], BF16)
-            nc.sync.dma_start(out=x_sb[:], in_=xv[:, cols])
-            h_sb = hp.tile([P, GW], BF16)
-            nc.sync.dma_start(out=h_sb[:], in_=hv[:, cols])
-            r_sb = rp.tile([P, GW], BF16)
-            nc.sync.dma_start(out=r_sb[:], in_=rv[:, cols])
-            z_sb = zp.tile([P, GW], BF16)
-            nc.sync.dma_start(out=z_sb[:], in_=zv[:, cols])
-            st[("x", g)] = x_sb
-            st[("h", g)] = h_sb
-            st[("r", g)] = r_sb
-            st[("z", g)] = z_sb
+        def load(key, g):
+            t_sb = pools[key].tile([P, GW], BF16, name="in_" + key)
+            nc.sync.dma_start(out=t_sb[:], in_=views[key][:, g * GW : (g + 1) * GW])
+            st[(key, g)] = t_sb
 
-        ident = const.tile([P, P], F32)
-        make_identity(nc, ident[:])
-        mhalf = const.tile([P, 2 * GT], F32)
-        nc.gpsimd.memset(mhalf[:], -0.5)
-
-        w_raw = []
-        for i, w in enumerate((W_in, W_hn)):
+        def load_w(i, w):
             w_sb = const.tile([P, 4 * K], BF16, name="w_sb%d" % i)
             nc.sync.dma_start(
                 out=w_sb[:].rearrange("p (a k) -> p a k", a=4),
                 in_=w.rearrange("(a p) k -> p a k", p=P),
             )
-            w_raw.append(w_sb)
-            if i == 0:
-                load(0)
+            return w_sb
+
+        ident = const.tile([P, P], F32)
+        make_identity(nc, ident[:])
+        expo = const.tile([P, 3 * GT], F32)
+        nc.gpsimd.memset(expo[:, 0 : 2 * GT], -0.5)
+        nc.gpsimd.memset(expo[:, 2 * GT : 3 * GT], 0.5)
+        eps_c = const.tile([P, 1], F32)
+        nc.gpsimd.memset(eps_c[:], EPS)
+
+        w_raw = [load_w(0, W_in)]
+        load("x", 0)
+        load("h", 0)
+        w_raw.append(load_w(1, W_hn))
         bias = []
         for i, b in enumerate((b_in, b_hn)):
             b_sb = const.tile([P, H], BF16, name="b_sb%d" % i)
             nc.gpsimd.dma_start(out=b_sb[:], in_=b.partition_broadcast(P))
             bias.append(b_sb)
+        load("x", 1)
+        load("h", 1)
+        load("r", 0)
 
         w_codes = []
         w_scales = []
-        for i in range(2):
+
+        def prep_w(i):
             wf = w_raw[i][:].bitcast(F32)
             wg = const.tile([P, 4 * H], BF16, name="wg%d" % i, align_bytes=64)
             wgf = wg[:].bitcast(F32)
@@ -117,7 +118,7 @@ def tile_layernormgrucell_pb_t_kernel(tc, x, h, r, z, W_in, b_in, W_hn, b_hn, ou
             w_codes.append(wc)
             w_scales.append(ws)
 
-        def stage_b(g):
+        def front(g):
             xf = st[("x", g)][:].bitcast(F32)
             hf = st[("h", g)][:].bitcast(F32)
             grp = gp.tile([P, 2 * GT * 512], BF16, align_bytes=64)
@@ -137,22 +138,25 @@ def tile_layernormgrucell_pb_t_kernel(tc, x, h, r, z, W_in, b_in, W_hn, b_hn, ou
                 )
             st[("grp", g)] = grp
 
-        def stage_q(g):
+        def quantise(g):
             codes = cp.tile([P, 2 * GT * P], U32, align_bytes=64)
             scl = cp.tile([P, 2 * GT * P], U8, align_bytes=64)
             nc.vector.quantize_mx(out=codes[:].bitcast(FP8X4), scales=scl[:], in_=st[("grp", g)][:])
             st[("codes", g)] = codes
             st[("scl", g)] = scl
 
-        def stage_mx(g):
+        def window(g):
             codes = st[("codes", g)]
             scl = st[("scl", g)]
             u1 = up.tile([P, GW], F32)
             u2 = up.tile([P, GW], F32)
             sums = sp.tile([P, 2 * GT], F32)
+            ssq = sp.tile([P, 2 * GT], F32)
             for t in range(GT):
+                cs = slice(t * H, (t + 1) * H)
                 for o, u_sb in enumerate((u1, u2)):
                     c = (o * GT + t) * P
+                    col = o * GT + t
                     acc = pac.tile([P, H], F32, tag="acc")
                     nc.tensor.matmul_mx(
                         out=acc[:],
@@ -164,71 +168,70 @@ def tile_layernormgrucell_pb_t_kernel(tc, x, h, r, z, W_in, b_in, W_hn, b_hn, ou
                         stop=True,
                     )
                     nc.vector.scalar_tensor_tensor(
-                        out=u_sb[:, t * H : (t + 1) * H],
+                        out=u_sb[:, cs],
                         in0=acc[:],
                         scalar=1.0,
                         in1=bias[o][:],
                         op0=ALU.mult,
                         op1=ALU.add,
-                        accum_out=sums[:, o * GT + t : o * GT + t + 1],
+                        accum_out=sums[:, col : col + 1],
                     )
+                    junk = jp.tile([P, H], BF16, tag="junk")
+                    nc.scalar.activation(
+                        out=junk[:],
+                        in_=u_sb[:, cs],
+                        func=ACT.Square,
+                        bias=sums[:, col : col + 1],
+                        scale=-1.0 * H,
+                        accum_out=ssq[:, col : col + 1],
+                    )
+            negmu2 = sp.tile([P, GT], F32)
+            nc.scalar.mul(out=negmu2[:], in_=sums[:, GT : 2 * GT], mul=-1.0 / H)
+            tv = sp.tile([P, 3 * GT], F32)
+            nc.scalar.activation(
+                out=tv[:, 0 : 2 * GT], in_=ssq[:], func=ACT.Identity, bias=eps_c[:], scale=1.0 / (H * H * H)
+            )
+            nc.scalar.activation(
+                out=tv[:, 2 * GT : 3 * GT], in_=ssq[:, 0:GT], func=ACT.Identity, bias=eps_c[:],
+                scale=1.0 / (H * H * H),
+            )
+            pw = sp.tile([P, 3 * GT], F32)
+            nc.gpsimd.tensor_tensor(out=pw[:], in0=tv[:], in1=expo[:], op=ALU.pow)
             st[("u1", g)] = u1
             st[("u2", g)] = u2
             st[("sums", g)] = sums
+            st[("negmu2", g)] = negmu2
+            st[("pw", g)] = pw
 
-        def stage_stats(g):
-            negmu = sp.tile([P, 2 * GT], F32)
-            nc.scalar.mul(out=negmu[:], in_=st[("sums", g)][:], mul=-1.0 / H)
-            ssq = sp.tile([P, 2 * GT], F32)
-            for t in range(GT):
-                for o, key in enumerate(("u1", "u2")):
-                    c = o * GT + t
-                    junk = jp.tile([P, H], BF16)
-                    nc.scalar.activation(
-                        out=junk[:],
-                        in_=st[(key, g)][:, t * H : (t + 1) * H],
-                        func=ACT.Square,
-                        bias=negmu[:, c : c + 1],
-                        scale=1.0,
-                        accum_out=ssq[:, c : c + 1],
-                    )
-            tv = sp.tile([P, 2 * GT], F32)
-            nc.gpsimd.tensor_scalar(
-                out=tv[:], in0=ssq[:], scalar1=1.0 / H, scalar2=EPS, op0=ALU.mult, op1=ALU.add
-            )
-            rstd = sp.tile([P, 2 * GT], F32)
-            nc.gpsimd.tensor_tensor(out=rstd[:], in0=tv[:], in1=mhalf[:], op=ALU.pow)
-            c1 = sp.tile([P, GT], F32)
-            nc.gpsimd.tensor_tensor(out=c1[:], in0=negmu[:, 0:GT], in1=rstd[:, 0:GT], op=ALU.mult)
-            std1 = sp.tile([P, GT], F32)
-            nc.gpsimd.tensor_tensor(out=std1[:], in0=tv[:, 0:GT], in1=rstd[:, 0:GT], op=ALU.mult)
-            q = sp.tile([P, GT], F32)
-            nc.gpsimd.tensor_tensor(out=q[:], in0=std1[:], in1=rstd[:, GT : 2 * GT], op=ALU.mult)
-            st[("negmu", g)] = negmu
-            st[("rstd", g)] = rstd
-            st[("c1", g)] = c1
-            st[("q", g)] = q
-
-        def stage_d(g):
+        def candidate(g):
             u1 = st[("u1", g)]
             u2 = st[("u2", g)]
             r_sb = st[("r", g)]
-            negmu = st[("negmu", g)]
+            pw = st[("pw", g)]
+            for t in range(GT):
+                cs = slice(t * H, (t + 1) * H)
+                nc.vector.scalar_tensor_tensor(
+                    out=u2[:, cs],
+                    in0=u2[:, cs],
+                    scalar=st[("negmu2", g)][:, t : t + 1],
+                    in1=r_sb[:, cs],
+                    op0=ALU.add,
+                    op1=ALU.mult,
+                )
+            c1 = sp.tile([P, GT], F32)
+            nc.vector.scalar_tensor_tensor(
+                out=c1[:], in0=st[("sums", g)][:, 0:GT], scalar=-1.0 / H, in1=pw[:, 0:GT],
+                op0=ALU.mult, op1=ALU.mult,
+            )
+            q = sp.tile([P, GT], F32)
+            nc.vector.tensor_tensor(out=q[:], in0=pw[:, 2 * GT : 3 * GT], in1=pw[:, GT : 2 * GT], op=ALU.mult)
             n_sb = npool.tile([P, GW], F32)
             for t in range(GT):
                 cs = slice(t * H, (t + 1) * H)
                 nc.vector.scalar_tensor_tensor(
                     out=u2[:, cs],
                     in0=u2[:, cs],
-                    scalar=negmu[:, GT + t : GT + t + 1],
-                    in1=r_sb[:, cs],
-                    op0=ALU.add,
-                    op1=ALU.mult,
-                )
-                nc.vector.scalar_tensor_tensor(
-                    out=u2[:, cs],
-                    in0=u2[:, cs],
-                    scalar=st[("q", g)][:, t : t + 1],
+                    scalar=q[:, t : t + 1],
                     in1=u1[:, cs],
                     op0=ALU.mult,
                     op1=ALU.add,
@@ -237,49 +240,58 @@ def tile_layernormgrucell_pb_t_kernel(tc, x, h, r, z, W_in, b_in, W_hn, b_hn, ou
                     out=n_sb[:, cs],
                     in_=u2[:, cs],
                     func=ACT.Tanh,
-                    bias=st[("c1", g)][:, t : t + 1],
-                    scale=st[("rstd", g)][:, t : t + 1],
+                    bias=c1[:, t : t + 1],
+                    scale=pw[:, t : t + 1],
                 )
             st[("n", g)] = n_sb
 
-        def stage_zh(g):
-            z_sb = st[("z", g)]
-            h_sb = st[("h", g)]
-            zh = op.tile([P, GW], F32)
-            eng = nc.gpsimd if GP9 else nc.vector
-            for t in range(GT):
+        def gate_product(g):
+            zh = st[("u1", g)]
+            for t in (3, 0, 1, 2):
                 cs = slice(t * H, (t + 1) * H)
-                eng.tensor_tensor(out=zh[:, cs], in0=z_sb[:, cs], in1=h_sb[:, cs], op=ALU.mult)
-            st[("zh", g)] = zh
+                nc.gpsimd.tensor_tensor(
+                    out=zh[:, cs], in0=st[("z", g)][:, cs], in1=st[("h", g)][:, cs], op=ALU.mult
+                )
 
-        def stage_e(g):
+        def blend(g):
             z_sb = st[("z", g)]
             n_sb = st[("n", g)]
-            zh = st[("zh", g)]
-            nc.vector.scalar_tensor_tensor(
-                out=n_sb[:],
-                in0=z_sb[:],
-                scalar=1.0,
-                in1=n_sb[:],
-                op0=ALU.subtract,
-                op1=ALU.mult,
-            )
-            nc.vector.tensor_tensor(out=zh[:], in0=zh[:], in1=n_sb[:], op=ALU.subtract)
-            nc.sync.dma_start(out=ov[:, g * GW : (g + 1) * GW], in_=zh[:])
+            zh = st[("u1", g)]
+            halves = (slice(0, HW), slice(HW, GW))
+            if not G9:
+                for cs in halves:
+                    nc.vector.tensor_tensor(out=zh[:, cs], in0=z_sb[:, cs], in1=st[("h", g)][:, cs], op=ALU.mult)
+            for cs in halves:
+                nc.vector.scalar_tensor_tensor(
+                    out=n_sb[:, cs], in0=z_sb[:, cs], scalar=1.0, in1=n_sb[:, cs],
+                    op0=ALU.subtract, op1=ALU.mult,
+                )
+            for i, cs in enumerate(halves):
+                nc.vector.tensor_tensor(out=zh[:, cs], in0=zh[:, cs], in1=n_sb[:, cs], op=ALU.subtract)
+                c0 = g * GW + i * HW
+                nc.sync.dma_start(out=ov[:, c0 : c0 + HW], in_=zh[:, cs])
 
-        for s in range(NG + 3):
+        prep_w(0)
+        front(0)
+        quantise(0)
+        prep_w(1)
+        for s in range(NG + 2):
+            if s + 2 < NG:
+                load("x", s + 2)
+                load("h", s + 2)
             if s + 1 < NG:
-                load(s + 1)
-            if s < NG:
-                stage_b(s)
+                load("r", s + 1)
             if 0 <= s - 1 < NG:
-                stage_mx(s - 1)
-            if s < NG:
-                stage_q(s)
+                load("z", s - 1)
+            if G9 and 0 <= s - 2 < NG:
+                gate_product(s - 2)
             if 0 <= s - 1 < NG:
-                stage_stats(s - 1)
+                window(s - 1)
+            if s + 1 < NG:
+                front(s + 1)
+            if 0 < s < NG:
+                quantise(s)
             if 0 <= s - 2 < NG:
-                stage_zh(s - 2)
-                stage_d(s - 2)
-            if 0 <= s - 3 < NG:
-                stage_e(s - 3)
+                blend(s - 2)
+            if 0 <= s - 1 < NG:
+                candidate(s - 1)

@@ -24,7 +24,7 @@ EPS = 1e-5
 
 FLOPS = 2 * 2 * B * K * H
 
-G9 = True
+G9 = False
 
 
 def tile_layernormgrucell_pb_t_kernel(tc, x, h, r, z, W_in, b_in, W_hn, b_hn, out):

@@ -24,7 +24,7 @@ EPS = 1e-5
 
 FLOPS = 2 * 2 * B * K * H
 
-G9 = False
+G9 = True
 
 
 def tile_layernormgrucell_pb_t_kernel(tc, x, h, r, z, W_in, b_in, W_hn, b_hn, out):
@@ -72,9 +72,6 @@ def tile_layernormgrucell_pb_t_kernel(tc, x, h, r, z, W_in, b_in, W_hn, b_hn, ou
 
         ident = const.tile([P, P], F32)
         make_identity(nc, ident[:])
-        expo = const.tile([P, 3 * GT], F32)
-        nc.gpsimd.memset(expo[:, 0 : 2 * GT], -0.5)
-        nc.gpsimd.memset(expo[:, 2 * GT : 3 * GT], 0.5)
         eps_c = const.tile([P, 1], F32)
         nc.gpsimd.memset(eps_c[:], EPS)
 
@@ -187,27 +184,23 @@ def tile_layernormgrucell_pb_t_kernel(tc, x, h, r, z, W_in, b_in, W_hn, b_hn, ou
                     )
             negmu2 = sp.tile([P, GT], F32)
             nc.scalar.mul(out=negmu2[:], in_=sums[:, GT : 2 * GT], mul=-1.0 / H)
-            tv = sp.tile([P, 3 * GT], F32)
+            std = sp.tile([P, 2 * GT], F32)
             nc.scalar.activation(
-                out=tv[:, 0 : 2 * GT], in_=ssq[:], func=ACT.Identity, bias=eps_c[:], scale=1.0 / (H * H * H)
+                out=std[:], in_=ssq[:], func=ACT.Sqrt, bias=eps_c[:], scale=1.0 / (H * H * H)
             )
-            nc.scalar.activation(
-                out=tv[:, 2 * GT : 3 * GT], in_=ssq[:, 0:GT], func=ACT.Identity, bias=eps_c[:],
-                scale=1.0 / (H * H * H),
-            )
-            pw = sp.tile([P, 3 * GT], F32)
-            nc.gpsimd.tensor_tensor(out=pw[:], in0=tv[:], in1=expo[:], op=ALU.pow)
             st[("u1", g)] = u1
             st[("u2", g)] = u2
             st[("sums", g)] = sums
             st[("negmu2", g)] = negmu2
-            st[("pw", g)] = pw
+            st[("std", g)] = std
 
         def candidate(g):
             u1 = st[("u1", g)]
             u2 = st[("u2", g)]
             r_sb = st[("r", g)]
-            pw = st[("pw", g)]
+            std = st[("std", g)]
+            rstd = sp.tile([P, 2 * GT], F32)
+            nc.vector.reciprocal(out=rstd[:], in_=std[:])
             for t in range(GT):
                 cs = slice(t * H, (t + 1) * H)
                 nc.vector.scalar_tensor_tensor(
@@ -218,13 +211,13 @@ def tile_layernormgrucell_pb_t_kernel(tc, x, h, r, z, W_in, b_in, W_hn, b_hn, ou
                     op0=ALU.add,
                     op1=ALU.mult,
                 )
+            q = sp.tile([P, GT], F32)
+            nc.vector.tensor_tensor(out=q[:], in0=std[:, 0:GT], in1=rstd[:, GT : 2 * GT], op=ALU.mult)
             c1 = sp.tile([P, GT], F32)
             nc.vector.scalar_tensor_tensor(
-                out=c1[:], in0=st[("sums", g)][:, 0:GT], scalar=-1.0 / H, in1=pw[:, 0:GT],
+                out=c1[:], in0=st[("sums", g)][:, 0:GT], scalar=-1.0 / H, in1=rstd[:, 0:GT],
                 op0=ALU.mult, op1=ALU.mult,
             )
-            q = sp.tile([P, GT], F32)
-            nc.vector.tensor_tensor(out=q[:], in0=pw[:, 2 * GT : 3 * GT], in1=pw[:, GT : 2 * GT], op=ALU.mult)
             n_sb = npool.tile([P, GW], F32)
             for t in range(GT):
                 cs = slice(t * H, (t + 1) * H)
@@ -241,7 +234,7 @@ def tile_layernormgrucell_pb_t_kernel(tc, x, h, r, z, W_in, b_in, W_hn, b_hn, ou
                     in_=u2[:, cs],
                     func=ACT.Tanh,
                     bias=c1[:, t : t + 1],
-                    scale=pw[:, t : t + 1],
+                    scale=rstd[:, t : t + 1],
                 )
             st[("n", g)] = n_sb
 

@@ -24,8 +24,6 @@ EPS = 1e-5
 
 FLOPS = 2 * 2 * B * K * H
 
-G9 = True
-
 
 def tile_layernormgrucell_pb_t_kernel(tc, x, h, r, z, W_in, b_in, W_hn, b_hn, out):
     nc = tc.nc
@@ -75,15 +73,17 @@ def tile_layernormgrucell_pb_t_kernel(tc, x, h, r, z, W_in, b_in, W_hn, b_hn, ou
         eps_c = const.tile([P, 1], F32)
         nc.gpsimd.memset(eps_c[:], EPS)
 
+        ones = const.tile([P, P], BF16)
+        nc.vector.memset(ones[:], 1.0)
+        brow = const.tile([P, 2 * H], BF16)
+        nc.vector.memset(brow[:], 0.0)
+        nc.scalar.dma_start(out=brow[0:1, 0:H], in_=b_in.rearrange("(o n) -> o n", o=1))
+        nc.scalar.dma_start(out=brow[0:1, H : 2 * H], in_=b_hn.rearrange("(o n) -> o n", o=1))
+
         w_raw = [load_w(0, W_in)]
         load("x", 0)
         load("h", 0)
         w_raw.append(load_w(1, W_hn))
-        bias = []
-        for i, b in enumerate((b_in, b_hn)):
-            b_sb = const.tile([P, H], BF16, name="b_sb%d" % i)
-            nc.gpsimd.dma_start(out=b_sb[:], in_=b.partition_broadcast(P))
-            bias.append(b_sb)
         load("x", 1)
         load("h", 1)
         load("r", 0)
@@ -240,20 +240,17 @@ def tile_layernormgrucell_pb_t_kernel(tc, x, h, r, z, W_in, b_in, W_hn, b_hn, ou
 
         def gate_product(g):
             zh = st[("u1", g)]
-            for t in (3, 0, 1, 2):
-                cs = slice(t * H, (t + 1) * H)
-                nc.gpsimd.tensor_tensor(
-                    out=zh[:, cs], in0=st[("z", g)][:, cs], in1=st[("h", g)][:, cs], op=ALU.mult
-                )
+            cs = slice(0 if g + 1 < NG else HW, GW)
+            nc.gpsimd.tensor_tensor(out=zh[:, cs], in0=st[("z", g)][:, cs], in1=st[("h", g)][:, cs], op=ALU.mult)
 
         def blend(g):
             z_sb = st[("z", g)]
             n_sb = st[("n", g)]
             zh = st[("u1", g)]
             halves = (slice(0, HW), slice(HW, GW))
-            if not G9:
-                for cs in halves:
-                    nc.vector.tensor_tensor(out=zh[:, cs], in0=z_sb[:, cs], in1=st[("h", g)][:, cs], op=ALU.mult)
+            if g + 1 == NG:
+                cs = halves[0]
+                nc.vector.tensor_tensor(out=zh[:, cs], in0=z_sb[:, cs], in1=st[("h", g)][:, cs], op=ALU.mult)
             for cs in halves:
                 nc.vector.scalar_tensor_tensor(
                     out=n_sb[:, cs], in0=z_sb[:, cs], scalar=1.0, in1=n_sb[:, cs],
@@ -264,6 +261,13 @@ def tile_layernormgrucell_pb_t_kernel(tc, x, h, r, z, W_in, b_in, W_hn, b_hn, ou
                 c0 = g * GW + i * HW
                 nc.sync.dma_start(out=ov[:, c0 : c0 + HW], in_=zh[:, cs])
 
+        bias = []
+        for i in range(2):
+            b_ps = pti.tile([P, H], F32, tag="ti")
+            nc.tensor.matmul(out=b_ps[:], lhsT=ones[:], rhs=brow[:, i * H : (i + 1) * H], start=True, stop=True)
+            b_sb = const.tile([P, H], F32, name="b_sb%d" % i)
+            nc.scalar.copy(out=b_sb[:], in_=b_ps[:])
+            bias.append(b_sb)
         prep_w(0)
         front(0)
         quantise(0)
@@ -276,7 +280,7 @@ def tile_layernormgrucell_pb_t_kernel(tc, x, h, r, z, W_in, b_in, W_hn, b_hn, ou
                 load("r", s + 1)
             if 0 <= s - 1 < NG:
                 load("z", s - 1)
-            if G9 and 0 <= s - 2 < NG:
+            if 0 <= s - 2 < NG:
                 gate_product(s - 2)
             if 0 <= s - 1 < NG:
                 window(s - 1)

@@ -240,8 +240,11 @@ def tile_layernormgrucell_pb_t_kernel(tc, x, h, r, z, W_in, b_in, W_hn, b_hn, ou
 
         def gate_product(g):
             zh = st[("u1", g)]
-            cs = slice(0 if g + 1 < NG else HW, GW)
-            nc.gpsimd.tensor_tensor(out=zh[:, cs], in0=st[("z", g)][:, cs], in1=st[("h", g)][:, cs], op=ALU.mult)
+            cuts = (0, (GT - 1) * H, GW) if g + 1 < NG else (HW, GW)
+            for c0, c1 in zip(cuts[:-1], cuts[1:]):
+                nc.gpsimd.tensor_tensor(
+                    out=zh[:, c0:c1], in0=st[("z", g)][:, c0:c1], in1=st[("h", g)][:, c0:c1], op=ALU.mult
+                )
 
         def blend(g):
             z_sb = st[("z", g)]
@@ -261,6 +264,9 @@ def tile_layernormgrucell_pb_t_kernel(tc, x, h, r, z, W_in, b_in, W_hn, b_hn, ou
                 c0 = g * GW + i * HW
                 nc.sync.dma_start(out=ov[:, c0 : c0 + HW], in_=zh[:, cs])
 
+        prep_w(0)
+        front(0)
+        quantise(0)
         bias = []
         for i in range(2):
             b_ps = pti.tile([P, H], F32, tag="ti")
@@ -268,9 +274,6 @@ def tile_layernormgrucell_pb_t_kernel(tc, x, h, r, z, W_in, b_in, W_hn, b_hn, ou
             b_sb = const.tile([P, H], F32, name="b_sb%d" % i)
             nc.scalar.copy(out=b_sb[:], in_=b_ps[:])
             bias.append(b_sb)
-        prep_w(0)
-        front(0)
-        quantise(0)
         prep_w(1)
         for s in range(NG + 2):
             if s + 2 < NG:

@@ -15,11 +15,13 @@ P = 128
 B = 4096
 K = 512
 H = 512
-NT = B // P
-GT = 4
-NG = NT // GT
-GW = GT * H
-HW = GW // 2
+WORDS = K // 2
+ROW_TILES = B // P
+GROUP_TILES = 4
+GROUPS = ROW_TILES // GROUP_TILES
+GROUP_COLS = GROUP_TILES * H
+HALF_COLS = GROUP_COLS // 2
+HALVES = (slice(0, HALF_COLS), slice(HALF_COLS, GROUP_COLS))
 EPS = 1e-5
 
 FLOPS = 2 * 2 * B * K * H
@@ -27,40 +29,51 @@ FLOPS = 2 * 2 * B * K * H
 
 def tile_layernormgrucell_pb_t_kernel(tc, x, h, r, z, W_in, b_in, W_hn, b_hn, out):
     nc = tc.nc
-    views = {
-        "x": x.rearrange("(p t) k -> p (t k)", t=NT),
-        "h": h.rearrange("(p t) k -> p (t k)", t=NT),
-        "r": r.rearrange("(p t) k -> p (t k)", t=NT),
-        "z": z.rearrange("(p t) k -> p (t k)", t=NT),
+    by_row_tile = "(p t) k -> p (t k)"
+    dram = {
+        "x": x.rearrange(by_row_tile, t=ROW_TILES),
+        "h": h.rearrange(by_row_tile, t=ROW_TILES),
+        "r": r.rearrange(by_row_tile, t=ROW_TILES),
+        "z": z.rearrange(by_row_tile, t=ROW_TILES),
     }
-    ov = out.rearrange("(p t) k -> p (t k)", t=NT)
+    out_rows = out.rearrange(by_row_tile, t=ROW_TILES)
 
     with ExitStack() as ctx:
         const = ctx.enter_context(tc.tile_pool(name="const", bufs=1))
-        pools = {
-            "x": ctx.enter_context(tc.tile_pool(name="xp", bufs=3)),
-            "h": ctx.enter_context(tc.tile_pool(name="hp", bufs=5)),
-            "r": ctx.enter_context(tc.tile_pool(name="rp", bufs=3)),
-            "z": ctx.enter_context(tc.tile_pool(name="zp", bufs=2)),
+        inputs = {
+            "x": ctx.enter_context(tc.tile_pool(name="in_x", bufs=3)),
+            "h": ctx.enter_context(tc.tile_pool(name="in_h", bufs=5)),
+            "r": ctx.enter_context(tc.tile_pool(name="in_r", bufs=3)),
+            "z": ctx.enter_context(tc.tile_pool(name="in_z", bufs=2)),
         }
-        gp = ctx.enter_context(tc.tile_pool(name="gp", bufs=2))
-        cp = ctx.enter_context(tc.tile_pool(name="cp", bufs=2))
-        up = ctx.enter_context(tc.tile_pool(name="up", bufs=2))
-        npool = ctx.enter_context(tc.tile_pool(name="npool", bufs=2))
-        sp = ctx.enter_context(tc.tile_pool(name="sp", bufs=3))
-        jp = ctx.enter_context(tc.tile_pool(name="jp", bufs=2))
-        pti = ctx.enter_context(tc.psum_pool(name="pti", bufs=4))
-        pac = ctx.enter_context(tc.psum_pool(name="pac", bufs=4))
+        work = ctx.enter_context(tc.tile_pool(name="work", bufs=2))
+        small = ctx.enter_context(tc.tile_pool(name="small", bufs=3))
+        psum_t = ctx.enter_context(tc.psum_pool(name="psum_t", bufs=4))
+        psum_mx = ctx.enter_context(tc.psum_pool(name="psum_mx", bufs=4))
         ctx.enter_context(tc.manual_schedule())
 
-        st = {}
+        live = {}
 
-        def load(key, g):
-            t_sb = pools[key].tile([P, GW], BF16, name="in_" + key)
-            nc.sync.dma_start(out=t_sb[:], in_=views[key][:, g * GW : (g + 1) * GW])
-            st[(key, g)] = t_sb
+        def new_input(name, g):
+            live[(name, g)] = inputs[name].tile([P, GROUP_COLS], BF16, name="in_" + name)
 
-        def load_w(i, w):
+        def fetch(name, g, lo, hi):
+            nc.sync.dma_start(
+                out=live[(name, g)][:, lo:hi], in_=dram[name][:, g * GROUP_COLS + lo : g * GROUP_COLS + hi]
+            )
+
+        def load_activations(g):
+            new_input("x", g)
+            new_input("h", g)
+            for lo in (0, HALF_COLS):
+                fetch("x", g, lo, lo + HALF_COLS)
+                fetch("h", g, lo, lo + HALF_COLS)
+
+        def load_gate(name, g):
+            new_input(name, g)
+            fetch(name, g, 0, GROUP_COLS)
+
+        def load_weight(i, w):
             w_sb = const.tile([P, 4 * K], BF16, name="w_sb%d" % i)
             nc.sync.dma_start(
                 out=w_sb[:].rearrange("p (a k) -> p a k", a=4),
@@ -68,230 +81,210 @@ def tile_layernormgrucell_pb_t_kernel(tc, x, h, r, z, W_in, b_in, W_hn, b_hn, ou
             )
             return w_sb
 
-        ident = const.tile([P, P], F32)
-        make_identity(nc, ident[:])
-        eps_c = const.tile([P, 1], F32)
-        nc.gpsimd.memset(eps_c[:], EPS)
-
+        bias_rows = const.tile([P, 2 * H], BF16)
+        nc.vector.memset(bias_rows[:], 0.0)
         ones = const.tile([P, P], BF16)
         nc.vector.memset(ones[:], 1.0)
-        brow = const.tile([P, 2 * H], BF16)
-        nc.vector.memset(brow[:], 0.0)
-        nc.scalar.dma_start(out=brow[0:1, 0:H], in_=b_in.rearrange("(o n) -> o n", o=1))
-        nc.scalar.dma_start(out=brow[0:1, H : 2 * H], in_=b_hn.rearrange("(o n) -> o n", o=1))
+        nc.scalar.dma_start(out=bias_rows[0:1, 0:H], in_=b_in.rearrange("(o n) -> o n", o=1))
+        nc.scalar.dma_start(out=bias_rows[0:1, H : 2 * H], in_=b_hn.rearrange("(o n) -> o n", o=1))
+        identity = const.tile([P, P], F32)
+        make_identity(nc, identity[:])
+        eps = const.tile([P, 1], F32)
+        nc.gpsimd.memset(eps[:], EPS)
+        first_sqrt = const.tile([P, 1], F32)
+        nc.scalar.activation(out=first_sqrt[:], in_=ones[:, 0:1], func=ACT.Sqrt)
 
-        w_raw = [load_w(0, W_in)]
-        load("x", 0)
-        load("h", 0)
-        w_raw.append(load_w(1, W_hn))
-        load("x", 1)
-        load("h", 1)
-        load("r", 0)
+        w_raw = [load_weight(0, W_in), load_weight(1, W_hn)]
+        load_activations(0)
+        load_activations(1)
+        load_gate("r", 0)
 
         w_codes = []
         w_scales = []
-
-        def prep_w(i):
-            wf = w_raw[i][:].bitcast(F32)
-            wg = const.tile([P, 4 * H], BF16, name="wg%d" % i, align_bytes=64)
-            wgf = wg[:].bitcast(F32)
-            for hb in range(2):
-                wt = pti.tile([P, 512], F32, tag="ti")
+        for i in range(2):
+            w_words = w_raw[i][:].bitcast(F32)
+            w_grouped = const.tile([P, 4 * H], BF16, name="w_grouped%d" % i, align_bytes=64)
+            w_grouped_words = w_grouped[:].bitcast(F32)
+            for pair in range(2):
+                w_t = psum_t.tile([P, 512], F32, tag="t")
                 for u in range(2):
-                    for jl in range(2):
-                        a = 2 * hb + jl
+                    for j in range(2):
+                        a = 2 * pair + j
                         nc.tensor.transpose(
-                            wt[:, u * 256 + jl * P : u * 256 + (jl + 1) * P],
-                            wf[:, a * 256 + u * P : a * 256 + (u + 1) * P],
-                            ident[:],
+                            w_t[:, u * 256 + j * P : u * 256 + (j + 1) * P],
+                            w_words[:, a * WORDS + u * P : a * WORDS + (u + 1) * P],
+                            identity[:],
                         )
                 nc.vector.tensor_copy(
-                    out=wgf[:, hb * 512 : (hb + 1) * 512].rearrange("p (n u) -> p n u", u=2),
-                    in_=wt[:].rearrange("p (u n) -> p n u", u=2),
+                    out=w_grouped_words[:, pair * 512 : (pair + 1) * 512].rearrange("p (n u) -> p n u", u=2),
+                    in_=w_t[:].rearrange("p (u n) -> p n u", u=2),
                 )
-            wc = const.tile([P, H], U32, name="wc%d" % i, align_bytes=64)
-            ws = const.tile([P, H], U8, name="ws%d" % i, align_bytes=64)
-            nc.vector.quantize_mx(out=wc[:].bitcast(FP8X4), scales=ws[:], in_=wg[:])
-            w_codes.append(wc)
-            w_scales.append(ws)
+            codes = const.tile([P, H], U32, name="w_codes%d" % i, align_bytes=64)
+            scales = const.tile([P, H], U8, name="w_scales%d" % i, align_bytes=64)
+            nc.vector.quantize_mx(out=codes[:].bitcast(FP8X4), scales=scales[:], in_=w_grouped[:])
+            w_codes.append(codes)
+            w_scales.append(scales)
 
-        def front(g):
-            xf = st[("x", g)][:].bitcast(F32)
-            hf = st[("h", g)][:].bitcast(F32)
-            grp = gp.tile([P, 2 * GT * 512], BF16, align_bytes=64)
-            grpv = grp[:].bitcast(F32).rearrange("p (o t i u) -> p o t i u", o=2, t=GT, u=2)
-            for t in range(GT):
-                ti = pti.tile([P, 512], F32, tag="ti")
-                for o, src in enumerate((xf, hf)):
+        def transpose_group(g):
+            sources = (live[("x", g)][:].bitcast(F32), live[("h", g)][:].bitcast(F32))
+            grouped = work.tile([P, 2 * GROUP_COLS], BF16, align_bytes=64)
+            grouped_words = grouped[:].bitcast(F32)
+            for t in range(GROUP_TILES):
+                bank = psum_t.tile([P, 512], F32, tag="t")
+                for o in range(2):
                     for u in range(2):
                         nc.tensor.transpose(
-                            ti[:, (o * 2 + u) * P : (o * 2 + u + 1) * P],
-                            src[:, t * 256 + u * P : t * 256 + (u + 1) * P],
-                            ident[:],
+                            bank[:, (2 * o + u) * P : (2 * o + u + 1) * P],
+                            sources[o][:, t * WORDS + u * P : t * WORDS + (u + 1) * P],
+                            identity[:],
                         )
                 nc.scalar.copy(
-                    out=grpv[:, :, t],
-                    in_=ti[:].rearrange("p (o u i) -> p o i u", o=2, u=2),
+                    out=grouped_words[:, t * 512 : (t + 1) * 512].rearrange("p (o i u) -> p o i u", o=2, u=2),
+                    in_=bank[:].rearrange("p (o u i) -> p o i u", o=2, u=2),
                 )
-            st[("grp", g)] = grp
+            live[("grouped", g)] = grouped
 
-        def quantise(g):
-            codes = cp.tile([P, 2 * GT * P], U32, align_bytes=64)
-            scl = cp.tile([P, 2 * GT * P], U8, align_bytes=64)
-            nc.vector.quantize_mx(out=codes[:].bitcast(FP8X4), scales=scl[:], in_=st[("grp", g)][:])
-            st[("codes", g)] = codes
-            st[("scl", g)] = scl
+        def quantise_group(g):
+            grouped = live[("grouped", g)]
+            codes = work.tile([P, 2 * GROUP_TILES * P], U32, align_bytes=64)
+            scales = work.tile([P, 2 * GROUP_TILES * P], U8, align_bytes=64)
+            for i in range(2):
+                nc.vector.quantize_mx(
+                    out=codes[:, i * 512 : (i + 1) * 512].bitcast(FP8X4),
+                    scales=scales[:, i * 512 : (i + 1) * 512],
+                    in_=grouped[:, i * GROUP_COLS : (i + 1) * GROUP_COLS],
+                )
+            live[("codes", g)] = codes
+            live[("scales", g)] = scales
 
-        def window(g):
-            codes = st[("codes", g)]
-            scl = st[("scl", g)]
-            u1 = up.tile([P, GW], F32)
-            u2 = up.tile([P, GW], F32)
-            sums = sp.tile([P, 2 * GT], F32)
-            ssq = sp.tile([P, 2 * GT], F32)
-            for t in range(GT):
-                cs = slice(t * H, (t + 1) * H)
+        def products_and_moments(g):
+            codes = live[("codes", g)]
+            scales = live[("scales", g)]
+            u1 = work.tile([P, GROUP_COLS], F32)
+            u2 = work.tile([P, GROUP_COLS], F32)
+            sums = small.tile([P, 2 * GROUP_TILES], F32)
+            squares = small.tile([P, 2 * GROUP_TILES], F32)
+            for t in range(GROUP_TILES):
+                cols = slice(t * H, (t + 1) * H)
                 for o, u_sb in enumerate((u1, u2)):
-                    c = (o * GT + t) * P
-                    col = o * GT + t
-                    acc = pac.tile([P, H], F32, tag="acc")
+                    c = (2 * t + o) * P
+                    stat = slice(o * GROUP_TILES + t, o * GROUP_TILES + t + 1)
+                    acc = psum_mx.tile([P, H], F32)
                     nc.tensor.matmul_mx(
                         out=acc[:],
                         lhsT=codes[:, c : c + P].bitcast(FP8X4),
-                        lhsT_scale=scl[:, c : c + P],
+                        lhsT_scale=scales[:, c : c + P],
                         rhs=w_codes[o][:].bitcast(FP8X4),
                         rhs_scale=w_scales[o][:],
                         start=True,
                         stop=True,
                     )
                     nc.vector.scalar_tensor_tensor(
-                        out=u_sb[:, cs],
-                        in0=acc[:],
-                        scalar=1.0,
-                        in1=bias[o][:],
-                        op0=ALU.mult,
-                        op1=ALU.add,
-                        accum_out=sums[:, col : col + 1],
+                        out=u_sb[:, cols], in0=acc[:], scalar=1.0, in1=bias[o][:],
+                        op0=ALU.mult, op1=ALU.add, accum_out=sums[:, stat],
                     )
-                    junk = jp.tile([P, H], BF16, tag="junk")
+                    unused = work.tile([P, H], BF16)
                     nc.scalar.activation(
-                        out=junk[:],
-                        in_=u_sb[:, cs],
-                        func=ACT.Square,
-                        bias=sums[:, col : col + 1],
-                        scale=-1.0 * H,
-                        accum_out=ssq[:, col : col + 1],
+                        out=unused[:], in_=u_sb[:, cols], func=ACT.Square,
+                        bias=sums[:, stat], scale=-1.0 * H, accum_out=squares[:, stat],
                     )
-            negmu2 = sp.tile([P, GT], F32)
-            nc.scalar.mul(out=negmu2[:], in_=sums[:, GT : 2 * GT], mul=-1.0 / H)
-            std = sp.tile([P, 2 * GT], F32)
-            nc.scalar.activation(
-                out=std[:], in_=ssq[:], func=ACT.Sqrt, bias=eps_c[:], scale=1.0 / (H * H * H)
-            )
-            st[("u1", g)] = u1
-            st[("u2", g)] = u2
-            st[("sums", g)] = sums
-            st[("negmu2", g)] = negmu2
-            st[("std", g)] = std
+            minus_mean2 = small.tile([P, GROUP_TILES], F32)
+            nc.scalar.mul(out=minus_mean2[:], in_=sums[:, GROUP_TILES : 2 * GROUP_TILES], mul=-1.0 / H)
+            std = small.tile([P, 2 * GROUP_TILES], F32)
+            nc.scalar.activation(out=std[:], in_=squares[:], func=ACT.Sqrt, bias=eps[:], scale=1.0 / (H * H * H))
+            live[("u1", g)] = u1
+            live[("u2", g)] = u2
+            live[("sums", g)] = sums
+            live[("minus_mean2", g)] = minus_mean2
+            live[("std", g)] = std
 
         def candidate(g):
-            u1 = st[("u1", g)]
-            u2 = st[("u2", g)]
-            r_sb = st[("r", g)]
-            std = st[("std", g)]
-            rstd = sp.tile([P, 2 * GT], F32)
+            u1 = live[("u1", g)]
+            u2 = live[("u2", g)]
+            r_sb = live[("r", g)]
+            std = live[("std", g)]
+            first = slice(0, GROUP_TILES)
+            second = slice(GROUP_TILES, 2 * GROUP_TILES)
+            rstd = small.tile([P, 2 * GROUP_TILES], F32)
             nc.vector.reciprocal(out=rstd[:], in_=std[:])
-            for t in range(GT):
-                cs = slice(t * H, (t + 1) * H)
+            for t in range(GROUP_TILES):
+                cols = slice(t * H, (t + 1) * H)
                 nc.vector.scalar_tensor_tensor(
-                    out=u2[:, cs],
-                    in0=u2[:, cs],
-                    scalar=st[("negmu2", g)][:, t : t + 1],
-                    in1=r_sb[:, cs],
-                    op0=ALU.add,
-                    op1=ALU.mult,
+                    out=u2[:, cols], in0=u2[:, cols], scalar=live[("minus_mean2", g)][:, t : t + 1], in1=r_sb[:, cols],
+                    op0=ALU.add, op1=ALU.mult,
                 )
-            q = sp.tile([P, GT], F32)
-            nc.vector.tensor_tensor(out=q[:], in0=std[:, 0:GT], in1=rstd[:, GT : 2 * GT], op=ALU.mult)
-            c1 = sp.tile([P, GT], F32)
+            q = small.tile([P, GROUP_TILES], F32)
+            nc.vector.tensor_tensor(out=q[:], in0=std[:, first], in1=rstd[:, second], op=ALU.mult)
+            shift = small.tile([P, GROUP_TILES], F32)
             nc.vector.scalar_tensor_tensor(
-                out=c1[:], in0=st[("sums", g)][:, 0:GT], scalar=-1.0 / H, in1=rstd[:, 0:GT],
+                out=shift[:], in0=live[("sums", g)][:, first], scalar=-1.0 / H, in1=rstd[:, first],
                 op0=ALU.mult, op1=ALU.mult,
             )
-            n_sb = npool.tile([P, GW], F32)
-            for t in range(GT):
-                cs = slice(t * H, (t + 1) * H)
+            n_sb = work.tile([P, GROUP_COLS], F32)
+            for t in range(GROUP_TILES):
+                cols = slice(t * H, (t + 1) * H)
                 nc.vector.scalar_tensor_tensor(
-                    out=u2[:, cs],
-                    in0=u2[:, cs],
-                    scalar=q[:, t : t + 1],
-                    in1=u1[:, cs],
-                    op0=ALU.mult,
-                    op1=ALU.add,
+                    out=u2[:, cols], in0=u2[:, cols], scalar=q[:, t : t + 1], in1=u1[:, cols],
+                    op0=ALU.mult, op1=ALU.add,
                 )
                 nc.scalar.activation(
-                    out=n_sb[:, cs],
-                    in_=u2[:, cs],
-                    func=ACT.Tanh,
-                    bias=c1[:, t : t + 1],
-                    scale=rstd[:, t : t + 1],
+                    out=n_sb[:, cols], in_=u2[:, cols], func=ACT.Tanh,
+                    bias=shift[:, t : t + 1], scale=rstd[:, t : t + 1],
                 )
-            st[("n", g)] = n_sb
+            live[("n", g)] = n_sb
 
         def gate_product(g):
-            zh = st[("u1", g)]
-            cuts = (0, (GT - 1) * H, GW) if g + 1 < NG else (HW, GW)
-            for c0, c1 in zip(cuts[:-1], cuts[1:]):
+            zh = live[("u1", g)]
+            cuts = (0, (GROUP_TILES - 1) * H, GROUP_COLS) if g + 1 < GROUPS else (HALF_COLS, GROUP_COLS)
+            for lo, hi in zip(cuts[:-1], cuts[1:]):
                 nc.gpsimd.tensor_tensor(
-                    out=zh[:, c0:c1], in0=st[("z", g)][:, c0:c1], in1=st[("h", g)][:, c0:c1], op=ALU.mult
+                    out=zh[:, lo:hi], in0=live[("z", g)][:, lo:hi], in1=live[("h", g)][:, lo:hi], op=ALU.mult
                 )
 
         def blend(g):
-            z_sb = st[("z", g)]
-            n_sb = st[("n", g)]
-            zh = st[("u1", g)]
-            halves = (slice(0, HW), slice(HW, GW))
-            if g + 1 == NG:
-                cs = halves[0]
-                nc.vector.tensor_tensor(out=zh[:, cs], in0=z_sb[:, cs], in1=st[("h", g)][:, cs], op=ALU.mult)
-            for cs in halves:
+            z_sb = live[("z", g)]
+            n_sb = live[("n", g)]
+            zh = live[("u1", g)]
+            if g + 1 == GROUPS:
+                cols = HALVES[0]
+                nc.vector.tensor_tensor(out=zh[:, cols], in0=z_sb[:, cols], in1=live[("h", g)][:, cols], op=ALU.mult)
+            for cols in HALVES:
                 nc.vector.scalar_tensor_tensor(
-                    out=n_sb[:, cs], in0=z_sb[:, cs], scalar=1.0, in1=n_sb[:, cs],
+                    out=n_sb[:, cols], in0=z_sb[:, cols], scalar=1.0, in1=n_sb[:, cols],
                     op0=ALU.subtract, op1=ALU.mult,
                 )
-            for i, cs in enumerate(halves):
-                nc.vector.tensor_tensor(out=zh[:, cs], in0=zh[:, cs], in1=n_sb[:, cs], op=ALU.subtract)
-                c0 = g * GW + i * HW
-                nc.sync.dma_start(out=ov[:, c0 : c0 + HW], in_=zh[:, cs])
+            for i, cols in enumerate(HALVES):
+                nc.vector.tensor_tensor(out=zh[:, cols], in0=zh[:, cols], in1=n_sb[:, cols], op=ALU.subtract)
+                first_col = g * GROUP_COLS + i * HALF_COLS
+                nc.sync.dma_start(out=out_rows[:, first_col : first_col + HALF_COLS], in_=zh[:, cols])
 
-        prep_w(0)
-        front(0)
-        quantise(0)
+        transpose_group(0)
+        quantise_group(0)
         bias = []
         for i in range(2):
-            b_ps = pti.tile([P, H], F32, tag="ti")
-            nc.tensor.matmul(out=b_ps[:], lhsT=ones[:], rhs=brow[:, i * H : (i + 1) * H], start=True, stop=True)
-            b_sb = const.tile([P, H], F32, name="b_sb%d" % i)
-            nc.scalar.copy(out=b_sb[:], in_=b_ps[:])
-            bias.append(b_sb)
-        prep_w(1)
-        for s in range(NG + 2):
-            if s + 2 < NG:
-                load("x", s + 2)
-                load("h", s + 2)
-            if s + 1 < NG:
-                load("r", s + 1)
-            if 0 <= s - 1 < NG:
-                load("z", s - 1)
-            if 0 <= s - 2 < NG:
+            bias_ps = psum_t.tile([P, H], F32, tag="t")
+            nc.tensor.matmul(
+                out=bias_ps[:], lhsT=ones[:], rhs=bias_rows[:, i * H : (i + 1) * H], start=True, stop=True
+            )
+            bias_sb = const.tile([P, H], F32, name="bias_sb%d" % i)
+            nc.scalar.copy(out=bias_sb[:], in_=bias_ps[:])
+            bias.append(bias_sb)
+        for s in range(GROUPS + 2):
+            if s + 2 < GROUPS:
+                load_activations(s + 2)
+            if s + 1 < GROUPS:
+                load_gate("r", s + 1)
+            if 0 <= s - 1 < GROUPS:
+                load_gate("z", s - 1)
+            if 0 <= s - 2 < GROUPS:
                 gate_product(s - 2)
-            if 0 <= s - 1 < NG:
-                window(s - 1)
-            if s + 1 < NG:
-                front(s + 1)
-            if 0 < s < NG:
-                quantise(s)
-            if 0 <= s - 2 < NG:
+            if 0 <= s - 1 < GROUPS:
+                products_and_moments(s - 1)
+            if s + 1 < GROUPS:
+                transpose_group(s + 1)
+            if 0 < s < GROUPS:
+                quantise_group(s)
+            if 0 <= s - 2 < GROUPS:
                 blend(s - 2)
-            if 0 <= s - 1 < NG:
+            if 0 <= s - 1 < GROUPS:
                 candidate(s - 1)

@@ -5,6 +5,7 @@ from concourse.masks import make_identity
 
 F32 = mybir.dt.float32
 BF16 = mybir.dt.bfloat16
+I32 = mybir.dt.int32
 U32 = mybir.dt.uint32
 U8 = mybir.dt.uint8
 FP8X4 = mybir.dt.float8_e4m3fn_x4
@@ -22,7 +23,9 @@ GROUPS = ROW_TILES // GROUP_TILES
 GROUP_COLS = GROUP_TILES * H
 HALF_COLS = GROUP_COLS // 2
 HALVES = (slice(0, HALF_COLS), slice(HALF_COLS, GROUP_COLS))
+CH_BLOCKS = H // P
 EPS = 1e-5
+RSQRT_BITS = 1597463007.0
 
 FLOPS = 2 * 2 * B * K * H
 
@@ -44,12 +47,15 @@ def tile_layernormgrucell_pb_t_kernel(tc, x, h, r, z, W_in, b_in, W_hn, b_hn, ou
             "x": ctx.enter_context(tc.tile_pool(name="in_x", bufs=3)),
             "h": ctx.enter_context(tc.tile_pool(name="in_h", bufs=5)),
             "r": ctx.enter_context(tc.tile_pool(name="in_r", bufs=3)),
-            "z": ctx.enter_context(tc.tile_pool(name="in_z", bufs=2)),
+            "z": ctx.enter_context(tc.tile_pool(name="in_z", bufs=3)),
         }
         work = ctx.enter_context(tc.tile_pool(name="work", bufs=2))
+        candidates = ctx.enter_context(tc.tile_pool(name="candidates", bufs=3))
         small = ctx.enter_context(tc.tile_pool(name="small", bufs=3))
-        psum_t = ctx.enter_context(tc.psum_pool(name="psum_t", bufs=4))
-        psum_mx = ctx.enter_context(tc.psum_pool(name="psum_mx", bufs=4))
+        psum_t = ctx.enter_context(tc.psum_pool(name="psum_t", bufs=2))
+        psum_y = ctx.enter_context(tc.psum_pool(name="psum_y", bufs=3))
+        psum_u = ctx.enter_context(tc.psum_pool(name="psum_u", bufs=2))
+        psum_s = ctx.enter_context(tc.psum_pool(name="psum_s", bufs=1))
         ctx.enter_context(tc.manual_schedule())
 
         live = {}
@@ -63,23 +69,21 @@ def tile_layernormgrucell_pb_t_kernel(tc, x, h, r, z, W_in, b_in, W_hn, b_hn, ou
             )
 
         def load_activations(g):
-            new_input("x", g)
             new_input("h", g)
+            new_input("x", g)
             for lo in (0, HALF_COLS):
-                fetch("x", g, lo, lo + HALF_COLS)
                 fetch("h", g, lo, lo + HALF_COLS)
+                fetch("x", g, lo, lo + HALF_COLS)
 
         def load_gate(name, g):
             new_input(name, g)
             fetch(name, g, 0, GROUP_COLS)
 
-        def load_weight(i, w):
-            w_sb = const.tile([P, 4 * K], BF16, name="w_sb%d" % i)
+        def load_weight(name, w, pair):
             nc.sync.dma_start(
-                out=w_sb[:].rearrange("p (a k) -> p a k", a=4),
-                in_=w.rearrange("(a p) k -> p a k", p=P),
+                out=w_raw[name][:, pair * 2 * K : (pair + 1) * 2 * K].rearrange("p (a k) -> p a k", a=2),
+                in_=w[pair * 2 * P : (pair + 1) * 2 * P, :].rearrange("(a p) k -> p a k", p=P),
             )
-            return w_sb
 
         bias_rows = const.tile([P, 2 * H], BF16)
         nc.vector.memset(bias_rows[:], 0.0)
@@ -91,22 +95,32 @@ def tile_layernormgrucell_pb_t_kernel(tc, x, h, r, z, W_in, b_in, W_hn, b_hn, ou
         make_identity(nc, identity[:])
         eps = const.tile([P, 1], F32)
         nc.gpsimd.memset(eps[:], EPS)
-        first_sqrt = const.tile([P, 1], F32)
-        nc.scalar.activation(out=first_sqrt[:], in_=ones[:, 0:1], func=ACT.Sqrt)
+        first_tanh = const.tile([P, 1], F32)
+        nc.scalar.activation(out=first_tanh[:], in_=ones[:, 0:1], func=ACT.Tanh)
 
-        w_raw = [load_weight(0, W_in), load_weight(1, W_hn)]
-        load_activations(0)
-        load_activations(1)
+        new_input("h", 0)
+        new_input("x", 0)
+        w_raw = {}
+        for name, w in (("h", W_hn), ("x", W_in)):
+            w_raw[name] = const.tile([P, 4 * K], BF16, name="w_sb_" + name)
+            for pair in range(2):
+                load_weight(name, w, pair)
+            for lo in (0, HALF_COLS):
+                fetch(name, 0, lo, lo + HALF_COLS)
         load_gate("r", 0)
+        load_activations(1)
+        load_activations(2)
 
-        w_codes = []
-        w_scales = []
-        for i in range(2):
-            w_words = w_raw[i][:].bitcast(F32)
-            w_grouped = const.tile([P, 4 * H], BF16, name="w_grouped%d" % i, align_bytes=64)
+        w_codes = {}
+        w_scales = {}
+        w_grouped_tiles = {}
+
+        def prepare_weight(name):
+            w_words = w_raw[name][:].bitcast(F32)
+            w_grouped = const.tile([P, 4 * H], BF16, name="w_grouped_" + name, align_bytes=64)
             w_grouped_words = w_grouped[:].bitcast(F32)
             for pair in range(2):
-                w_t = psum_t.tile([P, 512], F32, tag="t")
+                w_t = psum_y.tile([P, 512], F32, tag="y")
                 for u in range(2):
                     for j in range(2):
                         a = 2 * pair + j
@@ -115,128 +129,247 @@ def tile_layernormgrucell_pb_t_kernel(tc, x, h, r, z, W_in, b_in, W_hn, b_hn, ou
                             w_words[:, a * WORDS + u * P : a * WORDS + (u + 1) * P],
                             identity[:],
                         )
-                nc.vector.tensor_copy(
+                copy_out = nc.vector.tensor_copy if pair == 0 else nc.scalar.copy
+                copy_out(
                     out=w_grouped_words[:, pair * 512 : (pair + 1) * 512].rearrange("p (n u) -> p n u", u=2),
                     in_=w_t[:].rearrange("p (u n) -> p n u", u=2),
                 )
-            codes = const.tile([P, H], U32, name="w_codes%d" % i, align_bytes=64)
-            scales = const.tile([P, H], U8, name="w_scales%d" % i, align_bytes=64)
-            nc.vector.quantize_mx(out=codes[:].bitcast(FP8X4), scales=scales[:], in_=w_grouped[:])
-            w_codes.append(codes)
-            w_scales.append(scales)
+            w_grouped_tiles[name] = w_grouped
 
-        def transpose_group(g):
-            sources = (live[("x", g)][:].bitcast(F32), live[("h", g)][:].bitcast(F32))
-            grouped = work.tile([P, 2 * GROUP_COLS], BF16, align_bytes=64)
+        def quantise_weight(name):
+            codes = const.tile([P, H], U32, name="w_codes_" + name, align_bytes=64)
+            scales = const.tile([P, H], U8, name="w_scales_" + name, align_bytes=64)
+            nc.vector.quantize_mx(out=codes[:].bitcast(FP8X4), scales=scales[:], in_=w_grouped_tiles[name][:])
+            w_codes[name] = codes
+            w_scales[name] = scales
+
+        def transpose_operand(name, g, copy_out=(nc.scalar.copy, nc.scalar.copy)):
+            words = live[(name, g)][:].bitcast(F32)
+            grouped = work.tile([P, GROUP_COLS], BF16, name="grouped_" + name, align_bytes=64)
             grouped_words = grouped[:].bitcast(F32)
-            for t in range(GROUP_TILES):
+            for pair in range(GROUP_TILES // 2):
                 bank = psum_t.tile([P, 512], F32, tag="t")
-                for o in range(2):
+                for j in range(2):
+                    t = 2 * pair + j
                     for u in range(2):
                         nc.tensor.transpose(
-                            bank[:, (2 * o + u) * P : (2 * o + u + 1) * P],
-                            sources[o][:, t * WORDS + u * P : t * WORDS + (u + 1) * P],
+                            bank[:, (2 * j + u) * P : (2 * j + u + 1) * P],
+                            words[:, t * WORDS + u * P : t * WORDS + (u + 1) * P],
                             identity[:],
                         )
-                nc.scalar.copy(
-                    out=grouped_words[:, t * 512 : (t + 1) * 512].rearrange("p (o i u) -> p o i u", o=2, u=2),
-                    in_=bank[:].rearrange("p (o u i) -> p o i u", o=2, u=2),
+                copy_out[pair](
+                    out=grouped_words[:, pair * 512 : (pair + 1) * 512].rearrange("p (j i u) -> p j i u", j=2, u=2),
+                    in_=bank[:].rearrange("p (j u i) -> p j i u", j=2, u=2),
                 )
-            live[("grouped", g)] = grouped
+            live[("grouped_" + name, g)] = grouped
 
-        def quantise_group(g):
-            grouped = live[("grouped", g)]
-            codes = work.tile([P, 2 * GROUP_TILES * P], U32, align_bytes=64)
-            scales = work.tile([P, 2 * GROUP_TILES * P], U8, align_bytes=64)
-            for i in range(2):
-                nc.vector.quantize_mx(
-                    out=codes[:, i * 512 : (i + 1) * 512].bitcast(FP8X4),
-                    scales=scales[:, i * 512 : (i + 1) * 512],
-                    in_=grouped[:, i * GROUP_COLS : (i + 1) * GROUP_COLS],
+        def quantise_operand(name, g):
+            codes = work.tile([P, GROUP_TILES * P], U32, name="codes_" + name, align_bytes=64)
+            scales = work.tile([P, GROUP_TILES * P], U8, name="scales_" + name, align_bytes=64)
+            nc.vector.quantize_mx(
+                out=codes[:].bitcast(FP8X4), scales=scales[:], in_=live[("grouped_" + name, g)][:]
+            )
+            live[("codes_" + name, g)] = codes
+            live[("scales_" + name, g)] = scales
+
+        def h_product(g, vector_blocks=()):
+            codes = live[("codes_h", g)]
+            scales = live[("scales_h", g)]
+            u2t = work.tile([P, CH_BLOCKS * 512], F32)
+            for c in range(CH_BLOCKS):
+                acc = psum_y.tile([P, 512], F32, tag="y")
+                nc.tensor.matmul_mx(
+                    out=acc[:],
+                    lhsT=w_codes["h"][:, c * P : (c + 1) * P].bitcast(FP8X4),
+                    lhsT_scale=w_scales["h"][:, c * P : (c + 1) * P],
+                    rhs=codes[:].bitcast(FP8X4),
+                    rhs_scale=scales[:],
+                    start=True,
+                    stop=True,
                 )
-            live[("codes", g)] = codes
-            live[("scales", g)] = scales
-
-        def products_and_moments(g):
-            codes = live[("codes", g)]
-            scales = live[("scales", g)]
-            u1 = work.tile([P, GROUP_COLS], F32)
-            u2 = work.tile([P, GROUP_COLS], F32)
-            sums = small.tile([P, 2 * GROUP_TILES], F32)
-            squares = small.tile([P, 2 * GROUP_TILES], F32)
-            for t in range(GROUP_TILES):
-                cols = slice(t * H, (t + 1) * H)
-                for o, u_sb in enumerate((u1, u2)):
-                    c = (2 * t + o) * P
-                    stat = slice(o * GROUP_TILES + t, o * GROUP_TILES + t + 1)
-                    acc = psum_mx.tile([P, H], F32)
-                    nc.tensor.matmul_mx(
-                        out=acc[:],
-                        lhsT=codes[:, c : c + P].bitcast(FP8X4),
-                        lhsT_scale=scales[:, c : c + P],
-                        rhs=w_codes[o][:].bitcast(FP8X4),
-                        rhs_scale=w_scales[o][:],
-                        start=True,
-                        stop=True,
+                if c in vector_blocks:
+                    nc.vector.tensor_scalar(
+                        out=u2t[:, c * 512 : (c + 1) * 512], in0=acc[:], scalar1=bias_cols[:, c : c + 1],
+                        scalar2=None, op0=ALU.add,
                     )
-                    nc.vector.scalar_tensor_tensor(
-                        out=u_sb[:, cols], in0=acc[:], scalar=1.0, in1=bias[o][:],
-                        op0=ALU.mult, op1=ALU.add, accum_out=sums[:, stat],
-                    )
-                    unused = work.tile([P, H], BF16)
+                else:
                     nc.scalar.activation(
-                        out=unused[:], in_=u_sb[:, cols], func=ACT.Square,
-                        bias=sums[:, stat], scale=-1.0 * H, accum_out=squares[:, stat],
+                        out=u2t[:, c * 512 : (c + 1) * 512], in_=acc[:], func=ACT.Identity,
+                        bias=bias_cols[:, c : c + 1], scale=1.0,
                     )
+            live[("u2t", g)] = u2t
+
+        def h_sums(g):
+            codes = live[("codes_h", g)]
+            scales = live[("scales_h", g)]
+            bank = psum_s.tile([P, 512], F32, tag="s")
+            for t in range(GROUP_TILES):
+                rows = slice(t * P, (t + 1) * P)
+                for c in range(CH_BLOCKS):
+                    nc.tensor.matmul_mx(
+                        out=bank[:, rows],
+                        lhsT=codes[:, rows].bitcast(FP8X4),
+                        lhsT_scale=scales[:, rows],
+                        rhs=w_codes["h"][:, c * P : (c + 1) * P].bitcast(FP8X4),
+                        rhs_scale=w_scales["h"][:, c * P : (c + 1) * P],
+                        start=c == 0,
+                        stop=c == CH_BLOCKS - 1,
+                    )
+            live[("sum_bank", g)] = bank
+
+        def h_means(g):
+            bank = live[("sum_bank", g)]
             minus_mean2 = small.tile([P, GROUP_TILES], F32)
-            nc.scalar.mul(out=minus_mean2[:], in_=sums[:, GROUP_TILES : 2 * GROUP_TILES], mul=-1.0 / H)
-            std = small.tile([P, 2 * GROUP_TILES], F32)
-            nc.scalar.activation(out=std[:], in_=squares[:], func=ACT.Sqrt, bias=eps[:], scale=1.0 / (H * H * H))
-            live[("u1", g)] = u1
-            live[("u2", g)] = u2
-            live[("sums", g)] = sums
+            for t in range(GROUP_TILES):
+                unused = work.tile([P, P], BF16, name="unused_means")
+                nc.scalar.activation(
+                    out=unused[:], in_=bank[:, t * P : (t + 1) * P], func=ACT.Identity,
+                    bias=mean_bias[:], scale=-1.0 / H, accum_out=minus_mean2[:, t : t + 1],
+                )
             live[("minus_mean2", g)] = minus_mean2
-            live[("std", g)] = std
+
+        def h_rows(g, t):
+            u2t = live[("u2t", g)]
+            bank = psum_u.tile([P, H], F32, tag="u")
+            for c in range(CH_BLOCKS):
+                nc.tensor.transpose(
+                    bank[:, c * P : (c + 1) * P], u2t[:, c * 512 + t * P : c * 512 + (t + 1) * P], identity[:]
+                )
+            live[("u2", g, t)] = bank
+
+        def x_product(g, t):
+            acc = psum_y.tile([P, 512], F32, tag="y")
+            nc.tensor.matmul_mx(
+                out=acc[:],
+                lhsT=live[("codes_x", g)][:, t * P : (t + 1) * P].bitcast(FP8X4),
+                lhsT_scale=live[("scales_x", g)][:, t * P : (t + 1) * P],
+                rhs=w_codes["x"][:].bitcast(FP8X4),
+                rhs_scale=w_scales["x"][:],
+                start=True,
+                stop=True,
+            )
+            live[("y1", g, t)] = acc
+
+        def new_moments(g):
+            live[("u1", g)] = work.tile([P, GROUP_COLS], F32, name="u1")
+            live[("v", g)] = work.tile([P, GROUP_COLS], F32, name="v")
+            live[("sums1", g)] = small.tile([P, GROUP_TILES], F32, name="sums1")
+            live[("squares", g)] = small.tile([P, 2 * GROUP_TILES], F32, name="squares")
+
+        def x_moments(g, t):
+            cols = slice(t * H, (t + 1) * H)
+            u1 = live[("u1", g)]
+            sums = live[("sums1", g)]
+            nc.vector.scalar_tensor_tensor(
+                out=u1[:, cols], in0=live[("y1", g, t)][:], scalar=1.0, in1=bias1[:],
+                op0=ALU.mult, op1=ALU.add, accum_out=sums[:, t : t + 1],
+            )
+            unused = work.tile([P, H], BF16, name="unused")
+            nc.scalar.activation(
+                out=unused[:], in_=u1[:, cols], func=ACT.Square,
+                bias=sums[:, t : t + 1], scale=-1.0 * H, accum_out=live[("squares", g)][:, t : t + 1],
+            )
+
+        def h_moments(g, t):
+            cols = slice(t * H, (t + 1) * H)
+            bank = live[("u2", g, t)]
+            minus_mean = live[("minus_mean2", g)][:, t : t + 1]
+            nc.vector.scalar_tensor_tensor(
+                out=live[("v", g)][:, cols], in0=bank[:], scalar=minus_mean,
+                in1=live[("r", g)][:, cols], op0=ALU.add, op1=ALU.mult,
+            )
+            unused = work.tile([P, H], BF16, name="unused")
+            nc.scalar.activation(
+                out=unused[:], in_=bank[:], func=ACT.Square,
+                bias=minus_mean, scale=1.0,
+                accum_out=live[("squares", g)][:, GROUP_TILES + t : GROUP_TILES + t + 1],
+            )
+
+        def variance(g):
+            var = small.tile([P, 2 * GROUP_TILES], F32)
+            for part, scale in ((first, 1.0 / (H * H * H)), (second, 1.0 / H)):
+                nc.scalar.activation(
+                    out=var[:, part], in_=live[("squares", g)][:, part], func=ACT.Identity, bias=eps[:], scale=scale
+                )
+            live[("var", g)] = var
+
+        first = slice(0, GROUP_TILES)
+        second = slice(GROUP_TILES, 2 * GROUP_TILES)
+
+        def root_steps(g):
+            var = live[("var", g)]
+            guess = small.tile([P, 2 * GROUP_TILES], I32, name="guess")
+            a = small.tile([P, 2 * GROUP_TILES], F32, name="root_a")
+            b = small.tile([P, 2 * GROUP_TILES], F32, name="root_b")
+            ys = [small.tile([P, 2 * GROUP_TILES], F32, name="root_y%d" % i) for i in range(3)]
+            std1 = small.tile([P, GROUP_TILES], F32, name="std1")
+            q = small.tile([P, GROUP_TILES], F32, name="q")
+            shift = small.tile([P, GROUP_TILES], F32, name="shift")
+            steps = [
+                lambda: nc.vector.tensor_scalar(
+                    out=guess[:], in0=var[:].bitcast(I32), scalar1=-0.5, scalar2=RSQRT_BITS, op0=ALU.mult, op1=ALU.add
+                )
+            ]
+            y = guess[:].bitcast(F32)
+            for i in range(3):
+                steps.append(lambda y=y: nc.vector.tensor_tensor(out=a[:], in0=y, in1=y, op=ALU.mult))
+                steps.append(
+                    lambda: nc.vector.scalar_tensor_tensor(
+                        out=b[:], in0=a[:], scalar=-0.5, in1=var[:], op0=ALU.mult, op1=ALU.mult
+                    )
+                )
+                steps.append(
+                    lambda y=y, i=i: nc.vector.scalar_tensor_tensor(
+                        out=ys[i][:], in0=b[:], scalar=1.5, in1=y, op0=ALU.add, op1=ALU.mult
+                    )
+                )
+                y = ys[i][:]
+            rstd = ys[2]
+            steps.append(
+                lambda: nc.vector.tensor_tensor(out=std1[:], in0=var[:, first], in1=rstd[:, first], op=ALU.mult)
+            )
+            steps.append(
+                lambda: nc.vector.scalar_tensor_tensor(
+                    out=shift[:], in0=live[("sums1", g)][:], scalar=-1.0 / H, in1=rstd[:, first],
+                    op0=ALU.mult, op1=ALU.mult,
+                )
+            )
+            steps.append(lambda: nc.vector.tensor_tensor(out=q[:], in0=std1[:], in1=rstd[:, second], op=ALU.mult))
+            live[("rstd", g)] = rstd
+            live[("q", g)] = q
+            live[("shift", g)] = shift
+            live[("steps", g)] = steps
+
+        def root_step(g, count=1):
+            steps = live.get(("steps", g), [])
+            for step in steps[:count]:
+                step()
+            live[("steps", g)] = steps[count:]
 
         def candidate(g):
-            u1 = live[("u1", g)]
-            u2 = live[("u2", g)]
-            r_sb = live[("r", g)]
-            std = live[("std", g)]
-            first = slice(0, GROUP_TILES)
-            second = slice(GROUP_TILES, 2 * GROUP_TILES)
-            rstd = small.tile([P, 2 * GROUP_TILES], F32)
-            nc.vector.reciprocal(out=rstd[:], in_=std[:])
+            v = live[("v", g)]
+            n_sb = candidates.tile([P, GROUP_COLS], F32, name="n_sb")
             for t in range(GROUP_TILES):
                 cols = slice(t * H, (t + 1) * H)
                 nc.vector.scalar_tensor_tensor(
-                    out=u2[:, cols], in0=u2[:, cols], scalar=live[("minus_mean2", g)][:, t : t + 1], in1=r_sb[:, cols],
-                    op0=ALU.add, op1=ALU.mult,
-                )
-            q = small.tile([P, GROUP_TILES], F32)
-            nc.vector.tensor_tensor(out=q[:], in0=std[:, first], in1=rstd[:, second], op=ALU.mult)
-            shift = small.tile([P, GROUP_TILES], F32)
-            nc.vector.scalar_tensor_tensor(
-                out=shift[:], in0=live[("sums", g)][:, first], scalar=-1.0 / H, in1=rstd[:, first],
-                op0=ALU.mult, op1=ALU.mult,
-            )
-            n_sb = work.tile([P, GROUP_COLS], F32)
-            for t in range(GROUP_TILES):
-                cols = slice(t * H, (t + 1) * H)
-                nc.vector.scalar_tensor_tensor(
-                    out=u2[:, cols], in0=u2[:, cols], scalar=q[:, t : t + 1], in1=u1[:, cols],
-                    op0=ALU.mult, op1=ALU.add,
+                    out=v[:, cols], in0=v[:, cols], scalar=live[("q", g)][:, t : t + 1],
+                    in1=live[("u1", g)][:, cols], op0=ALU.mult, op1=ALU.add,
                 )
                 nc.scalar.activation(
-                    out=n_sb[:, cols], in_=u2[:, cols], func=ACT.Tanh,
-                    bias=shift[:, t : t + 1], scale=rstd[:, t : t + 1],
+                    out=n_sb[:, cols], in_=v[:, cols], func=ACT.Tanh,
+                    bias=live[("shift", g)][:, t : t + 1], scale=live[("rstd", g)][:, t : t + 1],
                 )
+                if t > 0:
+                    root_step(g + 1)
             live[("n", g)] = n_sb
 
         def gate_product(g):
-            zh = live[("u1", g)]
-            cuts = (0, (GROUP_TILES - 1) * H, GROUP_COLS) if g + 1 < GROUPS else (HALF_COLS, GROUP_COLS)
-            for lo, hi in zip(cuts[:-1], cuts[1:]):
+            zh = live[("n", g - 1)] if g > 0 else candidates.tile([P, GROUP_COLS], F32, name="n_sb")
+            live[("zh", g)] = zh
+            if g == 0:
+                nc.vector.memset(zh[:, HALF_COLS : HALF_COLS + 1], 0.0)
+            halves = ((HALF_COLS, GROUP_COLS), (0, HALF_COLS)) if g + 1 < GROUPS else ((HALF_COLS, GROUP_COLS),)
+            for lo, hi in halves:
                 nc.gpsimd.tensor_tensor(
                     out=zh[:, lo:hi], in0=live[("z", g)][:, lo:hi], in1=live[("h", g)][:, lo:hi], op=ALU.mult
                 )
@@ -244,47 +377,123 @@ def tile_layernormgrucell_pb_t_kernel(tc, x, h, r, z, W_in, b_in, W_hn, b_hn, ou
         def blend(g):
             z_sb = live[("z", g)]
             n_sb = live[("n", g)]
-            zh = live[("u1", g)]
+            zh = live[("zh", g)]
             if g + 1 == GROUPS:
                 cols = HALVES[0]
                 nc.vector.tensor_tensor(out=zh[:, cols], in0=z_sb[:, cols], in1=live[("h", g)][:, cols], op=ALU.mult)
-            for cols in HALVES:
+            for t in range(GROUP_TILES):
+                cols = slice(t * H, (t + 1) * H)
                 nc.vector.scalar_tensor_tensor(
                     out=n_sb[:, cols], in0=z_sb[:, cols], scalar=1.0, in1=n_sb[:, cols],
                     op0=ALU.subtract, op1=ALU.mult,
                 )
+                root_step(g + 1)
             for i, cols in enumerate(HALVES):
                 nc.vector.tensor_tensor(out=zh[:, cols], in0=zh[:, cols], in1=n_sb[:, cols], op=ALU.subtract)
                 first_col = g * GROUP_COLS + i * HALF_COLS
                 nc.sync.dma_start(out=out_rows[:, first_col : first_col + HALF_COLS], in_=zh[:, cols])
+                root_step(g + 1, 99)
 
-        transpose_group(0)
-        quantise_group(0)
-        bias = []
-        for i in range(2):
-            bias_ps = psum_t.tile([P, H], F32, tag="t")
+        on_vector = nc.vector.tensor_copy
+        on_scalar = nc.scalar.copy
+        prepare_weight("h")
+        cols_bank = psum_s.tile([P, 512], F32, tag="s")
+        for c in range(CH_BLOCKS):
             nc.tensor.matmul(
-                out=bias_ps[:], lhsT=ones[:], rhs=bias_rows[:, i * H : (i + 1) * H], start=True, stop=True
+                out=cols_bank[:, c : c + 1], lhsT=bias_rows[:, H + c * P : H + (c + 1) * P], rhs=ones[:, 0:1],
+                start=True, stop=True,
             )
-            bias_sb = const.tile([P, H], F32, name="bias_sb%d" % i)
-            nc.scalar.copy(out=bias_sb[:], in_=bias_ps[:])
-            bias.append(bias_sb)
-        for s in range(GROUPS + 2):
+        sum_bank = psum_u.tile([P, 512], F32, tag="u")
+        nc.tensor.matmul(out=sum_bank[:], lhsT=ones[:], rhs=bias_rows[:, H : 2 * H], start=True, stop=True)
+        bias_bank = psum_u.tile([P, 512], F32, tag="u")
+        nc.tensor.matmul(out=bias_bank[:], lhsT=ones[:], rhs=bias_rows[:, 0:H], start=True, stop=True)
+        transpose_operand("h", 0, (on_vector, on_scalar))
+        quantise_weight("h")
+        bias_cols = const.tile([P, CH_BLOCKS], F32)
+        nc.vector.tensor_copy(out=bias_cols[:], in_=cols_bank[:, 0:CH_BLOCKS])
+        quantise_operand("h", 0)
+        prepare_weight("x")
+        transpose_operand("x", 0, (on_vector, on_scalar))
+        h_product(0, vector_blocks=(0, 2))
+        quantise_weight("x")
+        quantise_operand("x", 0)
+        unused_bias = const.tile([P, H], BF16)
+        mean_bias = const.tile([P, 1], F32)
+        nc.scalar.activation(
+            out=unused_bias[:], in_=sum_bank[:], func=ACT.Copy, scale=-1.0 / (H * P), accum_out=mean_bias[:]
+        )
+        bias1 = const.tile([P, H], F32)
+        nc.scalar.copy(out=bias1[:], in_=bias_bank[:])
+        h_sums(0)
+        h_means(0)
+        for t in range(3):
+            x_product(0, t)
+        for t in range(2):
+            h_rows(0, t)
+
+        def window(a):
+            new_moments(a)
+            for t in range(GROUP_TILES):
+                x_moments(a, t)
+                if t == 0:
+                    x_product(a, 3)
+                h_moments(a, t)
+                if t < 2:
+                    h_rows(a, t + 2)
+            variance(a)
+            root_steps(a)
+
+        def load_step(s):
             if s + 2 < GROUPS:
                 load_activations(s + 2)
-            if s + 1 < GROUPS:
-                load_gate("r", s + 1)
-            if 0 <= s - 1 < GROUPS:
+            if s < GROUPS:
+                load_gate("r", s)
+            if s - 1 < GROUPS:
                 load_gate("z", s - 1)
-            if 0 <= s - 2 < GROUPS:
-                gate_product(s - 2)
-            if 0 <= s - 1 < GROUPS:
-                products_and_moments(s - 1)
+
+        load_step(1)
+        window(0)
+        transpose_operand("h", 1, (on_vector, on_vector))
+        root_step(0, 1)
+        transpose_operand("x", 1, (on_vector, on_scalar))
+        root_step(0, 1)
+        transpose_operand("h", 2)
+        quantise_operand("h", 1)
+        root_step(0, 1)
+        h_product(1, vector_blocks=(1,))
+        root_step(0, 1)
+        quantise_operand("x", 1)
+        h_sums(1)
+        h_means(1)
+        transpose_operand("x", 2)
+        root_step(0, 99)
+        for t in range(3):
+            x_product(1, t)
+        for t in range(2):
+            h_rows(1, t)
+        for s in range(2, GROUPS + 2):
+            a = s - 1
+            b = s - 2
+            load_step(s)
+            gate_product(b)
+            if a < GROUPS:
+                window(a)
+            candidate(b)
             if s + 1 < GROUPS:
-                transpose_group(s + 1)
-            if 0 < s < GROUPS:
-                quantise_group(s)
-            if 0 <= s - 2 < GROUPS:
-                blend(s - 2)
-            if 0 <= s - 1 < GROUPS:
-                candidate(s - 1)
+                transpose_operand("h", s + 1)
+            if s < GROUPS:
+                quantise_operand("h", s)
+                root_step(a)
+                h_product(s)
+                h_sums(s)
+                h_means(s)
+            if s + 1 < GROUPS:
+                transpose_operand("x", s + 1)
+            if s < GROUPS:
+                quantise_operand("x", s)
+                root_step(a)
+                for t in range(3):
+                    x_product(s, t)
+                for t in range(2):
+                    h_rows(s, t)
+            blend(b)

@@ -53,8 +53,8 @@ def tile_layernormgrucell_pb_t_kernel(tc, x, h, r, z, W_in, b_in, W_hn, b_hn, ou
         candidates = ctx.enter_context(tc.tile_pool(name="candidates", bufs=3))
         small = ctx.enter_context(tc.tile_pool(name="small", bufs=3))
         psum_t = ctx.enter_context(tc.psum_pool(name="psum_t", bufs=2))
-        psum_y = ctx.enter_context(tc.psum_pool(name="psum_y", bufs=3))
-        psum_u = ctx.enter_context(tc.psum_pool(name="psum_u", bufs=2))
+        psum_y = ctx.enter_context(tc.psum_pool(name="psum_y", bufs=2))
+        psum_u = ctx.enter_context(tc.psum_pool(name="psum_u", bufs=3))
         psum_s = ctx.enter_context(tc.psum_pool(name="psum_s", bufs=1))
         ctx.enter_context(tc.manual_schedule())
 
@@ -172,32 +172,34 @@ def tile_layernormgrucell_pb_t_kernel(tc, x, h, r, z, W_in, b_in, W_hn, b_hn, ou
             live[("codes_" + name, g)] = codes
             live[("scales_" + name, g)] = scales
 
-        def h_product(g, vector_blocks=()):
-            codes = live[("codes_h", g)]
-            scales = live[("scales_h", g)]
-            u2t = work.tile([P, CH_BLOCKS * 512], F32)
-            for c in range(CH_BLOCKS):
-                acc = psum_y.tile([P, 512], F32, tag="y")
-                nc.tensor.matmul_mx(
-                    out=acc[:],
-                    lhsT=w_codes["h"][:, c * P : (c + 1) * P].bitcast(FP8X4),
-                    lhsT_scale=w_scales["h"][:, c * P : (c + 1) * P],
-                    rhs=codes[:].bitcast(FP8X4),
-                    rhs_scale=scales[:],
-                    start=True,
-                    stop=True,
+        def h_block(g, c, on_vector=False):
+            if c == 0:
+                live[("u2t", g)] = work.tile([P, CH_BLOCKS * 512], F32, name="u2t")
+            u2t = live[("u2t", g)]
+            acc = psum_y.tile([P, 512], F32, tag="y")
+            nc.tensor.matmul_mx(
+                out=acc[:],
+                lhsT=w_codes["h"][:, c * P : (c + 1) * P].bitcast(FP8X4),
+                lhsT_scale=w_scales["h"][:, c * P : (c + 1) * P],
+                rhs=live[("codes_h", g)][:].bitcast(FP8X4),
+                rhs_scale=live[("scales_h", g)][:],
+                start=True,
+                stop=True,
+            )
+            if on_vector:
+                nc.vector.tensor_scalar(
+                    out=u2t[:, c * 512 : (c + 1) * 512], in0=acc[:], scalar1=bias_cols[:, c : c + 1],
+                    scalar2=None, op0=ALU.add,
                 )
-                if c in vector_blocks:
-                    nc.vector.tensor_scalar(
-                        out=u2t[:, c * 512 : (c + 1) * 512], in0=acc[:], scalar1=bias_cols[:, c : c + 1],
-                        scalar2=None, op0=ALU.add,
-                    )
-                else:
-                    nc.scalar.activation(
-                        out=u2t[:, c * 512 : (c + 1) * 512], in_=acc[:], func=ACT.Identity,
-                        bias=bias_cols[:, c : c + 1], scale=1.0,
-                    )
-            live[("u2t", g)] = u2t
+            else:
+                nc.scalar.activation(
+                    out=u2t[:, c * 512 : (c + 1) * 512], in_=acc[:], func=ACT.Identity,
+                    bias=bias_cols[:, c : c + 1], scale=1.0,
+                )
+
+        def h_product(g, vector_blocks=()):
+            for c in range(CH_BLOCKS):
+                h_block(g, c, c in vector_blocks)
 
         def h_sums(g):
             codes = live[("codes_h", g)]
@@ -346,22 +348,22 @@ def tile_layernormgrucell_pb_t_kernel(tc, x, h, r, z, W_in, b_in, W_hn, b_hn, ou
                 step()
             live[("steps", g)] = steps[count:]
 
-        def candidate(g):
+        def combine(g, t):
+            cols = slice(t * H, (t + 1) * H)
             v = live[("v", g)]
-            n_sb = candidates.tile([P, GROUP_COLS], F32, name="n_sb")
-            for t in range(GROUP_TILES):
-                cols = slice(t * H, (t + 1) * H)
-                nc.vector.scalar_tensor_tensor(
-                    out=v[:, cols], in0=v[:, cols], scalar=live[("q", g)][:, t : t + 1],
-                    in1=live[("u1", g)][:, cols], op0=ALU.mult, op1=ALU.add,
-                )
-                nc.scalar.activation(
-                    out=n_sb[:, cols], in_=v[:, cols], func=ACT.Tanh,
-                    bias=live[("shift", g)][:, t : t + 1], scale=live[("rstd", g)][:, t : t + 1],
-                )
-                if t > 0:
-                    root_step(g + 1)
-            live[("n", g)] = n_sb
+            nc.vector.scalar_tensor_tensor(
+                out=v[:, cols], in0=v[:, cols], scalar=live[("q", g)][:, t : t + 1],
+                in1=live[("u1", g)][:, cols], op0=ALU.mult, op1=ALU.add,
+            )
+
+        def squash(g, t):
+            if t == 0:
+                live[("n", g)] = candidates.tile([P, GROUP_COLS], F32, name="n_sb")
+            cols = slice(t * H, (t + 1) * H)
+            nc.scalar.activation(
+                out=live[("n", g)][:, cols], in_=live[("v", g)][:, cols], func=ACT.Tanh,
+                bias=live[("shift", g)][:, t : t + 1], scale=live[("rstd", g)][:, t : t + 1],
+            )
 
         def gate_product(g):
             zh = live[("n", g - 1)] if g > 0 else candidates.tile([P, GROUP_COLS], F32, name="n_sb")
@@ -374,13 +376,9 @@ def tile_layernormgrucell_pb_t_kernel(tc, x, h, r, z, W_in, b_in, W_hn, b_hn, ou
                     out=zh[:, lo:hi], in0=live[("z", g)][:, lo:hi], in1=live[("h", g)][:, lo:hi], op=ALU.mult
                 )
 
-        def blend(g):
+        def weigh(g):
             z_sb = live[("z", g)]
             n_sb = live[("n", g)]
-            zh = live[("zh", g)]
-            if g + 1 == GROUPS:
-                cols = HALVES[0]
-                nc.vector.tensor_tensor(out=zh[:, cols], in0=z_sb[:, cols], in1=live[("h", g)][:, cols], op=ALU.mult)
             for t in range(GROUP_TILES):
                 cols = slice(t * H, (t + 1) * H)
                 nc.vector.scalar_tensor_tensor(
@@ -388,11 +386,22 @@ def tile_layernormgrucell_pb_t_kernel(tc, x, h, r, z, W_in, b_in, W_hn, b_hn, ou
                     op0=ALU.subtract, op1=ALU.mult,
                 )
                 root_step(g + 1)
-            for i, cols in enumerate(HALVES):
+        def blend(g):
+            n_sb = live[("n", g)]
+            zh = live[("zh", g)]
+            if g + 1 == GROUPS:
+                cols = HALVES[0]
+                nc.vector.tensor_tensor(
+                    out=zh[:, cols], in0=live[("z", g)][:, cols], in1=live[("h", g)][:, cols], op=ALU.mult
+                )
+            for t in range(GROUP_TILES):
+                cols = slice(t * H, (t + 1) * H)
                 nc.vector.tensor_tensor(out=zh[:, cols], in0=zh[:, cols], in1=n_sb[:, cols], op=ALU.subtract)
-                first_col = g * GROUP_COLS + i * HALF_COLS
-                nc.sync.dma_start(out=out_rows[:, first_col : first_col + HALF_COLS], in_=zh[:, cols])
-                root_step(g + 1, 99)
+                if t % 2 == 1:
+                    half = HALVES[t // 2]
+                    first_col = g * GROUP_COLS + half.start
+                    nc.sync.dma_start(out=out_rows[:, first_col : first_col + HALF_COLS], in_=zh[:, half])
+                root_step(g + 1, 99 if t == GROUP_TILES - 2 else 1)
 
         on_vector = nc.vector.tensor_copy
         on_scalar = nc.scalar.copy
@@ -403,10 +412,6 @@ def tile_layernormgrucell_pb_t_kernel(tc, x, h, r, z, W_in, b_in, W_hn, b_hn, ou
                 out=cols_bank[:, c : c + 1], lhsT=bias_rows[:, H + c * P : H + (c + 1) * P], rhs=ones[:, 0:1],
                 start=True, stop=True,
             )
-        sum_bank = psum_u.tile([P, 512], F32, tag="u")
-        nc.tensor.matmul(out=sum_bank[:], lhsT=ones[:], rhs=bias_rows[:, H : 2 * H], start=True, stop=True)
-        bias_bank = psum_u.tile([P, 512], F32, tag="u")
-        nc.tensor.matmul(out=bias_bank[:], lhsT=ones[:], rhs=bias_rows[:, 0:H], start=True, stop=True)
         transpose_operand("h", 0, (on_vector, on_scalar))
         quantise_weight("h")
         bias_cols = const.tile([P, CH_BLOCKS], F32)
@@ -414,32 +419,39 @@ def tile_layernormgrucell_pb_t_kernel(tc, x, h, r, z, W_in, b_in, W_hn, b_hn, ou
         quantise_operand("h", 0)
         prepare_weight("x")
         transpose_operand("x", 0, (on_vector, on_scalar))
-        h_product(0, vector_blocks=(0, 2))
+        h_block(0, 0, True)
         quantise_weight("x")
+        h_block(0, 1)
+        h_block(0, 2, True)
         quantise_operand("x", 0)
+        h_block(0, 3)
+        sum_bank = psum_u.tile([P, 512], F32, tag="u")
+        nc.tensor.matmul(out=sum_bank[:], lhsT=ones[:], rhs=bias_rows[:, H : 2 * H], start=True, stop=True)
         unused_bias = const.tile([P, H], BF16)
         mean_bias = const.tile([P, 1], F32)
         nc.scalar.activation(
             out=unused_bias[:], in_=sum_bank[:], func=ACT.Copy, scale=-1.0 / (H * P), accum_out=mean_bias[:]
         )
+        bias_bank = psum_u.tile([P, 512], F32, tag="u")
+        nc.tensor.matmul(out=bias_bank[:], lhsT=ones[:], rhs=bias_rows[:, 0:H], start=True, stop=True)
         bias1 = const.tile([P, H], F32)
         nc.scalar.copy(out=bias1[:], in_=bias_bank[:])
+        for t in range(2):
+            x_product(0, t)
         h_sums(0)
         h_means(0)
         for t in range(3):
-            x_product(0, t)
-        for t in range(2):
             h_rows(0, t)
 
         def window(a):
             new_moments(a)
             for t in range(GROUP_TILES):
                 x_moments(a, t)
-                if t == 0:
-                    x_product(a, 3)
-                h_moments(a, t)
                 if t < 2:
-                    h_rows(a, t + 2)
+                    x_product(a, t + 2)
+                h_moments(a, t)
+                if t < 1:
+                    h_rows(a, t + 3)
             variance(a)
             root_steps(a)
 
@@ -467,10 +479,11 @@ def tile_layernormgrucell_pb_t_kernel(tc, x, h, r, z, W_in, b_in, W_hn, b_hn, ou
         h_means(1)
         transpose_operand("x", 2)
         root_step(0, 99)
-        for t in range(3):
-            x_product(1, t)
         for t in range(2):
+            x_product(1, t)
+        for t in range(3):
             h_rows(1, t)
+        quantise_operand("h", 2)
         for s in range(2, GROUPS + 2):
             a = s - 1
             b = s - 2
@@ -478,22 +491,29 @@ def tile_layernormgrucell_pb_t_kernel(tc, x, h, r, z, W_in, b_in, W_hn, b_hn, ou
             gate_product(b)
             if a < GROUPS:
                 window(a)
-            candidate(b)
+            if s == 2:
+                quantise_operand("x", 2)
+            if s < GROUPS:
+                h_sums(s)
+            for t in range(GROUP_TILES):
+                combine(b, t)
+                squash(b, t)
+                if t > 0:
+                    root_step(a)
             if s + 1 < GROUPS:
                 transpose_operand("h", s + 1)
-            if s < GROUPS:
-                quantise_operand("h", s)
-                root_step(a)
-                h_product(s)
-                h_sums(s)
-                h_means(s)
-            if s + 1 < GROUPS:
                 transpose_operand("x", s + 1)
-            if s < GROUPS:
-                quantise_operand("x", s)
+            weigh(b)
+            if s + 1 < GROUPS:
+                quantise_operand("h", s + 1)
                 root_step(a)
-                for t in range(3):
-                    x_product(s, t)
+                quantise_operand("x", s + 1)
+                root_step(a)
+            if s < GROUPS:
+                h_product(s)
                 for t in range(2):
+                    x_product(s, t)
+                for t in range(3):
                     h_rows(s, t)
+                h_means(s)
             blend(b)

@@ -50,11 +50,9 @@ def tile_layernormgrucell_pb_t_kernel(tc, x, h, r, z, W_in, b_in, W_hn, b_hn, ou
             "z": ctx.enter_context(tc.tile_pool(name="in_z", bufs=3)),
         }
         work = ctx.enter_context(tc.tile_pool(name="work", bufs=2))
-        candidates = ctx.enter_context(tc.tile_pool(name="candidates", bufs=3))
+        candidates = ctx.enter_context(tc.tile_pool(name="candidates", bufs=4))
         small = ctx.enter_context(tc.tile_pool(name="small", bufs=3))
-        psum_t = ctx.enter_context(tc.psum_pool(name="psum_t", bufs=2))
-        psum_y = ctx.enter_context(tc.psum_pool(name="psum_y", bufs=2))
-        psum_u = ctx.enter_context(tc.psum_pool(name="psum_u", bufs=3))
+        psum = ctx.enter_context(tc.psum_pool(name="psum", bufs=7))
         psum_s = ctx.enter_context(tc.psum_pool(name="psum_s", bufs=1))
         ctx.enter_context(tc.manual_schedule())
 
@@ -108,6 +106,7 @@ def tile_layernormgrucell_pb_t_kernel(tc, x, h, r, z, W_in, b_in, W_hn, b_hn, ou
             for lo in (0, HALF_COLS):
                 fetch(name, 0, lo, lo + HALF_COLS)
         load_gate("r", 0)
+        load_gate("z", 0)
         load_activations(1)
         load_activations(2)
 
@@ -115,12 +114,12 @@ def tile_layernormgrucell_pb_t_kernel(tc, x, h, r, z, W_in, b_in, W_hn, b_hn, ou
         w_scales = {}
         w_grouped_tiles = {}
 
-        def prepare_weight(name):
+        def prepare_weight(name, copy_out=(nc.vector.tensor_copy, nc.scalar.copy)):
             w_words = w_raw[name][:].bitcast(F32)
             w_grouped = const.tile([P, 4 * H], BF16, name="w_grouped_" + name, align_bytes=64)
             w_grouped_words = w_grouped[:].bitcast(F32)
             for pair in range(2):
-                w_t = psum_y.tile([P, 512], F32, tag="y")
+                w_t = psum.tile([P, 512], F32, tag="bank")
                 for u in range(2):
                     for j in range(2):
                         a = 2 * pair + j
@@ -129,8 +128,7 @@ def tile_layernormgrucell_pb_t_kernel(tc, x, h, r, z, W_in, b_in, W_hn, b_hn, ou
                             w_words[:, a * WORDS + u * P : a * WORDS + (u + 1) * P],
                             identity[:],
                         )
-                copy_out = nc.vector.tensor_copy if pair == 0 else nc.scalar.copy
-                copy_out(
+                copy_out[pair](
                     out=w_grouped_words[:, pair * 512 : (pair + 1) * 512].rearrange("p (n u) -> p n u", u=2),
                     in_=w_t[:].rearrange("p (u n) -> p n u", u=2),
                 )
@@ -148,7 +146,7 @@ def tile_layernormgrucell_pb_t_kernel(tc, x, h, r, z, W_in, b_in, W_hn, b_hn, ou
             grouped = work.tile([P, GROUP_COLS], BF16, name="grouped_" + name, align_bytes=64)
             grouped_words = grouped[:].bitcast(F32)
             for pair in range(GROUP_TILES // 2):
-                bank = psum_t.tile([P, 512], F32, tag="t")
+                bank = psum.tile([P, 512], F32, tag="bank")
                 for j in range(2):
                     t = 2 * pair + j
                     for u in range(2):
@@ -176,7 +174,7 @@ def tile_layernormgrucell_pb_t_kernel(tc, x, h, r, z, W_in, b_in, W_hn, b_hn, ou
             if c == 0:
                 live[("u2t", g)] = work.tile([P, CH_BLOCKS * 512], F32, name="u2t")
             u2t = live[("u2t", g)]
-            acc = psum_y.tile([P, 512], F32, tag="y")
+            acc = psum.tile([P, 512], F32, tag="bank")
             nc.tensor.matmul_mx(
                 out=acc[:],
                 lhsT=w_codes["h"][:, c * P : (c + 1) * P].bitcast(FP8X4),
@@ -232,7 +230,7 @@ def tile_layernormgrucell_pb_t_kernel(tc, x, h, r, z, W_in, b_in, W_hn, b_hn, ou
 
         def h_rows(g, t):
             u2t = live[("u2t", g)]
-            bank = psum_u.tile([P, H], F32, tag="u")
+            bank = psum.tile([P, 512], F32, tag="bank")
             for c in range(CH_BLOCKS):
                 nc.tensor.transpose(
                     bank[:, c * P : (c + 1) * P], u2t[:, c * 512 + t * P : c * 512 + (t + 1) * P], identity[:]
@@ -240,7 +238,7 @@ def tile_layernormgrucell_pb_t_kernel(tc, x, h, r, z, W_in, b_in, W_hn, b_hn, ou
             live[("u2", g, t)] = bank
 
         def x_product(g, t):
-            acc = psum_y.tile([P, 512], F32, tag="y")
+            acc = psum.tile([P, 512], F32, tag="bank")
             nc.tensor.matmul_mx(
                 out=acc[:],
                 lhsT=live[("codes_x", g)][:, t * P : (t + 1) * P].bitcast(FP8X4),
@@ -257,6 +255,8 @@ def tile_layernormgrucell_pb_t_kernel(tc, x, h, r, z, W_in, b_in, W_hn, b_hn, ou
             live[("v", g)] = work.tile([P, GROUP_COLS], F32, name="v")
             live[("sums1", g)] = small.tile([P, GROUP_TILES], F32, name="sums1")
             live[("squares", g)] = small.tile([P, 2 * GROUP_TILES], F32, name="squares")
+            if g == 0:
+                live[("sums2", g)] = small.tile([P, GROUP_TILES], F32, name="sums2")
 
         def x_moments(g, t):
             cols = slice(t * H, (t + 1) * H)
@@ -270,6 +270,42 @@ def tile_layernormgrucell_pb_t_kernel(tc, x, h, r, z, W_in, b_in, W_hn, b_hn, ou
             nc.scalar.activation(
                 out=unused[:], in_=u1[:, cols], func=ACT.Square,
                 bias=sums[:, t : t + 1], scale=-1.0 * H, accum_out=live[("squares", g)][:, t : t + 1],
+            )
+
+        def h_row_product(g, t):
+            acc = psum.tile([P, 512], F32, tag="bank")
+            nc.tensor.matmul_mx(
+                out=acc[:],
+                lhsT=live[("codes_h", g)][:, t * P : (t + 1) * P].bitcast(FP8X4),
+                lhsT_scale=live[("scales_h", g)][:, t * P : (t + 1) * P],
+                rhs=w_codes["h"][:].bitcast(FP8X4),
+                rhs_scale=w_scales["h"][:],
+                start=True,
+                stop=True,
+            )
+            live[("y2", g, t)] = acc
+
+        def h_row_moments(g, t):
+            cols = slice(t * H, (t + 1) * H)
+            v = live[("v", g)]
+            sums = live[("sums2", g)]
+            nc.vector.scalar_tensor_tensor(
+                out=v[:, cols], in0=live[("y2", g, t)][:], scalar=1.0, in1=bias2[:],
+                op0=ALU.mult, op1=ALU.add, accum_out=sums[:, t : t + 1],
+            )
+            unused = work.tile([P, H], BF16, name="unused")
+            nc.scalar.activation(
+                out=unused[:], in_=v[:, cols], func=ACT.Square,
+                bias=sums[:, t : t + 1], scale=-1.0 * H,
+                accum_out=live[("squares", g)][:, GROUP_TILES + t : GROUP_TILES + t + 1],
+            )
+
+        def reset_row(g, t):
+            cols = slice(t * H, (t + 1) * H)
+            v = live[("v", g)]
+            nc.vector.scalar_tensor_tensor(
+                out=v[:, cols], in0=v[:, cols], scalar=live[("minus_mean2", g)][:, t : t + 1],
+                in1=live[("r", g)][:, cols], op0=ALU.add, op1=ALU.mult,
             )
 
         def h_moments(g, t):
@@ -289,7 +325,7 @@ def tile_layernormgrucell_pb_t_kernel(tc, x, h, r, z, W_in, b_in, W_hn, b_hn, ou
 
         def variance(g):
             var = small.tile([P, 2 * GROUP_TILES], F32)
-            for part, scale in ((first, 1.0 / (H * H * H)), (second, 1.0 / H)):
+            for part, scale in ((first, 1.0 / (H * H * H)), (second, 1.0 / (H * H * H) if g == 0 else 1.0 / H)):
                 nc.scalar.activation(
                     out=var[:, part], in_=live[("squares", g)][:, part], func=ACT.Identity, bias=eps[:], scale=scale
                 )
@@ -366,12 +402,11 @@ def tile_layernormgrucell_pb_t_kernel(tc, x, h, r, z, W_in, b_in, W_hn, b_hn, ou
             )
 
         def gate_product(g):
-            zh = live[("n", g - 1)] if g > 0 else candidates.tile([P, GROUP_COLS], F32, name="n_sb")
+            zh = live[("n", g - 2)] if g > 1 else candidates.tile([P, GROUP_COLS], F32, name="n_sb")
             live[("zh", g)] = zh
-            if g == 0:
+            if g == 1:
                 nc.vector.memset(zh[:, HALF_COLS : HALF_COLS + 1], 0.0)
-            halves = ((HALF_COLS, GROUP_COLS), (0, HALF_COLS)) if g + 1 < GROUPS else ((HALF_COLS, GROUP_COLS),)
-            for lo, hi in halves:
+            for lo, hi in ((HALF_COLS, GROUP_COLS), (0, HALF_COLS)):
                 nc.gpsimd.tensor_tensor(
                     out=zh[:, lo:hi], in0=live[("z", g)][:, lo:hi], in1=live[("h", g)][:, lo:hi], op=ALU.mult
                 )
@@ -389,11 +424,6 @@ def tile_layernormgrucell_pb_t_kernel(tc, x, h, r, z, W_in, b_in, W_hn, b_hn, ou
         def blend(g):
             n_sb = live[("n", g)]
             zh = live[("zh", g)]
-            if g + 1 == GROUPS:
-                cols = HALVES[0]
-                nc.vector.tensor_tensor(
-                    out=zh[:, cols], in0=live[("z", g)][:, cols], in1=live[("h", g)][:, cols], op=ALU.mult
-                )
             for t in range(GROUP_TILES):
                 cols = slice(t * H, (t + 1) * H)
                 nc.vector.tensor_tensor(out=zh[:, cols], in0=zh[:, cols], in1=n_sb[:, cols], op=ALU.subtract)
@@ -406,42 +436,42 @@ def tile_layernormgrucell_pb_t_kernel(tc, x, h, r, z, W_in, b_in, W_hn, b_hn, ou
         on_vector = nc.vector.tensor_copy
         on_scalar = nc.scalar.copy
         prepare_weight("h")
+        bias2_bank = psum.tile([P, 512], F32, tag="bank")
+        nc.tensor.matmul(out=bias2_bank[:], lhsT=ones[:], rhs=bias_rows[:, H : 2 * H], start=True, stop=True)
+        bias2 = const.tile([P, H], F32)
+        bias_sum = const.tile([P, 1], F32)
+        mean_bias = const.tile([P, 1], F32)
+        nc.scalar.activation(out=bias2[:], in_=bias2_bank[:], func=ACT.Copy, scale=1.0, accum_out=bias_sum[:])
+        nc.scalar.mul(out=mean_bias[:], in_=bias_sum[:], mul=-1.0 / (H * P))
+        transpose_operand("h", 0, (on_vector, on_scalar))
+        quantise_weight("h")
+        quantise_operand("h", 0)
+        prepare_weight("x", (on_scalar, on_scalar))
+        new_moments(0)
+        for t in range(GROUP_TILES):
+            h_row_product(0, t)
+        transpose_operand("x", 0, (on_scalar, on_scalar))
+        bias_bank = psum_s.tile([P, 512], F32, tag="s")
+        nc.tensor.matmul(out=bias_bank[:], lhsT=ones[:], rhs=bias_rows[:, 0:H], start=True, stop=True)
+        bias1 = const.tile([P, H], F32)
+        nc.scalar.copy(out=bias1[:], in_=bias_bank[:])
+        for t in range(GROUP_TILES):
+            h_row_moments(0, t)
+        quantise_weight("x")
+        quantise_operand("x", 0)
         cols_bank = psum_s.tile([P, 512], F32, tag="s")
         for c in range(CH_BLOCKS):
             nc.tensor.matmul(
                 out=cols_bank[:, c : c + 1], lhsT=bias_rows[:, H + c * P : H + (c + 1) * P], rhs=ones[:, 0:1],
                 start=True, stop=True,
             )
-        transpose_operand("h", 0, (on_vector, on_scalar))
-        quantise_weight("h")
         bias_cols = const.tile([P, CH_BLOCKS], F32)
-        nc.vector.tensor_copy(out=bias_cols[:], in_=cols_bank[:, 0:CH_BLOCKS])
-        quantise_operand("h", 0)
-        prepare_weight("x")
-        transpose_operand("x", 0, (on_vector, on_scalar))
-        h_block(0, 0, True)
-        quantise_weight("x")
-        h_block(0, 1)
-        h_block(0, 2, True)
-        quantise_operand("x", 0)
-        h_block(0, 3)
-        sum_bank = psum_u.tile([P, 512], F32, tag="u")
-        nc.tensor.matmul(out=sum_bank[:], lhsT=ones[:], rhs=bias_rows[:, H : 2 * H], start=True, stop=True)
-        unused_bias = const.tile([P, H], BF16)
-        mean_bias = const.tile([P, 1], F32)
-        nc.scalar.activation(
-            out=unused_bias[:], in_=sum_bank[:], func=ACT.Copy, scale=-1.0 / (H * P), accum_out=mean_bias[:]
-        )
-        bias_bank = psum_u.tile([P, 512], F32, tag="u")
-        nc.tensor.matmul(out=bias_bank[:], lhsT=ones[:], rhs=bias_rows[:, 0:H], start=True, stop=True)
-        bias1 = const.tile([P, H], F32)
-        nc.scalar.copy(out=bias1[:], in_=bias_bank[:])
-        for t in range(2):
+        nc.scalar.copy(out=bias_cols[:], in_=cols_bank[:, 0:CH_BLOCKS])
+        for t in range(GROUP_TILES):
             x_product(0, t)
-        h_sums(0)
-        h_means(0)
-        for t in range(3):
-            h_rows(0, t)
+        minus_mean2 = small.tile([P, GROUP_TILES], F32, name="minus_mean2_0")
+        nc.scalar.mul(out=minus_mean2[:], in_=live[("sums2", 0)][:], mul=-1.0 / H)
+        live[("minus_mean2", 0)] = minus_mean2
 
         def window(a):
             new_moments(a)
@@ -460,38 +490,42 @@ def tile_layernormgrucell_pb_t_kernel(tc, x, h, r, z, W_in, b_in, W_hn, b_hn, ou
                 load_activations(s + 2)
             if s < GROUPS:
                 load_gate("r", s)
-            if s - 1 < GROUPS:
-                load_gate("z", s - 1)
+                load_gate("z", s)
 
         load_step(1)
-        window(0)
+        gate_product(0)
+        for t in range(GROUP_TILES):
+            x_moments(0, t)
         transpose_operand("h", 1, (on_vector, on_vector))
-        root_step(0, 1)
-        transpose_operand("x", 1, (on_vector, on_scalar))
-        root_step(0, 1)
-        transpose_operand("h", 2)
+        transpose_operand("x", 1, (on_scalar, on_scalar))
+        variance(0)
+        root_steps(0)
         quantise_operand("h", 1)
-        root_step(0, 1)
-        h_product(1, vector_blocks=(1,))
-        root_step(0, 1)
-        quantise_operand("x", 1)
-        h_sums(1)
-        h_means(1)
+        h_product(1)
+        transpose_operand("h", 2)
         transpose_operand("x", 2)
+        for t in range(GROUP_TILES):
+            reset_row(0, t)
+            root_step(0, 2)
+            if t == 1:
+                quantise_operand("x", 1)
+                root_step(0)
         root_step(0, 99)
+        h_sums(1)
         for t in range(2):
             x_product(1, t)
         for t in range(3):
             h_rows(1, t)
-        quantise_operand("h", 2)
+        h_means(1)
         for s in range(2, GROUPS + 2):
             a = s - 1
             b = s - 2
             load_step(s)
-            gate_product(b)
             if a < GROUPS:
+                gate_product(a)
                 window(a)
             if s == 2:
+                quantise_operand("h", 2)
                 quantise_operand("x", 2)
             if s < GROUPS:
                 h_sums(s)

@@ -20,6 +20,8 @@ WORDS = K // 2
 ROW_TILES = B // P
 GROUP_TILES = 4
 GROUPS = ROW_TILES // GROUP_TILES
+LAST = GROUPS - 1
+ROW_GROUPS = (0, 1)
 GROUP_COLS = GROUP_TILES * H
 HALF_COLS = GROUP_COLS // 2
 HALVES = (slice(0, HALF_COLS), slice(HALF_COLS, GROUP_COLS))
@@ -106,8 +108,8 @@ def tile_layernormgrucell_pb_t_kernel(tc, x, h, r, z, W_in, b_in, W_hn, b_hn, ou
             for lo in (0, HALF_COLS):
                 fetch(name, 0, lo, lo + HALF_COLS)
         load_gate("r", 0)
-        load_gate("z", 0)
         load_activations(1)
+        load_gate("z", 0)
         load_activations(2)
 
         w_codes = {}
@@ -255,7 +257,7 @@ def tile_layernormgrucell_pb_t_kernel(tc, x, h, r, z, W_in, b_in, W_hn, b_hn, ou
             live[("v", g)] = work.tile([P, GROUP_COLS], F32, name="v")
             live[("sums1", g)] = small.tile([P, GROUP_TILES], F32, name="sums1")
             live[("squares", g)] = small.tile([P, 2 * GROUP_TILES], F32, name="squares")
-            if g == 0:
+            if g in ROW_GROUPS:
                 live[("sums2", g)] = small.tile([P, GROUP_TILES], F32, name="sums2")
 
         def x_moments(g, t):
@@ -300,6 +302,11 @@ def tile_layernormgrucell_pb_t_kernel(tc, x, h, r, z, W_in, b_in, W_hn, b_hn, ou
                 accum_out=live[("squares", g)][:, GROUP_TILES + t : GROUP_TILES + t + 1],
             )
 
+        def row_means(g):
+            minus_mean2 = small.tile([P, GROUP_TILES], F32, name="minus_mean2_0")
+            nc.scalar.mul(out=minus_mean2[:], in_=live[("sums2", g)][:], mul=-1.0 / H)
+            live[("minus_mean2", g)] = minus_mean2
+
         def reset_row(g, t):
             cols = slice(t * H, (t + 1) * H)
             v = live[("v", g)]
@@ -325,7 +332,7 @@ def tile_layernormgrucell_pb_t_kernel(tc, x, h, r, z, W_in, b_in, W_hn, b_hn, ou
 
         def variance(g):
             var = small.tile([P, 2 * GROUP_TILES], F32)
-            for part, scale in ((first, 1.0 / (H * H * H)), (second, 1.0 / (H * H * H) if g == 0 else 1.0 / H)):
+            for part, scale in ((first, 1.0 / (H * H * H)), (second, 1.0 / (H * H * H) if g in ROW_GROUPS else 1.0 / H)):
                 nc.scalar.activation(
                     out=var[:, part], in_=live[("squares", g)][:, part], func=ACT.Identity, bias=eps[:], scale=scale
                 )
@@ -350,7 +357,10 @@ def tile_layernormgrucell_pb_t_kernel(tc, x, h, r, z, W_in, b_in, W_hn, b_hn, ou
             ]
             y = guess[:].bitcast(F32)
             for i in range(3):
-                steps.append(lambda y=y: nc.vector.tensor_tensor(out=a[:], in0=y, in1=y, op=ALU.mult))
+                if g == 0:
+                    steps.append(lambda y=y: nc.vector.tensor_tensor(out=a[:], in0=y, in1=y, op=ALU.mult))
+                else:
+                    steps.append(lambda y=y: nc.scalar.activation(out=a[:], in_=y, func=ACT.Square))
                 steps.append(
                     lambda: nc.vector.scalar_tensor_tensor(
                         out=b[:], in0=a[:], scalar=-0.5, in1=var[:], op0=ALU.mult, op1=ALU.mult
@@ -405,37 +415,43 @@ def tile_layernormgrucell_pb_t_kernel(tc, x, h, r, z, W_in, b_in, W_hn, b_hn, ou
             zh = live[("n", g - 2)] if g > 1 else candidates.tile([P, GROUP_COLS], F32, name="n_sb")
             live[("zh", g)] = zh
             if g == 1:
-                nc.vector.memset(zh[:, HALF_COLS : HALF_COLS + 1], 0.0)
-            for lo, hi in ((HALF_COLS, GROUP_COLS), (0, HALF_COLS)):
+                nc.vector.memset(zh[:, 0:1], 0.0)
+            for lo, hi in ((0, 3 * H), (3 * H, GROUP_COLS)):
                 nc.gpsimd.tensor_tensor(
                     out=zh[:, lo:hi], in0=live[("z", g)][:, lo:hi], in1=live[("h", g)][:, lo:hi], op=ALU.mult
                 )
 
-        def weigh(g):
+        def weigh(g, tiles):
             z_sb = live[("z", g)]
             n_sb = live[("n", g)]
-            for t in range(GROUP_TILES):
+            for t in tiles:
                 cols = slice(t * H, (t + 1) * H)
                 nc.vector.scalar_tensor_tensor(
                     out=n_sb[:, cols], in0=z_sb[:, cols], scalar=1.0, in1=n_sb[:, cols],
                     op0=ALU.subtract, op1=ALU.mult,
                 )
-                root_step(g + 1)
+                root_step(g + 1, (2, 0, 1, 2)[t])
         def blend(g):
             n_sb = live[("n", g)]
             zh = live[("zh", g)]
             for t in range(GROUP_TILES):
                 cols = slice(t * H, (t + 1) * H)
                 nc.vector.tensor_tensor(out=zh[:, cols], in0=zh[:, cols], in1=n_sb[:, cols], op=ALU.subtract)
-                if t % 2 == 1:
+                if g == LAST:
+                    first_col = g * GROUP_COLS + cols.start
+                    nc.sync.dma_start(out=out_rows[:, first_col : first_col + H], in_=zh[:, cols])
+                elif t % 2 == 1:
                     half = HALVES[t // 2]
                     first_col = g * GROUP_COLS + half.start
                     nc.sync.dma_start(out=out_rows[:, first_col : first_col + HALF_COLS], in_=zh[:, half])
-                root_step(g + 1, 99 if t == GROUP_TILES - 2 else 1)
+                root_step(g + 1, (1, 2, 99, 0)[t])
 
         on_vector = nc.vector.tensor_copy
         on_scalar = nc.scalar.copy
         prepare_weight("h")
+        transpose_operand("h", 0, (on_vector, on_scalar))
+        quantise_weight("h")
+        quantise_operand("h", 0)
         bias2_bank = psum.tile([P, 512], F32, tag="bank")
         nc.tensor.matmul(out=bias2_bank[:], lhsT=ones[:], rhs=bias_rows[:, H : 2 * H], start=True, stop=True)
         bias2 = const.tile([P, H], F32)
@@ -443,22 +459,20 @@ def tile_layernormgrucell_pb_t_kernel(tc, x, h, r, z, W_in, b_in, W_hn, b_hn, ou
         mean_bias = const.tile([P, 1], F32)
         nc.scalar.activation(out=bias2[:], in_=bias2_bank[:], func=ACT.Copy, scale=1.0, accum_out=bias_sum[:])
         nc.scalar.mul(out=mean_bias[:], in_=bias_sum[:], mul=-1.0 / (H * P))
-        transpose_operand("h", 0, (on_vector, on_scalar))
-        quantise_weight("h")
-        quantise_operand("h", 0)
         prepare_weight("x", (on_scalar, on_scalar))
+        quantise_weight("x")
+        transpose_operand("x", 0, (on_scalar, on_scalar))
         new_moments(0)
         for t in range(GROUP_TILES):
             h_row_product(0, t)
-        transpose_operand("x", 0, (on_scalar, on_scalar))
         bias_bank = psum_s.tile([P, 512], F32, tag="s")
         nc.tensor.matmul(out=bias_bank[:], lhsT=ones[:], rhs=bias_rows[:, 0:H], start=True, stop=True)
         bias1 = const.tile([P, H], F32)
         nc.scalar.copy(out=bias1[:], in_=bias_bank[:])
         for t in range(GROUP_TILES):
             h_row_moments(0, t)
-        quantise_weight("x")
-        quantise_operand("x", 0)
+            if t == 1:
+                quantise_operand("x", 0)
         cols_bank = psum_s.tile([P, 512], F32, tag="s")
         for c in range(CH_BLOCKS):
             nc.tensor.matmul(
@@ -469,9 +483,20 @@ def tile_layernormgrucell_pb_t_kernel(tc, x, h, r, z, W_in, b_in, W_hn, b_hn, ou
         nc.scalar.copy(out=bias_cols[:], in_=cols_bank[:, 0:CH_BLOCKS])
         for t in range(GROUP_TILES):
             x_product(0, t)
-        minus_mean2 = small.tile([P, GROUP_TILES], F32, name="minus_mean2_0")
-        nc.scalar.mul(out=minus_mean2[:], in_=live[("sums2", 0)][:], mul=-1.0 / H)
-        live[("minus_mean2", 0)] = minus_mean2
+        row_means(0)
+
+        def row_window(a):
+            new_moments(a)
+            for t in range(GROUP_TILES):
+                h_row_moments(a, t)
+                if t < 2:
+                    h_row_product(a, t + 2)
+                x_moments(a, t)
+                if t < 2:
+                    x_product(a, t + 2)
+            row_means(a)
+            variance(a)
+            root_steps(a)
 
         def window(a):
             new_moments(a)
@@ -501,9 +526,8 @@ def tile_layernormgrucell_pb_t_kernel(tc, x, h, r, z, W_in, b_in, W_hn, b_hn, ou
         variance(0)
         root_steps(0)
         quantise_operand("h", 1)
-        h_product(1)
-        transpose_operand("h", 2)
-        transpose_operand("x", 2)
+        for t in range(2):
+            h_row_product(1, t)
         for t in range(GROUP_TILES):
             reset_row(0, t)
             root_step(0, 2)
@@ -511,19 +535,20 @@ def tile_layernormgrucell_pb_t_kernel(tc, x, h, r, z, W_in, b_in, W_hn, b_hn, ou
                 quantise_operand("x", 1)
                 root_step(0)
         root_step(0, 99)
-        h_sums(1)
         for t in range(2):
             x_product(1, t)
-        for t in range(3):
-            h_rows(1, t)
-        h_means(1)
+        transpose_operand("h", 2)
+        transpose_operand("x", 2)
         for s in range(2, GROUPS + 2):
             a = s - 1
             b = s - 2
             load_step(s)
             if a < GROUPS:
                 gate_product(a)
-                window(a)
+                if a in ROW_GROUPS:
+                    row_window(a)
+                else:
+                    window(a)
             if s == 2:
                 quantise_operand("h", 2)
                 quantise_operand("x", 2)
@@ -532,15 +557,17 @@ def tile_layernormgrucell_pb_t_kernel(tc, x, h, r, z, W_in, b_in, W_hn, b_hn, ou
             for t in range(GROUP_TILES):
                 combine(b, t)
                 squash(b, t)
-                if t > 0:
-                    root_step(a)
+                root_step(a, (0, 2, 0, 1)[t])
+            weigh(b, (0,))
             if s + 1 < GROUPS:
                 transpose_operand("h", s + 1)
                 transpose_operand("x", s + 1)
-            weigh(b)
+            weigh(b, (1, 2, 3))
+            if a in ROW_GROUPS:
+                for t in range(GROUP_TILES):
+                    reset_row(a, t)
             if s + 1 < GROUPS:
                 quantise_operand("h", s + 1)
-                root_step(a)
                 quantise_operand("x", s + 1)
                 root_step(a)
             if s < GROUPS:

@@ -27,7 +27,8 @@ HALF_COLS = GROUP_COLS // 2
 HALVES = (slice(0, HALF_COLS), slice(HALF_COLS, GROUP_COLS))
 CH_BLOCKS = H // P
 EPS = 1e-5
-RSQRT_BITS = 1597463007.0
+ROOT_BITS = 1597463007.0
+ROOT_SCALE = -0.3125
 
 FLOPS = 2 * 2 * B * K * H
 
@@ -95,8 +96,8 @@ def tile_layernormgrucell_pb_t_kernel(tc, x, h, r, z, W_in, b_in, W_hn, b_hn, ou
         make_identity(nc, identity[:])
         eps = const.tile([P, 1], F32)
         nc.gpsimd.memset(eps[:], EPS)
-        first_tanh = const.tile([P, 1], F32)
-        nc.scalar.activation(out=first_tanh[:], in_=ones[:, 0:1], func=ACT.Tanh)
+        warm_up = const.tile([P, 1], F32)
+        nc.scalar.activation(out=warm_up[:], in_=ones[:, 0:1], func=ACT.Sqrt)
 
         new_input("h", 0)
         new_input("x", 0)
@@ -332,6 +333,13 @@ def tile_layernormgrucell_pb_t_kernel(tc, x, h, r, z, W_in, b_in, W_hn, b_hn, ou
 
         def variance(g):
             var = small.tile([P, 2 * GROUP_TILES], F32)
+            if g == 0:
+                nc.scalar.activation(
+                    out=var[:], in_=live[("squares", g)][:], func=ACT.Sqrt, bias=eps[:], scale=1.0 / (H * H * H)
+                )
+                nc.scalar.activation(out=warm_up[:], in_=ones[:, 0:1], func=ACT.Tanh)
+                live[("var", g)] = var
+                return
             for part, scale in ((first, 1.0 / (H * H * H)), (second, 1.0 / (H * H * H) if g in ROW_GROUPS else 1.0 / H)):
                 nc.scalar.activation(
                     out=var[:, part], in_=live[("squares", g)][:, part], func=ACT.Identity, bias=eps[:], scale=scale
@@ -343,50 +351,75 @@ def tile_layernormgrucell_pb_t_kernel(tc, x, h, r, z, W_in, b_in, W_hn, b_hn, ou
 
         def root_steps(g):
             var = live[("var", g)]
-            guess = small.tile([P, 2 * GROUP_TILES], I32, name="guess")
-            a = small.tile([P, 2 * GROUP_TILES], F32, name="root_a")
-            b = small.tile([P, 2 * GROUP_TILES], F32, name="root_b")
-            ys = [small.tile([P, 2 * GROUP_TILES], F32, name="root_y%d" % i) for i in range(3)]
-            std1 = small.tile([P, GROUP_TILES], F32, name="std1")
+            if g == 0:
+                std = var
+                rstd = small.tile([P, 2 * GROUP_TILES], F32, name="rstd")
+                q = small.tile([P, GROUP_TILES], F32, name="q")
+                shift = small.tile([P, GROUP_TILES], F32, name="shift")
+                live[("rstd", g)] = rstd
+                live[("q", g)] = q
+                live[("shift", g)] = shift
+                live[("steps", g)] = [
+                    lambda: nc.vector.reciprocal(out=rstd[:], in_=std[:]),
+                    lambda: nc.vector.tensor_tensor(out=q[:], in0=std[:, first], in1=rstd[:, second], op=ALU.mult),
+                    lambda: nc.vector.scalar_tensor_tensor(
+                        out=shift[:], in0=live[("sums1", g)][:], scalar=-1.0 / H, in1=rstd[:, first],
+                        op0=ALU.mult, op1=ALU.mult,
+                    ),
+                ]
+                return
+            guess = small.tile([P, 2 * GROUP_TILES], U32, name="guess")
+            y0 = guess[:].bitcast(F32)
+            new = lambda name: small.tile([P, 2 * GROUP_TILES], F32, name=name)
+            a0 = new("root_a0")
+            b = new("root_b")
+            y1 = new("root_y1")
+            a1 = new("root_a1")
+            s1 = new("root_s1")
+            w = new("root_w")
+            c1 = new("root_c1")
+            c2 = new("root_c2")
+            rstd = new("rstd")
+            std = new("std")
             q = small.tile([P, GROUP_TILES], F32, name="q")
             shift = small.tile([P, GROUP_TILES], F32, name="shift")
-            steps = [
-                lambda: nc.vector.tensor_scalar(
-                    out=guess[:], in0=var[:].bitcast(I32), scalar1=-0.5, scalar2=RSQRT_BITS, op0=ALU.mult, op1=ALU.add
+
+            def times(out, in0, scalar, in1, op0):
+                nc.vector.scalar_tensor_tensor(
+                    out=out[:], in0=in0, scalar=scalar, in1=in1, op0=op0, op1=ALU.mult
                 )
+
+            live[("scalar steps", g)] = [
+                lambda: nc.scalar.activation(
+                    out=guess[:], in_=var[:].bitcast(U32), func=ACT.Copy, scale=-0.5, bias=ROOT_BITS
+                ),
+                lambda: nc.scalar.activation(out=a0[:], in_=y0, func=ACT.Square),
+                lambda: nc.scalar.activation(out=a1[:], in_=y1[:], func=ACT.Square, scale=1.0 / ROOT_SCALE),
             ]
-            y = guess[:].bitcast(F32)
-            for i in range(3):
-                if g == 0:
-                    steps.append(lambda y=y: nc.vector.tensor_tensor(out=a[:], in0=y, in1=y, op=ALU.mult))
-                else:
-                    steps.append(lambda y=y: nc.scalar.activation(out=a[:], in_=y, func=ACT.Square))
-                steps.append(
-                    lambda: nc.vector.scalar_tensor_tensor(
-                        out=b[:], in0=a[:], scalar=-0.5, in1=var[:], op0=ALU.mult, op1=ALU.mult
-                    )
-                )
-                steps.append(
-                    lambda y=y, i=i: nc.vector.scalar_tensor_tensor(
-                        out=ys[i][:], in0=b[:], scalar=1.5, in1=y, op0=ALU.add, op1=ALU.mult
-                    )
-                )
-                y = ys[i][:]
-            rstd = ys[2]
-            steps.append(
-                lambda: nc.vector.tensor_tensor(out=std1[:], in0=var[:, first], in1=rstd[:, first], op=ALU.mult)
-            )
-            steps.append(
+            live[("steps", g)] = [
+                lambda: times(b, a0[:], -0.5 * ROOT_SCALE, var[:], ALU.mult),
+                lambda: times(y1, b[:], 1.5 * ROOT_SCALE, y0, ALU.add),
+                lambda: nc.vector.tensor_tensor(out=s1[:], in0=y1[:], in1=var[:], op=ALU.mult),
+                lambda: nc.vector.tensor_tensor(out=w[:], in0=a1[:], in1=var[:], op=ALU.mult),
+                lambda: times(c1, w[:], -4.2, w[:], ALU.add),
+                lambda: times(c2, c1[:], 7.0, w[:], ALU.add),
+                lambda: times(rstd, c2[:], -7.0, y1[:], ALU.add),
+                lambda: times(std, c2[:], -7.0, s1[:], ALU.add),
+                lambda: nc.vector.tensor_tensor(out=q[:], in0=std[:, first], in1=rstd[:, second], op=ALU.mult),
                 lambda: nc.vector.scalar_tensor_tensor(
                     out=shift[:], in0=live[("sums1", g)][:], scalar=-1.0 / H, in1=rstd[:, first],
                     op0=ALU.mult, op1=ALU.mult,
-                )
-            )
-            steps.append(lambda: nc.vector.tensor_tensor(out=q[:], in0=std1[:], in1=rstd[:, second], op=ALU.mult))
+                ),
+            ]
             live[("rstd", g)] = rstd
             live[("q", g)] = q
             live[("shift", g)] = shift
-            live[("steps", g)] = steps
+
+        def scalar_step(g):
+            steps = live.get(("scalar steps", g), [])
+            if steps:
+                steps[0]()
+            live[("scalar steps", g)] = steps[1:]
 
         def root_step(g, count=1):
             steps = live.get(("steps", g), [])
@@ -430,11 +463,11 @@ def tile_layernormgrucell_pb_t_kernel(tc, x, h, r, z, W_in, b_in, W_hn, b_hn, ou
                     out=n_sb[:, cols], in0=z_sb[:, cols], scalar=1.0, in1=n_sb[:, cols],
                     op0=ALU.subtract, op1=ALU.mult,
                 )
-                root_step(g + 1, (2, 0, 1, 2)[t])
-        def blend(g):
+                root_step(g + 1, (1, 1, 1, 1)[t])
+        def blend(g, tiles):
             n_sb = live[("n", g)]
             zh = live[("zh", g)]
-            for t in range(GROUP_TILES):
+            for t in tiles:
                 cols = slice(t * H, (t + 1) * H)
                 nc.vector.tensor_tensor(out=zh[:, cols], in0=zh[:, cols], in1=n_sb[:, cols], op=ALU.subtract)
                 if g == LAST:
@@ -444,7 +477,7 @@ def tile_layernormgrucell_pb_t_kernel(tc, x, h, r, z, W_in, b_in, W_hn, b_hn, ou
                     half = HALVES[t // 2]
                     first_col = g * GROUP_COLS + half.start
                     nc.sync.dma_start(out=out_rows[:, first_col : first_col + HALF_COLS], in_=zh[:, half])
-                root_step(g + 1, (1, 2, 99, 0)[t])
+                root_step(g + 1, (1, 1, 2, 2)[t] if g + 1 == LAST else (1, 2, 0, 0)[t])
 
         on_vector = nc.vector.tensor_copy
         on_scalar = nc.scalar.copy
@@ -459,7 +492,7 @@ def tile_layernormgrucell_pb_t_kernel(tc, x, h, r, z, W_in, b_in, W_hn, b_hn, ou
         mean_bias = const.tile([P, 1], F32)
         nc.scalar.activation(out=bias2[:], in_=bias2_bank[:], func=ACT.Copy, scale=1.0, accum_out=bias_sum[:])
         nc.scalar.mul(out=mean_bias[:], in_=bias_sum[:], mul=-1.0 / (H * P))
-        prepare_weight("x", (on_scalar, on_scalar))
+        prepare_weight("x", (on_scalar, on_vector))
         quantise_weight("x")
         transpose_operand("x", 0, (on_scalar, on_scalar))
         new_moments(0)
@@ -495,20 +528,14 @@ def tile_layernormgrucell_pb_t_kernel(tc, x, h, r, z, W_in, b_in, W_hn, b_hn, ou
                 if t < 2:
                     x_product(a, t + 2)
             row_means(a)
-            variance(a)
-            root_steps(a)
 
         def window(a):
             new_moments(a)
             for t in range(GROUP_TILES):
                 x_moments(a, t)
-                if t < 2:
-                    x_product(a, t + 2)
                 h_moments(a, t)
                 if t < 1:
                     h_rows(a, t + 3)
-            variance(a)
-            root_steps(a)
 
         def load_step(s):
             if s + 2 < GROUPS:
@@ -530,11 +557,10 @@ def tile_layernormgrucell_pb_t_kernel(tc, x, h, r, z, W_in, b_in, W_hn, b_hn, ou
             h_row_product(1, t)
         for t in range(GROUP_TILES):
             reset_row(0, t)
-            root_step(0, 2)
             if t == 1:
                 quantise_operand("x", 1)
+            if t > 0:
                 root_step(0)
-        root_step(0, 99)
         for t in range(2):
             x_product(1, t)
         transpose_operand("h", 2)
@@ -557,24 +583,36 @@ def tile_layernormgrucell_pb_t_kernel(tc, x, h, r, z, W_in, b_in, W_hn, b_hn, ou
             for t in range(GROUP_TILES):
                 combine(b, t)
                 squash(b, t)
-                root_step(a, (0, 2, 0, 1)[t])
+                if t == 0 and a < GROUPS:
+                    variance(a)
+                    root_steps(a)
+                elif t < 3:
+                    scalar_step(a)
             weigh(b, (0,))
             if s + 1 < GROUPS:
                 transpose_operand("h", s + 1)
+            weigh(b, (1,))
+            scalar_step(a)
+            if s + 1 < GROUPS:
                 transpose_operand("x", s + 1)
-            weigh(b, (1, 2, 3))
+            weigh(b, (2, 3))
             if a in ROW_GROUPS:
                 for t in range(GROUP_TILES):
                     reset_row(a, t)
             if s + 1 < GROUPS:
                 quantise_operand("h", s + 1)
-                quantise_operand("x", s + 1)
+            if a != LAST:
                 root_step(a)
+            blend(b, (0,))
+            if s + 1 < GROUPS:
+                quantise_operand("x", s + 1)
+            if a != LAST:
+                root_step(a, 2)
             if s < GROUPS:
                 h_product(s)
-                for t in range(2):
+                for t in range(GROUP_TILES):
                     x_product(s, t)
                 for t in range(3):
                     h_rows(s, t)
                 h_means(s)
-            blend(b)
+            blend(b, (1, 2, 3))

@@ -21,6 +21,7 @@ ROW_TILES = B // P
 GROUP_TILES = 4
 GROUPS = ROW_TILES // GROUP_TILES
 LAST = GROUPS - 1
+WARM_UP = 3
 ROW_GROUPS = (0, 1)
 GROUP_COLS = GROUP_TILES * H
 HALF_COLS = GROUP_COLS // 2
@@ -86,10 +87,13 @@ def tile_layernormgrucell_pb_t_kernel(tc, x, h, r, z, W_in, b_in, W_hn, b_hn, ou
                 in_=w[pair * 2 * P : (pair + 1) * 2 * P, :].rearrange("(a p) k -> p a k", p=P),
             )
 
+        ones = const.tile([P, H], BF16)
+        nc.vector.memset(ones[:], 1.0)
         bias_rows = const.tile([P, 2 * H], BF16)
         nc.vector.memset(bias_rows[:], 0.0)
-        ones = const.tile([P, P], BF16)
-        nc.vector.memset(ones[:], 1.0)
+        warm_bank = psum_s.tile([P, 512], F32, tag="s")
+        for i in range(WARM_UP):
+            nc.tensor.matmul(out=warm_bank[:], lhsT=ones[:, 0:P], rhs=ones[:], start=True, stop=True)
         nc.scalar.dma_start(out=bias_rows[0:1, 0:H], in_=b_in.rearrange("(o n) -> o n", o=1))
         nc.scalar.dma_start(out=bias_rows[0:1, H : 2 * H], in_=b_hn.rearrange("(o n) -> o n", o=1))
         identity = const.tile([P, P], F32)
@@ -449,10 +453,7 @@ def tile_layernormgrucell_pb_t_kernel(tc, x, h, r, z, W_in, b_in, W_hn, b_hn, ou
             live[("zh", g)] = zh
             if g == 1:
                 nc.vector.memset(zh[:, 0:1], 0.0)
-            for lo, hi in ((0, 3 * H), (3 * H, GROUP_COLS)):
-                nc.gpsimd.tensor_tensor(
-                    out=zh[:, lo:hi], in0=live[("z", g)][:, lo:hi], in1=live[("h", g)][:, lo:hi], op=ALU.mult
-                )
+            nc.gpsimd.tensor_tensor(out=zh[:], in0=live[("z", g)][:], in1=live[("h", g)][:], op=ALU.mult)
 
         def weigh(g, tiles):
             z_sb = live[("z", g)]
@@ -486,7 +487,7 @@ def tile_layernormgrucell_pb_t_kernel(tc, x, h, r, z, W_in, b_in, W_hn, b_hn, ou
         quantise_weight("h")
         quantise_operand("h", 0)
         bias2_bank = psum.tile([P, 512], F32, tag="bank")
-        nc.tensor.matmul(out=bias2_bank[:], lhsT=ones[:], rhs=bias_rows[:, H : 2 * H], start=True, stop=True)
+        nc.tensor.matmul(out=bias2_bank[:], lhsT=ones[:, 0:P], rhs=bias_rows[:, H : 2 * H], start=True, stop=True)
         bias2 = const.tile([P, H], F32)
         bias_sum = const.tile([P, 1], F32)
         mean_bias = const.tile([P, 1], F32)
@@ -499,7 +500,7 @@ def tile_layernormgrucell_pb_t_kernel(tc, x, h, r, z, W_in, b_in, W_hn, b_hn, ou
         for t in range(GROUP_TILES):
             h_row_product(0, t)
         bias_bank = psum_s.tile([P, 512], F32, tag="s")
-        nc.tensor.matmul(out=bias_bank[:], lhsT=ones[:], rhs=bias_rows[:, 0:H], start=True, stop=True)
+        nc.tensor.matmul(out=bias_bank[:], lhsT=ones[:, 0:P], rhs=bias_rows[:, 0:H], start=True, stop=True)
         bias1 = const.tile([P, H], F32)
         nc.scalar.copy(out=bias1[:], in_=bias_bank[:])
         for t in range(GROUP_TILES):

@@ -21,6 +21,7 @@ ROW_TILES = B // P
 GROUP_TILES = 4
 GROUPS = ROW_TILES // GROUP_TILES
 LAST = GROUPS - 1
+BY_SQRT = (0, LAST)
 WARM_UP = 3
 ROW_GROUPS = (0, 1)
 GROUP_COLS = GROUP_TILES * H
@@ -337,10 +338,11 @@ def tile_layernormgrucell_pb_t_kernel(tc, x, h, r, z, W_in, b_in, W_hn, b_hn, ou
 
         def variance(g):
             var = small.tile([P, 2 * GROUP_TILES], F32)
-            if g == 0:
-                nc.scalar.activation(
-                    out=var[:], in_=live[("squares", g)][:], func=ACT.Sqrt, bias=eps[:], scale=1.0 / (H * H * H)
-                )
+            if g in BY_SQRT:
+                for part, scale in ((first, 1.0 / (H * H * H)), (second, 1.0 / (H * H * H) if g in ROW_GROUPS else 1.0 / H)):
+                    nc.scalar.activation(
+                        out=var[:, part], in_=live[("squares", g)][:, part], func=ACT.Sqrt, bias=eps[:], scale=scale
+                    )
                 nc.scalar.activation(out=warm_up[:], in_=ones[:, 0:1], func=ACT.Tanh)
                 live[("var", g)] = var
                 return
@@ -355,7 +357,7 @@ def tile_layernormgrucell_pb_t_kernel(tc, x, h, r, z, W_in, b_in, W_hn, b_hn, ou
 
         def root_steps(g):
             var = live[("var", g)]
-            if g == 0:
+            if g in BY_SQRT:
                 std = var
                 rstd = small.tile([P, 2 * GROUP_TILES], F32, name="rstd")
                 q = small.tile([P, GROUP_TILES], F32, name="q")
@@ -419,6 +421,21 @@ def tile_layernormgrucell_pb_t_kernel(tc, x, h, r, z, W_in, b_in, W_hn, b_hn, ou
             live[("q", g)] = q
             live[("shift", g)] = shift
 
+        def root_slot(g, place, t=0):
+            if g == LAST:
+                plan = {("blend", 1): 1, ("blend", 2): 2}
+            elif g == LAST - 1:
+                plan = {
+                    ("weigh", 0): 1, ("weigh", 1): 1, ("weigh", 2): 1, ("weigh", 3): 1,
+                    ("blend", 0): 1, ("blend", 1): 1, ("blend", 2): 4,
+                }
+            else:
+                plan = {
+                    ("weigh", 1): 1, ("weigh", 2): 1, ("weigh", 3): 1, ("quantise h", 0): 1, ("blend", 0): 1,
+                    ("quantise x", 0): 1, ("blend", 1): 2, ("blend", 2): 2,
+                }
+            root_step(g, plan.get((place, t), 0))
+
         def scalar_step(g):
             steps = live.get(("scalar steps", g), [])
             if steps:
@@ -464,7 +481,7 @@ def tile_layernormgrucell_pb_t_kernel(tc, x, h, r, z, W_in, b_in, W_hn, b_hn, ou
                     out=n_sb[:, cols], in0=z_sb[:, cols], scalar=1.0, in1=n_sb[:, cols],
                     op0=ALU.subtract, op1=ALU.mult,
                 )
-                root_step(g + 1, (1, 1, 1, 1)[t])
+                root_slot(g + 1, "weigh", t)
         def blend(g, tiles):
             n_sb = live[("n", g)]
             zh = live[("zh", g)]
@@ -478,7 +495,7 @@ def tile_layernormgrucell_pb_t_kernel(tc, x, h, r, z, W_in, b_in, W_hn, b_hn, ou
                     half = HALVES[t // 2]
                     first_col = g * GROUP_COLS + half.start
                     nc.sync.dma_start(out=out_rows[:, first_col : first_col + HALF_COLS], in_=zh[:, half])
-                root_step(g + 1, (1, 1, 2, 2)[t] if g + 1 == LAST else (1, 2, 0, 0)[t])
+                root_slot(g + 1, "blend", t)
 
         on_vector = nc.vector.tensor_copy
         on_scalar = nc.scalar.copy
@@ -584,7 +601,7 @@ def tile_layernormgrucell_pb_t_kernel(tc, x, h, r, z, W_in, b_in, W_hn, b_hn, ou
             for t in range(GROUP_TILES):
                 combine(b, t)
                 squash(b, t)
-                if t == 0 and a < GROUPS:
+                if t == (3 if a == LAST else 0) and a < GROUPS:
                     variance(a)
                     root_steps(a)
                 elif t < 3:
@@ -592,23 +609,21 @@ def tile_layernormgrucell_pb_t_kernel(tc, x, h, r, z, W_in, b_in, W_hn, b_hn, ou
             weigh(b, (0,))
             if s + 1 < GROUPS:
                 transpose_operand("h", s + 1)
-            weigh(b, (1,))
+            weigh(b, (1,) if a == LAST - 1 else (1, 2))
             scalar_step(a)
             if s + 1 < GROUPS:
                 transpose_operand("x", s + 1)
-            weigh(b, (2, 3))
+            weigh(b, (2, 3) if a == LAST - 1 else (3,))
             if a in ROW_GROUPS:
                 for t in range(GROUP_TILES):
                     reset_row(a, t)
             if s + 1 < GROUPS:
                 quantise_operand("h", s + 1)
-            if a != LAST:
-                root_step(a)
+            root_slot(a, "quantise h")
             blend(b, (0,))
             if s + 1 < GROUPS:
                 quantise_operand("x", s + 1)
-            if a != LAST:
-                root_step(a, 2)
+            root_slot(a, "quantise x")
             if s < GROUPS:
                 h_product(s)
                 for t in range(GROUP_TILES):

@@ -22,6 +22,7 @@ GROUP_TILES = 4
 GROUPS = ROW_TILES // GROUP_TILES
 LAST = GROUPS - 1
 BY_SQRT = (0, LAST)
+ON_TENSOR = ((LAST - 1, 0), (LAST - 1, 1))
 WARM_UP = 3
 ROW_GROUPS = (0, 1)
 GROUP_COLS = GROUP_TILES * H
@@ -99,6 +100,10 @@ def tile_layernormgrucell_pb_t_kernel(tc, x, h, r, z, W_in, b_in, W_hn, b_hn, ou
         nc.scalar.dma_start(out=bias_rows[0:1, H : 2 * H], in_=b_hn.rearrange("(o n) -> o n", o=1))
         identity = const.tile([P, P], F32)
         make_identity(nc, identity[:])
+        minus_identity = const.tile([P, P], F32)
+        nc.gpsimd.tensor_scalar(
+            out=minus_identity[:], in0=identity[:], scalar1=-1.0, scalar2=0.0, op0=ALU.mult, op1=ALU.add
+        )
         eps = const.tile([P, 1], F32)
         nc.gpsimd.memset(eps[:], EPS)
         warm_up = const.tile([P, 1], F32)
@@ -423,7 +428,7 @@ def tile_layernormgrucell_pb_t_kernel(tc, x, h, r, z, W_in, b_in, W_hn, b_hn, ou
 
         def root_slot(g, place, t=0):
             if g == LAST:
-                plan = {("blend", 1): 1, ("blend", 2): 2}
+                plan = {("blend", 2): 1, ("blend", 3): 2}
             elif g == LAST - 1:
                 plan = {
                     ("weigh", 0): 1, ("weigh", 1): 1, ("weigh", 2): 1, ("weigh", 3): 1,
@@ -482,13 +487,31 @@ def tile_layernormgrucell_pb_t_kernel(tc, x, h, r, z, W_in, b_in, W_hn, b_hn, ou
                     op0=ALU.subtract, op1=ALU.mult,
                 )
                 root_slot(g + 1, "weigh", t)
+                if (g, t) in ON_TENSOR:
+                    blend_on_tensor(g, t)
+        def blend_on_tensor(g, t):
+            cols = slice(t * H, (t + 1) * H)
+            bank = psum.tile([P, 512], F32, tag="bank")
+            nc.tensor.matmul(out=bank[:], lhsT=identity[:], rhs=live[("zh", g)][:, cols], start=True, stop=False)
+            nc.tensor.matmul(out=bank[:], lhsT=minus_identity[:], rhs=live[("n", g)][:, cols], start=False, stop=True)
+            live[("blend", g, t)] = bank
+
+        def store_from_tensor(g, t):
+            cols = slice(t * H, (t + 1) * H)
+            done = live[("n", g)]
+            nc.scalar.copy(out=done[:, cols], in_=live[("blend", g, t)][:])
+            first_col = g * GROUP_COLS + cols.start
+            nc.sync.dma_start(out=out_rows[:, first_col : first_col + H], in_=done[:, cols])
+
         def blend(g, tiles):
             n_sb = live[("n", g)]
             zh = live[("zh", g)]
             for t in tiles:
+                if (g, t) in ON_TENSOR:
+                    continue
                 cols = slice(t * H, (t + 1) * H)
                 nc.vector.tensor_tensor(out=zh[:, cols], in0=zh[:, cols], in1=n_sb[:, cols], op=ALU.subtract)
-                if g == LAST:
+                if g >= LAST - 1:
                     first_col = g * GROUP_COLS + cols.start
                     nc.sync.dma_start(out=out_rows[:, first_col : first_col + H], in_=zh[:, cols])
                 elif t % 2 == 1:
@@ -606,6 +629,9 @@ def tile_layernormgrucell_pb_t_kernel(tc, x, h, r, z, W_in, b_in, W_hn, b_hn, ou
                     root_steps(a)
                 elif t < 3:
                     scalar_step(a)
+            if b == LAST:
+                for g, t in ON_TENSOR:
+                    store_from_tensor(g, t)
             weigh(b, (0,))
             if s + 1 < GROUPS:
                 transpose_operand("h", s + 1)

@@ -5,7 +5,6 @@ from concourse.masks import make_identity
 
 F32 = mybir.dt.float32
 BF16 = mybir.dt.bfloat16
-I32 = mybir.dt.int32
 U32 = mybir.dt.uint32
 U8 = mybir.dt.uint8
 FP8X4 = mybir.dt.float8_e4m3fn_x4
@@ -16,22 +15,25 @@ P = 128
 B = 4096
 K = 512
 H = 512
+OUT_BLOCKS = H // P
 WORDS = K // 2
 ROW_TILES = B // P
 GROUP_TILES = 4
 GROUPS = ROW_TILES // GROUP_TILES
 LAST = GROUPS - 1
-BY_SQRT = (0, LAST)
-ON_TENSOR = ((LAST - 1, 0), (LAST - 1, 1))
-WARM_UP = 3
-ROW_GROUPS = (0, 1)
 GROUP_COLS = GROUP_TILES * H
 HALF_COLS = GROUP_COLS // 2
-HALVES = (slice(0, HALF_COLS), slice(HALF_COLS, GROUP_COLS))
-CH_BLOCKS = H // P
 EPS = 1e-5
+FIRST_NORM = slice(0, GROUP_TILES)
+SECOND_NORM = slice(GROUP_TILES, 2 * GROUP_TILES)
+
+TURNED_FROM = (4, 3) + (GROUPS - 2) * (0,)
+SQRT_GROUPS = (0, LAST)
+TENSOR_BLENDS = (0, 1)
+WARM_UPS = 3
+
 ROOT_BITS = 1597463007.0
-ROOT_SCALE = -0.3125
+ROOT_SCALE = -5.0 / 16.0
 
 FLOPS = 2 * 2 * B * K * H
 
@@ -59,10 +61,17 @@ def tile_layernormgrucell_pb_t_kernel(tc, x, h, r, z, W_in, b_in, W_hn, b_hn, ou
         candidates = ctx.enter_context(tc.tile_pool(name="candidates", bufs=4))
         small = ctx.enter_context(tc.tile_pool(name="small", bufs=3))
         psum = ctx.enter_context(tc.psum_pool(name="psum", bufs=7))
-        psum_s = ctx.enter_context(tc.psum_pool(name="psum_s", bufs=1))
+        psum_sums = ctx.enter_context(tc.psum_pool(name="psum_s", bufs=1))
         ctx.enter_context(tc.manual_schedule())
 
         live = {}
+
+        def columns(t):
+            return slice(t * H, (t + 1) * H)
+
+        def new_bank():
+            bank = psum.tile([P, H], F32, tag="bank")
+            return bank
 
         def new_input(name, g):
             live[(name, g)] = inputs[name].tile([P, GROUP_COLS], BF16, name="in_" + name)
@@ -83,7 +92,7 @@ def tile_layernormgrucell_pb_t_kernel(tc, x, h, r, z, W_in, b_in, W_hn, b_hn, ou
             new_input(name, g)
             fetch(name, g, 0, GROUP_COLS)
 
-        def load_weight(name, w, pair):
+        def load_weight_half(name, w, pair):
             nc.sync.dma_start(
                 out=w_raw[name][:, pair * 2 * K : (pair + 1) * 2 * K].rearrange("p (a k) -> p a k", a=2),
                 in_=w[pair * 2 * P : (pair + 1) * 2 * P, :].rearrange("(a p) k -> p a k", p=P),
@@ -93,8 +102,8 @@ def tile_layernormgrucell_pb_t_kernel(tc, x, h, r, z, W_in, b_in, W_hn, b_hn, ou
         nc.vector.memset(ones[:], 1.0)
         bias_rows = const.tile([P, 2 * H], BF16)
         nc.vector.memset(bias_rows[:], 0.0)
-        warm_bank = psum_s.tile([P, 512], F32, tag="s")
-        for i in range(WARM_UP):
+        warm_bank = psum_sums.tile([P, H], F32, tag="s")
+        for i in range(WARM_UPS):
             nc.tensor.matmul(out=warm_bank[:], lhsT=ones[:, 0:P], rhs=ones[:], start=True, stop=True)
         nc.scalar.dma_start(out=bias_rows[0:1, 0:H], in_=b_in.rearrange("(o n) -> o n", o=1))
         nc.scalar.dma_start(out=bias_rows[0:1, H : 2 * H], in_=b_hn.rearrange("(o n) -> o n", o=1))
@@ -106,16 +115,16 @@ def tile_layernormgrucell_pb_t_kernel(tc, x, h, r, z, W_in, b_in, W_hn, b_hn, ou
         )
         eps = const.tile([P, 1], F32)
         nc.gpsimd.memset(eps[:], EPS)
-        warm_up = const.tile([P, 1], F32)
-        nc.scalar.activation(out=warm_up[:], in_=ones[:, 0:1], func=ACT.Sqrt)
+        table_load = const.tile([P, 1], F32)
+        nc.scalar.activation(out=table_load[:], in_=ones[:, 0:1], func=ACT.Sqrt)
 
         new_input("h", 0)
         new_input("x", 0)
         w_raw = {}
         for name, w in (("h", W_hn), ("x", W_in)):
-            w_raw[name] = const.tile([P, 4 * K], BF16, name="w_sb_" + name)
+            w_raw[name] = const.tile([P, OUT_BLOCKS * K], BF16, name="w_sb_" + name)
             for pair in range(2):
-                load_weight(name, w, pair)
+                load_weight_half(name, w, pair)
             for lo in (0, HALF_COLS):
                 fetch(name, 0, lo, lo + HALF_COLS)
         load_gate("r", 0)
@@ -123,43 +132,42 @@ def tile_layernormgrucell_pb_t_kernel(tc, x, h, r, z, W_in, b_in, W_hn, b_hn, ou
         load_gate("z", 0)
         load_activations(2)
 
+        w_grouped = {}
         w_codes = {}
         w_scales = {}
-        w_grouped_tiles = {}
 
-        def prepare_weight(name, copy_out=(nc.vector.tensor_copy, nc.scalar.copy)):
-            w_words = w_raw[name][:].bitcast(F32)
-            w_grouped = const.tile([P, 4 * H], BF16, name="w_grouped_" + name, align_bytes=64)
-            w_grouped_words = w_grouped[:].bitcast(F32)
+        def transpose_weight(name, copy_out):
+            words = w_raw[name][:].bitcast(F32)
+            w_grouped[name] = const.tile([P, 4 * H], BF16, name="w_grouped_" + name, align_bytes=64)
+            grouped_words = w_grouped[name][:].bitcast(F32)
             for pair in range(2):
-                w_t = psum.tile([P, 512], F32, tag="bank")
+                bank = new_bank()
                 for u in range(2):
                     for j in range(2):
                         a = 2 * pair + j
                         nc.tensor.transpose(
-                            w_t[:, u * 256 + j * P : u * 256 + (j + 1) * P],
-                            w_words[:, a * WORDS + u * P : a * WORDS + (u + 1) * P],
+                            bank[:, u * 256 + j * P : u * 256 + (j + 1) * P],
+                            words[:, a * WORDS + u * P : a * WORDS + (u + 1) * P],
                             identity[:],
                         )
                 copy_out[pair](
-                    out=w_grouped_words[:, pair * 512 : (pair + 1) * 512].rearrange("p (n u) -> p n u", u=2),
-                    in_=w_t[:].rearrange("p (u n) -> p n u", u=2),
+                    out=grouped_words[:, pair * 512 : (pair + 1) * 512].rearrange("p (n u) -> p n u", u=2),
+                    in_=bank[:].rearrange("p (u n) -> p n u", u=2),
                 )
-            w_grouped_tiles[name] = w_grouped
 
         def quantise_weight(name):
-            codes = const.tile([P, H], U32, name="w_codes_" + name, align_bytes=64)
-            scales = const.tile([P, H], U8, name="w_scales_" + name, align_bytes=64)
-            nc.vector.quantize_mx(out=codes[:].bitcast(FP8X4), scales=scales[:], in_=w_grouped_tiles[name][:])
-            w_codes[name] = codes
-            w_scales[name] = scales
+            w_codes[name] = const.tile([P, H], U32, name="w_codes_" + name, align_bytes=64)
+            w_scales[name] = const.tile([P, H], U8, name="w_scales_" + name, align_bytes=64)
+            nc.vector.quantize_mx(
+                out=w_codes[name][:].bitcast(FP8X4), scales=w_scales[name][:], in_=w_grouped[name][:]
+            )
 
         def transpose_operand(name, g, copy_out=(nc.scalar.copy, nc.scalar.copy)):
             words = live[(name, g)][:].bitcast(F32)
             grouped = work.tile([P, GROUP_COLS], BF16, name="grouped_" + name, align_bytes=64)
             grouped_words = grouped[:].bitcast(F32)
             for pair in range(GROUP_TILES // 2):
-                bank = psum.tile([P, 512], F32, tag="bank")
+                bank = new_bank()
                 for j in range(2):
                     t = 2 * pair + j
                     for u in range(2):
@@ -183,278 +191,250 @@ def tile_layernormgrucell_pb_t_kernel(tc, x, h, r, z, W_in, b_in, W_hn, b_hn, ou
             live[("codes_" + name, g)] = codes
             live[("scales_" + name, g)] = scales
 
-        def h_block(g, c, on_vector=False):
-            if c == 0:
-                live[("u2t", g)] = work.tile([P, CH_BLOCKS * 512], F32, name="u2t")
-            u2t = live[("u2t", g)]
-            acc = psum.tile([P, 512], F32, tag="bank")
+        def row_product(name, g, t):
+            rows = slice(t * P, (t + 1) * P)
+            bank = new_bank()
             nc.tensor.matmul_mx(
-                out=acc[:],
-                lhsT=w_codes["h"][:, c * P : (c + 1) * P].bitcast(FP8X4),
-                lhsT_scale=w_scales["h"][:, c * P : (c + 1) * P],
-                rhs=live[("codes_h", g)][:].bitcast(FP8X4),
-                rhs_scale=live[("scales_h", g)][:],
+                out=bank[:],
+                lhsT=live[("codes_" + name, g)][:, rows].bitcast(FP8X4),
+                lhsT_scale=live[("scales_" + name, g)][:, rows],
+                rhs=w_codes[name][:].bitcast(FP8X4),
+                rhs_scale=w_scales[name][:],
                 start=True,
                 stop=True,
             )
-            if on_vector:
-                nc.vector.tensor_scalar(
-                    out=u2t[:, c * 512 : (c + 1) * 512], in0=acc[:], scalar1=bias_cols[:, c : c + 1],
-                    scalar2=None, op0=ALU.add,
+            live[("product_" + name, g, t)] = bank
+
+        def row_moments(name, g, t):
+            cols = columns(t)
+            u = live[("u1" if name == "x" else "v", g)]
+            total = live[("sums_" + name, g)][:, t : t + 1]
+            norm = FIRST_NORM if name == "x" else SECOND_NORM
+            nc.vector.scalar_tensor_tensor(
+                out=u[:, cols], in0=live[("product_" + name, g, t)][:], scalar=1.0, in1=bias_wide[name][:],
+                op0=ALU.mult, op1=ALU.add, accum_out=total,
+            )
+            unused = work.tile([P, H], BF16, name="unused")
+            nc.scalar.activation(
+                out=unused[:], in_=u[:, cols], func=ACT.Square, bias=total, scale=-1.0 * H,
+                accum_out=live[("squares", g)][:, norm.start + t : norm.start + t + 1],
+            )
+
+        def row_means(g):
+            rows = slice(0, TURNED_FROM[g])
+            minus_mean2 = small.tile([P, GROUP_TILES], F32, name="minus_mean2_0")
+            nc.scalar.mul(out=minus_mean2[:, rows], in_=live[("sums_h", g)][:, rows], mul=-1.0 / H)
+            live[("row_minus_mean2", g)] = minus_mean2
+
+        def reset_row(g, t):
+            cols = columns(t)
+            v = live[("v", g)]
+            nc.vector.scalar_tensor_tensor(
+                out=v[:, cols], in0=v[:, cols], scalar=live[("row_minus_mean2", g)][:, t : t + 1],
+                in1=live[("r", g)][:, cols], op0=ALU.add, op1=ALU.mult,
+            )
+
+        def turned_product(g):
+            u2_turned = work.tile([P, OUT_BLOCKS * H], F32, name="u2t")
+            rows = slice(TURNED_FROM[g] * P, GROUP_TILES * P)
+            for c in range(OUT_BLOCKS):
+                outputs = slice(c * P, (c + 1) * P)
+                bank = new_bank()
+                nc.tensor.matmul_mx(
+                    out=bank[:, rows],
+                    lhsT=w_codes["h"][:, outputs].bitcast(FP8X4),
+                    lhsT_scale=w_scales["h"][:, outputs],
+                    rhs=live[("codes_h", g)][:, rows].bitcast(FP8X4),
+                    rhs_scale=live[("scales_h", g)][:, rows],
+                    start=True,
+                    stop=True,
                 )
-            else:
                 nc.scalar.activation(
-                    out=u2t[:, c * 512 : (c + 1) * 512], in_=acc[:], func=ACT.Identity,
+                    out=u2_turned[:, c * H + rows.start : (c + 1) * H], in_=bank[:, rows], func=ACT.Identity,
                     bias=bias_cols[:, c : c + 1], scale=1.0,
                 )
+            live[("u2_turned", g)] = u2_turned
 
-        def h_product(g, vector_blocks=()):
-            for c in range(CH_BLOCKS):
-                h_block(g, c, c in vector_blocks)
-
-        def h_sums(g):
+        def turned_sums(g):
             codes = live[("codes_h", g)]
             scales = live[("scales_h", g)]
-            bank = psum_s.tile([P, 512], F32, tag="s")
-            for t in range(GROUP_TILES):
+            bank = psum_sums.tile([P, H], F32, tag="s")
+            for t in range(TURNED_FROM[g], GROUP_TILES):
                 rows = slice(t * P, (t + 1) * P)
-                for c in range(CH_BLOCKS):
+                for c in range(OUT_BLOCKS):
+                    outputs = slice(c * P, (c + 1) * P)
                     nc.tensor.matmul_mx(
                         out=bank[:, rows],
                         lhsT=codes[:, rows].bitcast(FP8X4),
                         lhsT_scale=scales[:, rows],
-                        rhs=w_codes["h"][:, c * P : (c + 1) * P].bitcast(FP8X4),
-                        rhs_scale=w_scales["h"][:, c * P : (c + 1) * P],
+                        rhs=w_codes["h"][:, outputs].bitcast(FP8X4),
+                        rhs_scale=w_scales["h"][:, outputs],
                         start=c == 0,
-                        stop=c == CH_BLOCKS - 1,
+                        stop=c == OUT_BLOCKS - 1,
                     )
             live[("sum_bank", g)] = bank
 
-        def h_means(g):
+        def turned_means(g):
             bank = live[("sum_bank", g)]
-            minus_mean2 = small.tile([P, GROUP_TILES], F32)
-            for t in range(GROUP_TILES):
+            minus_mean2 = small.tile([P, GROUP_TILES], F32, name="minus_mean2")
+            for t in range(TURNED_FROM[g], GROUP_TILES):
                 unused = work.tile([P, P], BF16, name="unused_means")
                 nc.scalar.activation(
                     out=unused[:], in_=bank[:, t * P : (t + 1) * P], func=ACT.Identity,
-                    bias=mean_bias[:], scale=-1.0 / H, accum_out=minus_mean2[:, t : t + 1],
+                    bias=mean_share[:], scale=-1.0 / H, accum_out=minus_mean2[:, t : t + 1],
                 )
             live[("minus_mean2", g)] = minus_mean2
 
-        def h_rows(g, t):
-            u2t = live[("u2t", g)]
-            bank = psum.tile([P, 512], F32, tag="bank")
-            for c in range(CH_BLOCKS):
+        def turn_back(g, t):
+            u2_turned = live[("u2_turned", g)]
+            bank = new_bank()
+            for c in range(OUT_BLOCKS):
                 nc.tensor.transpose(
-                    bank[:, c * P : (c + 1) * P], u2t[:, c * 512 + t * P : c * 512 + (t + 1) * P], identity[:]
+                    bank[:, c * P : (c + 1) * P], u2_turned[:, c * H + t * P : c * H + (t + 1) * P], identity[:]
                 )
             live[("u2", g, t)] = bank
 
-        def x_product(g, t):
-            acc = psum.tile([P, 512], F32, tag="bank")
-            nc.tensor.matmul_mx(
-                out=acc[:],
-                lhsT=live[("codes_x", g)][:, t * P : (t + 1) * P].bitcast(FP8X4),
-                lhsT_scale=live[("scales_x", g)][:, t * P : (t + 1) * P],
-                rhs=w_codes["x"][:].bitcast(FP8X4),
-                rhs_scale=w_scales["x"][:],
-                start=True,
-                stop=True,
+        def turned_moments(g, t):
+            cols = columns(t)
+            bank = live[("u2", g, t)]
+            minus_mean2 = live[("minus_mean2", g)][:, t : t + 1]
+            nc.vector.scalar_tensor_tensor(
+                out=live[("v", g)][:, cols], in0=bank[:], scalar=minus_mean2,
+                in1=live[("r", g)][:, cols], op0=ALU.add, op1=ALU.mult,
             )
-            live[("y1", g, t)] = acc
+            unused = work.tile([P, H], BF16, name="unused")
+            nc.scalar.activation(
+                out=unused[:], in_=bank[:], func=ACT.Square, bias=minus_mean2, scale=1.0,
+                accum_out=live[("squares", g)][:, GROUP_TILES + t : GROUP_TILES + t + 1],
+            )
 
         def new_moments(g):
             live[("u1", g)] = work.tile([P, GROUP_COLS], F32, name="u1")
             live[("v", g)] = work.tile([P, GROUP_COLS], F32, name="v")
-            live[("sums1", g)] = small.tile([P, GROUP_TILES], F32, name="sums1")
+            live[("sums_x", g)] = small.tile([P, GROUP_TILES], F32, name="sums1")
             live[("squares", g)] = small.tile([P, 2 * GROUP_TILES], F32, name="squares")
-            if g in ROW_GROUPS:
-                live[("sums2", g)] = small.tile([P, GROUP_TILES], F32, name="sums2")
-
-        def x_moments(g, t):
-            cols = slice(t * H, (t + 1) * H)
-            u1 = live[("u1", g)]
-            sums = live[("sums1", g)]
-            nc.vector.scalar_tensor_tensor(
-                out=u1[:, cols], in0=live[("y1", g, t)][:], scalar=1.0, in1=bias1[:],
-                op0=ALU.mult, op1=ALU.add, accum_out=sums[:, t : t + 1],
-            )
-            unused = work.tile([P, H], BF16, name="unused")
-            nc.scalar.activation(
-                out=unused[:], in_=u1[:, cols], func=ACT.Square,
-                bias=sums[:, t : t + 1], scale=-1.0 * H, accum_out=live[("squares", g)][:, t : t + 1],
-            )
-
-        def h_row_product(g, t):
-            acc = psum.tile([P, 512], F32, tag="bank")
-            nc.tensor.matmul_mx(
-                out=acc[:],
-                lhsT=live[("codes_h", g)][:, t * P : (t + 1) * P].bitcast(FP8X4),
-                lhsT_scale=live[("scales_h", g)][:, t * P : (t + 1) * P],
-                rhs=w_codes["h"][:].bitcast(FP8X4),
-                rhs_scale=w_scales["h"][:],
-                start=True,
-                stop=True,
-            )
-            live[("y2", g, t)] = acc
-
-        def h_row_moments(g, t):
-            cols = slice(t * H, (t + 1) * H)
-            v = live[("v", g)]
-            sums = live[("sums2", g)]
-            nc.vector.scalar_tensor_tensor(
-                out=v[:, cols], in0=live[("y2", g, t)][:], scalar=1.0, in1=bias2[:],
-                op0=ALU.mult, op1=ALU.add, accum_out=sums[:, t : t + 1],
-            )
-            unused = work.tile([P, H], BF16, name="unused")
-            nc.scalar.activation(
-                out=unused[:], in_=v[:, cols], func=ACT.Square,
-                bias=sums[:, t : t + 1], scale=-1.0 * H,
-                accum_out=live[("squares", g)][:, GROUP_TILES + t : GROUP_TILES + t + 1],
-            )
-
-        def row_means(g):
-            minus_mean2 = small.tile([P, GROUP_TILES], F32, name="minus_mean2_0")
-            nc.scalar.mul(out=minus_mean2[:], in_=live[("sums2", g)][:], mul=-1.0 / H)
-            live[("minus_mean2", g)] = minus_mean2
-
-        def reset_row(g, t):
-            cols = slice(t * H, (t + 1) * H)
-            v = live[("v", g)]
-            nc.vector.scalar_tensor_tensor(
-                out=v[:, cols], in0=v[:, cols], scalar=live[("minus_mean2", g)][:, t : t + 1],
-                in1=live[("r", g)][:, cols], op0=ALU.add, op1=ALU.mult,
-            )
-
-        def h_moments(g, t):
-            cols = slice(t * H, (t + 1) * H)
-            bank = live[("u2", g, t)]
-            minus_mean = live[("minus_mean2", g)][:, t : t + 1]
-            nc.vector.scalar_tensor_tensor(
-                out=live[("v", g)][:, cols], in0=bank[:], scalar=minus_mean,
-                in1=live[("r", g)][:, cols], op0=ALU.add, op1=ALU.mult,
-            )
-            unused = work.tile([P, H], BF16, name="unused")
-            nc.scalar.activation(
-                out=unused[:], in_=bank[:], func=ACT.Square,
-                bias=minus_mean, scale=1.0,
-                accum_out=live[("squares", g)][:, GROUP_TILES + t : GROUP_TILES + t + 1],
-            )
+            if TURNED_FROM[g] > 0:
+                live[("sums_h", g)] = small.tile([P, GROUP_TILES], F32, name="sums2")
 
         def variance(g):
-            var = small.tile([P, 2 * GROUP_TILES], F32)
-            if g in BY_SQRT:
-                for part, scale in ((first, 1.0 / (H * H * H)), (second, 1.0 / (H * H * H) if g in ROW_GROUPS else 1.0 / H)):
+            by_sqrt = g in SQRT_GROUPS
+            var = small.tile([P, 2 * GROUP_TILES], F32, name="var")
+            cut = GROUP_TILES + TURNED_FROM[g]
+            for part, scale in ((slice(0, cut), 1.0 / (H * H * H)), (slice(cut, 2 * GROUP_TILES), 1.0 / H)):
+                if part.start < part.stop:
                     nc.scalar.activation(
-                        out=var[:, part], in_=live[("squares", g)][:, part], func=ACT.Sqrt, bias=eps[:], scale=scale
+                        out=var[:, part], in_=live[("squares", g)][:, part], func=ACT.Sqrt if by_sqrt else ACT.Identity,
+                        bias=eps[:], scale=scale,
                     )
-                nc.scalar.activation(out=warm_up[:], in_=ones[:, 0:1], func=ACT.Tanh)
-                live[("var", g)] = var
-                return
-            for part, scale in ((first, 1.0 / (H * H * H)), (second, 1.0 / (H * H * H) if g in ROW_GROUPS else 1.0 / H)):
-                nc.scalar.activation(
-                    out=var[:, part], in_=live[("squares", g)][:, part], func=ACT.Identity, bias=eps[:], scale=scale
-                )
+            if by_sqrt:
+                nc.scalar.activation(out=table_load[:], in_=ones[:, 0:1], func=ACT.Tanh)
             live[("var", g)] = var
 
-        first = slice(0, GROUP_TILES)
-        second = slice(GROUP_TILES, 2 * GROUP_TILES)
+        def shift_step(g, rstd, shift):
+            nc.vector.scalar_tensor_tensor(
+                out=shift[:], in0=live[("sums_x", g)][:], scalar=-1.0 / H, in1=rstd[:, FIRST_NORM],
+                op0=ALU.mult, op1=ALU.mult,
+            )
 
-        def root_steps(g):
+        def plan_sqrt_roots(g):
+            std = live[("var", g)]
+            rstd = small.tile([P, 2 * GROUP_TILES], F32, name="rstd")
+            q = small.tile([P, GROUP_TILES], F32, name="q")
+            shift = small.tile([P, GROUP_TILES], F32, name="shift")
+            live[("scalar steps", g)] = []
+            live[("steps", g)] = [
+                lambda: nc.vector.reciprocal(out=rstd[:], in_=std[:]),
+                lambda: nc.vector.tensor_tensor(
+                    out=q[:], in0=std[:, FIRST_NORM], in1=rstd[:, SECOND_NORM], op=ALU.mult
+                ),
+                lambda: shift_step(g, rstd, shift),
+            ]
+            live[("rstd", g)] = rstd
+            live[("q", g)] = q
+            live[("shift", g)] = shift
+
+        def plan_iterated_roots(g):
             var = live[("var", g)]
-            if g in BY_SQRT:
-                std = var
-                rstd = small.tile([P, 2 * GROUP_TILES], F32, name="rstd")
-                q = small.tile([P, GROUP_TILES], F32, name="q")
-                shift = small.tile([P, GROUP_TILES], F32, name="shift")
-                live[("rstd", g)] = rstd
-                live[("q", g)] = q
-                live[("shift", g)] = shift
-                live[("steps", g)] = [
-                    lambda: nc.vector.reciprocal(out=rstd[:], in_=std[:]),
-                    lambda: nc.vector.tensor_tensor(out=q[:], in0=std[:, first], in1=rstd[:, second], op=ALU.mult),
-                    lambda: nc.vector.scalar_tensor_tensor(
-                        out=shift[:], in0=live[("sums1", g)][:], scalar=-1.0 / H, in1=rstd[:, first],
-                        op0=ALU.mult, op1=ALU.mult,
-                    ),
-                ]
-                return
+
+            def new(name):
+                return small.tile([P, 2 * GROUP_TILES], F32, name=name)
+
             guess = small.tile([P, 2 * GROUP_TILES], U32, name="guess")
             y0 = guess[:].bitcast(F32)
-            new = lambda name: small.tile([P, 2 * GROUP_TILES], F32, name=name)
-            a0 = new("root_a0")
-            b = new("root_b")
+            y0_squared = new("root_a0")
+            newton = new("root_b")
             y1 = new("root_y1")
-            a1 = new("root_a1")
-            s1 = new("root_s1")
+            y1_squared = new("root_a1")
+            y1_var = new("root_s1")
             w = new("root_w")
-            c1 = new("root_c1")
-            c2 = new("root_c2")
+            inner = new("root_c1")
+            outer = new("root_c2")
             rstd = new("rstd")
             std = new("std")
             q = small.tile([P, GROUP_TILES], F32, name="q")
             shift = small.tile([P, GROUP_TILES], F32, name="shift")
 
-            def times(out, in0, scalar, in1, op0):
+            def times(result, in0, scalar, in1, op0):
                 nc.vector.scalar_tensor_tensor(
-                    out=out[:], in0=in0, scalar=scalar, in1=in1, op0=op0, op1=ALU.mult
+                    out=result[:], in0=in0, scalar=scalar, in1=in1, op0=op0, op1=ALU.mult
                 )
 
             live[("scalar steps", g)] = [
                 lambda: nc.scalar.activation(
                     out=guess[:], in_=var[:].bitcast(U32), func=ACT.Copy, scale=-0.5, bias=ROOT_BITS
                 ),
-                lambda: nc.scalar.activation(out=a0[:], in_=y0, func=ACT.Square),
-                lambda: nc.scalar.activation(out=a1[:], in_=y1[:], func=ACT.Square, scale=1.0 / ROOT_SCALE),
+                lambda: nc.scalar.activation(out=y0_squared[:], in_=y0, func=ACT.Square),
+                lambda: nc.scalar.activation(
+                    out=y1_squared[:], in_=y1[:], func=ACT.Square, scale=1.0 / ROOT_SCALE
+                ),
             ]
             live[("steps", g)] = [
-                lambda: times(b, a0[:], -0.5 * ROOT_SCALE, var[:], ALU.mult),
-                lambda: times(y1, b[:], 1.5 * ROOT_SCALE, y0, ALU.add),
-                lambda: nc.vector.tensor_tensor(out=s1[:], in0=y1[:], in1=var[:], op=ALU.mult),
-                lambda: nc.vector.tensor_tensor(out=w[:], in0=a1[:], in1=var[:], op=ALU.mult),
-                lambda: times(c1, w[:], -4.2, w[:], ALU.add),
-                lambda: times(c2, c1[:], 7.0, w[:], ALU.add),
-                lambda: times(rstd, c2[:], -7.0, y1[:], ALU.add),
-                lambda: times(std, c2[:], -7.0, s1[:], ALU.add),
-                lambda: nc.vector.tensor_tensor(out=q[:], in0=std[:, first], in1=rstd[:, second], op=ALU.mult),
-                lambda: nc.vector.scalar_tensor_tensor(
-                    out=shift[:], in0=live[("sums1", g)][:], scalar=-1.0 / H, in1=rstd[:, first],
-                    op0=ALU.mult, op1=ALU.mult,
+                lambda: times(newton, y0_squared[:], -0.5 * ROOT_SCALE, var[:], ALU.mult),
+                lambda: times(y1, newton[:], 1.5 * ROOT_SCALE, y0, ALU.add),
+                lambda: nc.vector.tensor_tensor(out=y1_var[:], in0=y1[:], in1=var[:], op=ALU.mult),
+                lambda: nc.vector.tensor_tensor(out=w[:], in0=y1_squared[:], in1=var[:], op=ALU.mult),
+                lambda: times(inner, w[:], -4.2, w[:], ALU.add),
+                lambda: times(outer, inner[:], 7.0, w[:], ALU.add),
+                lambda: times(rstd, outer[:], -7.0, y1[:], ALU.add),
+                lambda: times(std, outer[:], -7.0, y1_var[:], ALU.add),
+                lambda: nc.vector.tensor_tensor(
+                    out=q[:], in0=std[:, FIRST_NORM], in1=rstd[:, SECOND_NORM], op=ALU.mult
                 ),
+                lambda: shift_step(g, rstd, shift),
             ]
             live[("rstd", g)] = rstd
             live[("q", g)] = q
             live[("shift", g)] = shift
 
-        def root_slot(g, place, t=0):
+        def plan_roots(g):
+            if g in SQRT_GROUPS:
+                plan_sqrt_roots(g)
+            else:
+                plan_iterated_roots(g)
+
+        def take_steps(kind, g, count):
+            steps = live.get((kind, g), [])
+            for step in steps[:count]:
+                step()
+            live[(kind, g)] = steps[count:]
+
+        def roots_behind(g, place, t=0):
             if g == LAST:
-                plan = {("blend", 2): 1, ("blend", 3): 2}
+                behind = {("blend", 2): 1, ("blend", 3): 2}
             elif g == LAST - 1:
-                plan = {
+                behind = {
                     ("weigh", 0): 1, ("weigh", 1): 1, ("weigh", 2): 1, ("weigh", 3): 1,
                     ("blend", 0): 1, ("blend", 1): 1, ("blend", 2): 4,
                 }
             else:
-                plan = {
+                behind = {
                     ("weigh", 1): 1, ("weigh", 2): 1, ("weigh", 3): 1, ("quantise h", 0): 1, ("blend", 0): 1,
                     ("quantise x", 0): 1, ("blend", 1): 2, ("blend", 2): 2,
                 }
-            root_step(g, plan.get((place, t), 0))
-
-        def scalar_step(g):
-            steps = live.get(("scalar steps", g), [])
-            if steps:
-                steps[0]()
-            live[("scalar steps", g)] = steps[1:]
-
-        def root_step(g, count=1):
-            steps = live.get(("steps", g), [])
-            for step in steps[:count]:
-                step()
-            live[("steps", g)] = steps[count:]
+            take_steps("steps", g, behind.get((place, t), 0))
 
         def combine(g, t):
-            cols = slice(t * H, (t + 1) * H)
+            cols = columns(t)
             v = live[("v", g)]
             nc.vector.scalar_tensor_tensor(
                 out=v[:, cols], in0=v[:, cols], scalar=live[("q", g)][:, t : t + 1],
@@ -464,7 +444,7 @@ def tile_layernormgrucell_pb_t_kernel(tc, x, h, r, z, W_in, b_in, W_hn, b_hn, ou
         def squash(g, t):
             if t == 0:
                 live[("n", g)] = candidates.tile([P, GROUP_COLS], F32, name="n_sb")
-            cols = slice(t * H, (t + 1) * H)
+            cols = columns(t)
             nc.scalar.activation(
                 out=live[("n", g)][:, cols], in_=live[("v", g)][:, cols], func=ACT.Tanh,
                 bias=live[("shift", g)][:, t : t + 1], scale=live[("rstd", g)][:, t : t + 1],
@@ -481,102 +461,115 @@ def tile_layernormgrucell_pb_t_kernel(tc, x, h, r, z, W_in, b_in, W_hn, b_hn, ou
             z_sb = live[("z", g)]
             n_sb = live[("n", g)]
             for t in tiles:
-                cols = slice(t * H, (t + 1) * H)
+                cols = columns(t)
                 nc.vector.scalar_tensor_tensor(
                     out=n_sb[:, cols], in0=z_sb[:, cols], scalar=1.0, in1=n_sb[:, cols],
                     op0=ALU.subtract, op1=ALU.mult,
                 )
-                root_slot(g + 1, "weigh", t)
-                if (g, t) in ON_TENSOR:
+                roots_behind(g + 1, "weigh", t)
+                if on_tensor(g, t):
                     blend_on_tensor(g, t)
+
+        def on_tensor(g, t):
+            return g == LAST - 1 and t in TENSOR_BLENDS
+
+        def store(g, source, cols):
+            first_col = g * GROUP_COLS + cols.start
+            nc.sync.dma_start(
+                out=out_rows[:, first_col : first_col + cols.stop - cols.start], in_=source[:, cols]
+            )
+
         def blend_on_tensor(g, t):
-            cols = slice(t * H, (t + 1) * H)
-            bank = psum.tile([P, 512], F32, tag="bank")
+            cols = columns(t)
+            bank = new_bank()
             nc.tensor.matmul(out=bank[:], lhsT=identity[:], rhs=live[("zh", g)][:, cols], start=True, stop=False)
             nc.tensor.matmul(out=bank[:], lhsT=minus_identity[:], rhs=live[("n", g)][:, cols], start=False, stop=True)
             live[("blend", g, t)] = bank
 
         def store_from_tensor(g, t):
-            cols = slice(t * H, (t + 1) * H)
-            done = live[("n", g)]
-            nc.scalar.copy(out=done[:, cols], in_=live[("blend", g, t)][:])
-            first_col = g * GROUP_COLS + cols.start
-            nc.sync.dma_start(out=out_rows[:, first_col : first_col + H], in_=done[:, cols])
+            cols = columns(t)
+            n_sb = live[("n", g)]
+            nc.scalar.copy(out=n_sb[:, cols], in_=live[("blend", g, t)][:])
+            store(g, n_sb, cols)
 
         def blend(g, tiles):
             n_sb = live[("n", g)]
             zh = live[("zh", g)]
             for t in tiles:
-                if (g, t) in ON_TENSOR:
+                if on_tensor(g, t):
                     continue
-                cols = slice(t * H, (t + 1) * H)
+                cols = columns(t)
                 nc.vector.tensor_tensor(out=zh[:, cols], in0=zh[:, cols], in1=n_sb[:, cols], op=ALU.subtract)
                 if g >= LAST - 1:
-                    first_col = g * GROUP_COLS + cols.start
-                    nc.sync.dma_start(out=out_rows[:, first_col : first_col + H], in_=zh[:, cols])
+                    store(g, zh, cols)
                 elif t % 2 == 1:
-                    half = HALVES[t // 2]
-                    first_col = g * GROUP_COLS + half.start
-                    nc.sync.dma_start(out=out_rows[:, first_col : first_col + HALF_COLS], in_=zh[:, half])
-                root_slot(g + 1, "blend", t)
+                    store(g, zh, slice((t - 1) * H, (t + 1) * H))
+                roots_behind(g + 1, "blend", t)
 
         on_vector = nc.vector.tensor_copy
         on_scalar = nc.scalar.copy
-        prepare_weight("h")
+        bias_wide = {}
+        transpose_weight("h", (on_vector, on_scalar))
         transpose_operand("h", 0, (on_vector, on_scalar))
         quantise_weight("h")
         quantise_operand("h", 0)
-        bias2_bank = psum.tile([P, 512], F32, tag="bank")
-        nc.tensor.matmul(out=bias2_bank[:], lhsT=ones[:, 0:P], rhs=bias_rows[:, H : 2 * H], start=True, stop=True)
-        bias2 = const.tile([P, H], F32)
-        bias_sum = const.tile([P, 1], F32)
-        mean_bias = const.tile([P, 1], F32)
-        nc.scalar.activation(out=bias2[:], in_=bias2_bank[:], func=ACT.Copy, scale=1.0, accum_out=bias_sum[:])
-        nc.scalar.mul(out=mean_bias[:], in_=bias_sum[:], mul=-1.0 / (H * P))
-        prepare_weight("x", (on_scalar, on_vector))
+        bank = new_bank()
+        nc.tensor.matmul(out=bank[:], lhsT=ones[:, 0:P], rhs=bias_rows[:, H : 2 * H], start=True, stop=True)
+        bias_wide["h"] = const.tile([P, H], F32, name="bias2")
+        bias_total = const.tile([P, 1], F32)
+        mean_share = const.tile([P, 1], F32)
+        nc.scalar.activation(
+            out=bias_wide["h"][:], in_=bank[:], func=ACT.Copy, scale=1.0, accum_out=bias_total[:]
+        )
+        nc.scalar.mul(out=mean_share[:], in_=bias_total[:], mul=-1.0 / (H * P))
+        transpose_weight("x", (on_scalar, on_vector))
         quantise_weight("x")
-        transpose_operand("x", 0, (on_scalar, on_scalar))
+        transpose_operand("x", 0)
         new_moments(0)
         for t in range(GROUP_TILES):
-            h_row_product(0, t)
-        bias_bank = psum_s.tile([P, 512], F32, tag="s")
-        nc.tensor.matmul(out=bias_bank[:], lhsT=ones[:, 0:P], rhs=bias_rows[:, 0:H], start=True, stop=True)
-        bias1 = const.tile([P, H], F32)
-        nc.scalar.copy(out=bias1[:], in_=bias_bank[:])
+            row_product("h", 0, t)
+        bank = psum_sums.tile([P, H], F32, tag="s")
+        nc.tensor.matmul(out=bank[:], lhsT=ones[:, 0:P], rhs=bias_rows[:, 0:H], start=True, stop=True)
+        bias_wide["x"] = const.tile([P, H], F32, name="bias1")
+        nc.scalar.copy(out=bias_wide["x"][:], in_=bank[:])
         for t in range(GROUP_TILES):
-            h_row_moments(0, t)
+            row_moments("h", 0, t)
             if t == 1:
                 quantise_operand("x", 0)
-        cols_bank = psum_s.tile([P, 512], F32, tag="s")
-        for c in range(CH_BLOCKS):
+        bank = psum_sums.tile([P, H], F32, tag="s")
+        for c in range(OUT_BLOCKS):
             nc.tensor.matmul(
-                out=cols_bank[:, c : c + 1], lhsT=bias_rows[:, H + c * P : H + (c + 1) * P], rhs=ones[:, 0:1],
+                out=bank[:, c : c + 1], lhsT=bias_rows[:, H + c * P : H + (c + 1) * P], rhs=ones[:, 0:1],
                 start=True, stop=True,
             )
-        bias_cols = const.tile([P, CH_BLOCKS], F32)
-        nc.scalar.copy(out=bias_cols[:], in_=cols_bank[:, 0:CH_BLOCKS])
+        bias_cols = const.tile([P, OUT_BLOCKS], F32)
+        nc.scalar.copy(out=bias_cols[:], in_=bank[:, 0:OUT_BLOCKS])
         for t in range(GROUP_TILES):
-            x_product(0, t)
+            row_product("x", 0, t)
         row_means(0)
 
-        def row_window(a):
-            new_moments(a)
+        def row_window(g):
+            new_moments(g)
             for t in range(GROUP_TILES):
-                h_row_moments(a, t)
+                if t < TURNED_FROM[g]:
+                    row_moments("h", g, t)
+                if t + 2 < TURNED_FROM[g]:
+                    row_product("h", g, t + 2)
+                row_moments("x", g, t)
                 if t < 2:
-                    h_row_product(a, t + 2)
-                x_moments(a, t)
-                if t < 2:
-                    x_product(a, t + 2)
-            row_means(a)
+                    row_product("x", g, t + 2)
+                if t + 1 == TURNED_FROM[g]:
+                    row_means(g)
+                if t >= TURNED_FROM[g]:
+                    turned_moments(g, t)
 
-        def window(a):
-            new_moments(a)
+        def window(g):
+            new_moments(g)
             for t in range(GROUP_TILES):
-                x_moments(a, t)
-                h_moments(a, t)
-                if t < 1:
-                    h_rows(a, t + 3)
+                row_moments("x", g, t)
+                turned_moments(g, t)
+                if t == 0:
+                    turn_back(g, 3)
 
         def load_step(s):
             if s + 2 < GROUPS:
@@ -588,22 +581,27 @@ def tile_layernormgrucell_pb_t_kernel(tc, x, h, r, z, W_in, b_in, W_hn, b_hn, ou
         load_step(1)
         gate_product(0)
         for t in range(GROUP_TILES):
-            x_moments(0, t)
+            row_moments("x", 0, t)
         transpose_operand("h", 1, (on_vector, on_vector))
-        transpose_operand("x", 1, (on_scalar, on_scalar))
+        transpose_operand("x", 1)
         variance(0)
-        root_steps(0)
+        plan_roots(0)
         quantise_operand("h", 1)
+        turned_product(1)
         for t in range(2):
-            h_row_product(1, t)
+            row_product("h", 1, t)
         for t in range(GROUP_TILES):
             reset_row(0, t)
             if t == 1:
                 quantise_operand("x", 1)
             if t > 0:
-                root_step(0)
+                take_steps("steps", 0, 1)
+        turned_sums(1)
         for t in range(2):
-            x_product(1, t)
+            row_product("x", 1, t)
+        for t in range(TURNED_FROM[1], GROUP_TILES):
+            turn_back(1, t)
+        turned_means(1)
         transpose_operand("h", 2)
         transpose_operand("x", 2)
         for s in range(2, GROUPS + 2):
@@ -612,7 +610,7 @@ def tile_layernormgrucell_pb_t_kernel(tc, x, h, r, z, W_in, b_in, W_hn, b_hn, ou
             load_step(s)
             if a < GROUPS:
                 gate_product(a)
-                if a in ROW_GROUPS:
+                if a == 1:
                     row_window(a)
                 else:
                     window(a)
@@ -620,41 +618,42 @@ def tile_layernormgrucell_pb_t_kernel(tc, x, h, r, z, W_in, b_in, W_hn, b_hn, ou
                 quantise_operand("h", 2)
                 quantise_operand("x", 2)
             if s < GROUPS:
-                h_sums(s)
+                turned_sums(s)
             for t in range(GROUP_TILES):
                 combine(b, t)
                 squash(b, t)
-                if t == (3 if a == LAST else 0) and a < GROUPS:
+                if a < GROUPS and t == (3 if a == LAST else 0):
                     variance(a)
-                    root_steps(a)
+                    plan_roots(a)
                 elif t < 3:
-                    scalar_step(a)
+                    take_steps("scalar steps", a, 1)
             if b == LAST:
-                for g, t in ON_TENSOR:
-                    store_from_tensor(g, t)
+                for t in TENSOR_BLENDS:
+                    store_from_tensor(LAST - 1, t)
+            if a == 1:
+                for t in range(TURNED_FROM[1]):
+                    reset_row(1, t)
             weigh(b, (0,))
             if s + 1 < GROUPS:
                 transpose_operand("h", s + 1)
-            weigh(b, (1,) if a == LAST - 1 else (1, 2))
-            scalar_step(a)
+            early = (1,) if a == LAST - 1 else (1, 2)
+            weigh(b, early)
+            take_steps("scalar steps", a, 1)
             if s + 1 < GROUPS:
                 transpose_operand("x", s + 1)
-            weigh(b, (2, 3) if a == LAST - 1 else (3,))
-            if a in ROW_GROUPS:
-                for t in range(GROUP_TILES):
-                    reset_row(a, t)
+            weigh(b, range(1 + len(early), GROUP_TILES))
             if s + 1 < GROUPS:
                 quantise_operand("h", s + 1)
-            root_slot(a, "quantise h")
+            roots_behind(a, "quantise h")
             blend(b, (0,))
             if s + 1 < GROUPS:
                 quantise_operand("x", s + 1)
-            root_slot(a, "quantise x")
+            roots_behind(a, "quantise x")
             if s < GROUPS:
-                h_product(s)
+                turned_product(s)
                 for t in range(GROUP_TILES):
-                    x_product(s, t)
+                    row_product("x", s, t)
                 for t in range(3):
-                    h_rows(s, t)
-                h_means(s)
+                    turn_back(s, t)
+                turned_means(s)
             blend(b, (1, 2, 3))

from contextlib import ExitStack

import concourse.mybir as mybir
from concourse.masks import make_identity

F32 = mybir.dt.float32
BF16 = mybir.dt.bfloat16
U32 = mybir.dt.uint32
U8 = mybir.dt.uint8
FP8X4 = mybir.dt.float8_e4m3fn_x4
ALU = mybir.AluOpType
ACT = mybir.ActivationFunctionType

P = 128
B = 4096
K = 512
H = 512
OUT_BLOCKS = H // P
WORDS = K // 2
ROW_TILES = B // P
GROUP_TILES = 4
GROUPS = ROW_TILES // GROUP_TILES
LAST = GROUPS - 1
GROUP_COLS = GROUP_TILES * H
HALF_COLS = GROUP_COLS // 2
EPS = 1e-5
FIRST_NORM = slice(0, GROUP_TILES)
SECOND_NORM = slice(GROUP_TILES, 2 * GROUP_TILES)

TURNED_FROM = (4, 3) + (GROUPS - 2) * (0,)
SQRT_GROUPS = (0, LAST)
TENSOR_BLENDS = (0, 1)
WARM_UPS = 3

ROOT_BITS = 1597463007.0
ROOT_SCALE = -5.0 / 16.0

FLOPS = 2 * 2 * B * K * H


def tile_layernormgrucell_pb_t_kernel(tc, x, h, r, z, W_in, b_in, W_hn, b_hn, out):
    nc = tc.nc
    by_row_tile = "(p t) k -> p (t k)"
    dram = {
        "x": x.rearrange(by_row_tile, t=ROW_TILES),
        "h": h.rearrange(by_row_tile, t=ROW_TILES),
        "r": r.rearrange(by_row_tile, t=ROW_TILES),
        "z": z.rearrange(by_row_tile, t=ROW_TILES),
    }
    out_rows = out.rearrange(by_row_tile, t=ROW_TILES)

    with ExitStack() as ctx:
        const = ctx.enter_context(tc.tile_pool(name="const", bufs=1))
        inputs = {
            "x": ctx.enter_context(tc.tile_pool(name="in_x", bufs=3)),
            "h": ctx.enter_context(tc.tile_pool(name="in_h", bufs=5)),
            "r": ctx.enter_context(tc.tile_pool(name="in_r", bufs=3)),
            "z": ctx.enter_context(tc.tile_pool(name="in_z", bufs=3)),
        }
        work = ctx.enter_context(tc.tile_pool(name="work", bufs=2))
        candidates = ctx.enter_context(tc.tile_pool(name="candidates", bufs=4))
        small = ctx.enter_context(tc.tile_pool(name="small", bufs=3))
        psum = ctx.enter_context(tc.psum_pool(name="psum", bufs=7))
        psum_sums = ctx.enter_context(tc.psum_pool(name="psum_s", bufs=1))
        ctx.enter_context(tc.manual_schedule())

        live = {}

        def columns(t):
            return slice(t * H, (t + 1) * H)

        def new_bank():
            bank = psum.tile([P, H], F32, tag="bank")
            return bank

        def new_input(name, g):
            live[(name, g)] = inputs[name].tile([P, GROUP_COLS], BF16, name="in_" + name)

        def fetch(name, g, lo, hi):
            nc.sync.dma_start(
                out=live[(name, g)][:, lo:hi], in_=dram[name][:, g * GROUP_COLS + lo : g * GROUP_COLS + hi]
            )

        def load_activations(g):
            new_input("h", g)
            new_input("x", g)
            for lo in (0, HALF_COLS):
                fetch("h", g, lo, lo + HALF_COLS)
                fetch("x", g, lo, lo + HALF_COLS)

        def load_gate(name, g):
            new_input(name, g)
            fetch(name, g, 0, GROUP_COLS)

        def load_weight_half(name, w, pair):
            nc.sync.dma_start(
                out=w_raw[name][:, pair * 2 * K : (pair + 1) * 2 * K].rearrange("p (a k) -> p a k", a=2),
                in_=w[pair * 2 * P : (pair + 1) * 2 * P, :].rearrange("(a p) k -> p a k", p=P),
            )

        ones = const.tile([P, H], BF16)
        nc.vector.memset(ones[:], 1.0)
        bias_rows = const.tile([P, 2 * H], BF16)
        nc.vector.memset(bias_rows[:], 0.0)
        warm_bank = psum_sums.tile([P, H], F32, tag="s")
        for i in range(WARM_UPS):
            nc.tensor.matmul(out=warm_bank[:], lhsT=ones[:, 0:P], rhs=ones[:], start=True, stop=True)
        nc.scalar.dma_start(out=bias_rows[0:1, 0:H], in_=b_in.rearrange("(o n) -> o n", o=1))
        nc.scalar.dma_start(out=bias_rows[0:1, H : 2 * H], in_=b_hn.rearrange("(o n) -> o n", o=1))
        identity = const.tile([P, P], F32)
        make_identity(nc, identity[:])
        minus_identity = const.tile([P, P], F32)
        nc.gpsimd.tensor_scalar(
            out=minus_identity[:], in0=identity[:], scalar1=-1.0, scalar2=0.0, op0=ALU.mult, op1=ALU.add
        )
        eps = const.tile([P, 1], F32)
        nc.gpsimd.memset(eps[:], EPS)
        table_load = const.tile([P, 1], F32)
        nc.scalar.activation(out=table_load[:], in_=ones[:, 0:1], func=ACT.Sqrt)

        new_input("h", 0)
        new_input("x", 0)
        w_raw = {}
        for name, w in (("h", W_hn), ("x", W_in)):
            w_raw[name] = const.tile([P, OUT_BLOCKS * K], BF16, name="w_sb_" + name)
            for pair in range(2):
                load_weight_half(name, w, pair)
            for lo in (0, HALF_COLS):
                fetch(name, 0, lo, lo + HALF_COLS)
        load_gate("r", 0)
        load_activations(1)
        load_gate("z", 0)
        load_activations(2)

        w_grouped = {}
        w_codes = {}
        w_scales = {}

        def transpose_weight(name, copy_out):
            words = w_raw[name][:].bitcast(F32)
            w_grouped[name] = const.tile([P, 4 * H], BF16, name="w_grouped_" + name, align_bytes=64)
            grouped_words = w_grouped[name][:].bitcast(F32)
            for pair in range(2):
                bank = new_bank()
                for u in range(2):
                    for j in range(2):
                        a = 2 * pair + j
                        nc.tensor.transpose(
                            bank[:, u * 256 + j * P : u * 256 + (j + 1) * P],
                            words[:, a * WORDS + u * P : a * WORDS + (u + 1) * P],
                            identity[:],
                        )
                copy_out[pair](
                    out=grouped_words[:, pair * 512 : (pair + 1) * 512].rearrange("p (n u) -> p n u", u=2),
                    in_=bank[:].rearrange("p (u n) -> p n u", u=2),
                )

        def quantise_weight(name):
            w_codes[name] = const.tile([P, H], U32, name="w_codes_" + name, align_bytes=64)
            w_scales[name] = const.tile([P, H], U8, name="w_scales_" + name, align_bytes=64)
            nc.vector.quantize_mx(
                out=w_codes[name][:].bitcast(FP8X4), scales=w_scales[name][:], in_=w_grouped[name][:]
            )

        def transpose_operand(name, g, copy_out=(nc.scalar.copy, nc.scalar.copy)):
            words = live[(name, g)][:].bitcast(F32)
            grouped = work.tile([P, GROUP_COLS], BF16, name="grouped_" + name, align_bytes=64)
            grouped_words = grouped[:].bitcast(F32)
            for pair in range(GROUP_TILES // 2):
                bank = new_bank()
                for j in range(2):
                    t = 2 * pair + j
                    for u in range(2):
                        nc.tensor.transpose(
                            bank[:, (2 * j + u) * P : (2 * j + u + 1) * P],
                            words[:, t * WORDS + u * P : t * WORDS + (u + 1) * P],
                            identity[:],
                        )
                copy_out[pair](
                    out=grouped_words[:, pair * 512 : (pair + 1) * 512].rearrange("p (j i u) -> p j i u", j=2, u=2),
                    in_=bank[:].rearrange("p (j u i) -> p j i u", j=2, u=2),
                )
            live[("grouped_" + name, g)] = grouped

        def quantise_operand(name, g):
            codes = work.tile([P, GROUP_TILES * P], U32, name="codes_" + name, align_bytes=64)
            scales = work.tile([P, GROUP_TILES * P], U8, name="scales_" + name, align_bytes=64)
            nc.vector.quantize_mx(
                out=codes[:].bitcast(FP8X4), scales=scales[:], in_=live[("grouped_" + name, g)][:]
            )
            live[("codes_" + name, g)] = codes
            live[("scales_" + name, g)] = scales

        def row_product(name, g, t):
            rows = slice(t * P, (t + 1) * P)
            bank = new_bank()
            nc.tensor.matmul_mx(
                out=bank[:],
                lhsT=live[("codes_" + name, g)][:, rows].bitcast(FP8X4),
                lhsT_scale=live[("scales_" + name, g)][:, rows],
                rhs=w_codes[name][:].bitcast(FP8X4),
                rhs_scale=w_scales[name][:],
                start=True,
                stop=True,
            )
            live[("product_" + name, g, t)] = bank

        def row_moments(name, g, t):
            cols = columns(t)
            u = live[("u1" if name == "x" else "v", g)]
            total = live[("sums_" + name, g)][:, t : t + 1]
            norm = FIRST_NORM if name == "x" else SECOND_NORM
            nc.vector.scalar_tensor_tensor(
                out=u[:, cols], in0=live[("product_" + name, g, t)][:], scalar=1.0, in1=bias_wide[name][:],
                op0=ALU.mult, op1=ALU.add, accum_out=total,
            )
            unused = work.tile([P, H], BF16, name="unused")
            nc.scalar.activation(
                out=unused[:], in_=u[:, cols], func=ACT.Square, bias=total, scale=-1.0 * H,
                accum_out=live[("squares", g)][:, norm.start + t : norm.start + t + 1],
            )

        def row_means(g):
            rows = slice(0, TURNED_FROM[g])
            minus_mean2 = small.tile([P, GROUP_TILES], F32, name="minus_mean2_0")
            nc.scalar.mul(out=minus_mean2[:, rows], in_=live[("sums_h", g)][:, rows], mul=-1.0 / H)
            live[("row_minus_mean2", g)] = minus_mean2

        def reset_row(g, t):
            cols = columns(t)
            v = live[("v", g)]
            nc.vector.scalar_tensor_tensor(
                out=v[:, cols], in0=v[:, cols], scalar=live[("row_minus_mean2", g)][:, t : t + 1],
                in1=live[("r", g)][:, cols], op0=ALU.add, op1=ALU.mult,
            )

        def turned_product(g):
            u2_turned = work.tile([P, OUT_BLOCKS * H], F32, name="u2t")
            rows = slice(TURNED_FROM[g] * P, GROUP_TILES * P)
            for c in range(OUT_BLOCKS):
                outputs = slice(c * P, (c + 1) * P)
                bank = new_bank()
                nc.tensor.matmul_mx(
                    out=bank[:, rows],
                    lhsT=w_codes["h"][:, outputs].bitcast(FP8X4),
                    lhsT_scale=w_scales["h"][:, outputs],
                    rhs=live[("codes_h", g)][:, rows].bitcast(FP8X4),
                    rhs_scale=live[("scales_h", g)][:, rows],
                    start=True,
                    stop=True,
                )
                nc.scalar.activation(
                    out=u2_turned[:, c * H + rows.start : (c + 1) * H], in_=bank[:, rows], func=ACT.Identity,
                    bias=bias_cols[:, c : c + 1], scale=1.0,
                )
            live[("u2_turned", g)] = u2_turned

        def turned_sums(g):
            codes = live[("codes_h", g)]
            scales = live[("scales_h", g)]
            bank = psum_sums.tile([P, H], F32, tag="s")
            for t in range(TURNED_FROM[g], GROUP_TILES):
                rows = slice(t * P, (t + 1) * P)
                for c in range(OUT_BLOCKS):
                    outputs = slice(c * P, (c + 1) * P)
                    nc.tensor.matmul_mx(
                        out=bank[:, rows],
                        lhsT=codes[:, rows].bitcast(FP8X4),
                        lhsT_scale=scales[:, rows],
                        rhs=w_codes["h"][:, outputs].bitcast(FP8X4),
                        rhs_scale=w_scales["h"][:, outputs],
                        start=c == 0,
                        stop=c == OUT_BLOCKS - 1,
                    )
            live[("sum_bank", g)] = bank

        def turned_means(g):
            bank = live[("sum_bank", g)]
            minus_mean2 = small.tile([P, GROUP_TILES], F32, name="minus_mean2")
            for t in range(TURNED_FROM[g], GROUP_TILES):
                unused = work.tile([P, P], BF16, name="unused_means")
                nc.scalar.activation(
                    out=unused[:], in_=bank[:, t * P : (t + 1) * P], func=ACT.Identity,
                    bias=mean_share[:], scale=-1.0 / H, accum_out=minus_mean2[:, t : t + 1],
                )
            live[("minus_mean2", g)] = minus_mean2

        def turn_back(g, t):
            u2_turned = live[("u2_turned", g)]
            bank = new_bank()
            for c in range(OUT_BLOCKS):
                nc.tensor.transpose(
                    bank[:, c * P : (c + 1) * P], u2_turned[:, c * H + t * P : c * H + (t + 1) * P], identity[:]
                )
            live[("u2", g, t)] = bank

        def turned_moments(g, t):
            cols = columns(t)
            bank = live[("u2", g, t)]
            minus_mean2 = live[("minus_mean2", g)][:, t : t + 1]
            nc.vector.scalar_tensor_tensor(
                out=live[("v", g)][:, cols], in0=bank[:], scalar=minus_mean2,
                in1=live[("r", g)][:, cols], op0=ALU.add, op1=ALU.mult,
            )
            unused = work.tile([P, H], BF16, name="unused")
            nc.scalar.activation(
                out=unused[:], in_=bank[:], func=ACT.Square, bias=minus_mean2, scale=1.0,
                accum_out=live[("squares", g)][:, GROUP_TILES + t : GROUP_TILES + t + 1],
            )

        def new_moments(g):
            live[("u1", g)] = work.tile([P, GROUP_COLS], F32, name="u1")
            live[("v", g)] = work.tile([P, GROUP_COLS], F32, name="v")
            live[("sums_x", g)] = small.tile([P, GROUP_TILES], F32, name="sums1")
            live[("squares", g)] = small.tile([P, 2 * GROUP_TILES], F32, name="squares")
            if TURNED_FROM[g] > 0:
                live[("sums_h", g)] = small.tile([P, GROUP_TILES], F32, name="sums2")

        def variance(g):
            by_sqrt = g in SQRT_GROUPS
            var = small.tile([P, 2 * GROUP_TILES], F32, name="var")
            cut = GROUP_TILES + TURNED_FROM[g]
            for part, scale in ((slice(0, cut), 1.0 / (H * H * H)), (slice(cut, 2 * GROUP_TILES), 1.0 / H)):
                if part.start < part.stop:
                    nc.scalar.activation(
                        out=var[:, part], in_=live[("squares", g)][:, part], func=ACT.Sqrt if by_sqrt else ACT.Identity,
                        bias=eps[:], scale=scale,
                    )
            if by_sqrt:
                nc.scalar.activation(out=table_load[:], in_=ones[:, 0:1], func=ACT.Tanh)
            live[("var", g)] = var

        def shift_step(g, rstd, shift):
            nc.vector.scalar_tensor_tensor(
                out=shift[:], in0=live[("sums_x", g)][:], scalar=-1.0 / H, in1=rstd[:, FIRST_NORM],
                op0=ALU.mult, op1=ALU.mult,
            )

        def plan_sqrt_roots(g):
            std = live[("var", g)]
            rstd = small.tile([P, 2 * GROUP_TILES], F32, name="rstd")
            q = small.tile([P, GROUP_TILES], F32, name="q")
            shift = small.tile([P, GROUP_TILES], F32, name="shift")
            live[("scalar steps", g)] = []
            live[("steps", g)] = [
                lambda: nc.vector.reciprocal(out=rstd[:], in_=std[:]),
                lambda: nc.vector.tensor_tensor(
                    out=q[:], in0=std[:, FIRST_NORM], in1=rstd[:, SECOND_NORM], op=ALU.mult
                ),
                lambda: shift_step(g, rstd, shift),
            ]
            live[("rstd", g)] = rstd
            live[("q", g)] = q
            live[("shift", g)] = shift

        def plan_iterated_roots(g):
            var = live[("var", g)]

            def new(name):
                return small.tile([P, 2 * GROUP_TILES], F32, name=name)

            guess = small.tile([P, 2 * GROUP_TILES], U32, name="guess")
            y0 = guess[:].bitcast(F32)
            y0_squared = new("root_a0")
            newton = new("root_b")
            y1 = new("root_y1")
            y1_squared = new("root_a1")
            y1_var = new("root_s1")
            w = new("root_w")
            inner = new("root_c1")
            outer = new("root_c2")
            rstd = new("rstd")
            std = new("std")
            q = small.tile([P, GROUP_TILES], F32, name="q")
            shift = small.tile([P, GROUP_TILES], F32, name="shift")

            def times(result, in0, scalar, in1, op0):
                nc.vector.scalar_tensor_tensor(
                    out=result[:], in0=in0, scalar=scalar, in1=in1, op0=op0, op1=ALU.mult
                )

            live[("scalar steps", g)] = [
                lambda: nc.scalar.activation(
                    out=guess[:], in_=var[:].bitcast(U32), func=ACT.Copy, scale=-0.5, bias=ROOT_BITS
                ),
                lambda: nc.scalar.activation(out=y0_squared[:], in_=y0, func=ACT.Square),
                lambda: nc.scalar.activation(
                    out=y1_squared[:], in_=y1[:], func=ACT.Square, scale=1.0 / ROOT_SCALE
                ),
            ]
            live[("steps", g)] = [
                lambda: times(newton, y0_squared[:], -0.5 * ROOT_SCALE, var[:], ALU.mult),
                lambda: times(y1, newton[:], 1.5 * ROOT_SCALE, y0, ALU.add),
                lambda: nc.vector.tensor_tensor(out=y1_var[:], in0=y1[:], in1=var[:], op=ALU.mult),
                lambda: nc.vector.tensor_tensor(out=w[:], in0=y1_squared[:], in1=var[:], op=ALU.mult),
                lambda: times(inner, w[:], -4.2, w[:], ALU.add),
                lambda: times(outer, inner[:], 7.0, w[:], ALU.add),
                lambda: times(rstd, outer[:], -7.0, y1[:], ALU.add),
                lambda: times(std, outer[:], -7.0, y1_var[:], ALU.add),
                lambda: nc.vector.tensor_tensor(
                    out=q[:], in0=std[:, FIRST_NORM], in1=rstd[:, SECOND_NORM], op=ALU.mult
                ),
                lambda: shift_step(g, rstd, shift),
            ]
            live[("rstd", g)] = rstd
            live[("q", g)] = q
            live[("shift", g)] = shift

        def plan_roots(g):
            if g in SQRT_GROUPS:
                plan_sqrt_roots(g)
            else:
                plan_iterated_roots(g)

        def take_steps(kind, g, count):
            steps = live.get((kind, g), [])
            for step in steps[:count]:
                step()
            live[(kind, g)] = steps[count:]

        def roots_behind(g, place, t=0):
            if g == LAST:
                behind = {("blend", 2): 1, ("blend", 3): 2}
            elif g == LAST - 1:
                behind = {
                    ("weigh", 0): 1, ("weigh", 1): 1, ("weigh", 2): 1, ("weigh", 3): 1,
                    ("blend", 0): 1, ("blend", 1): 1, ("blend", 2): 4,
                }
            else:
                behind = {
                    ("weigh", 1): 1, ("weigh", 2): 1, ("weigh", 3): 1, ("quantise h", 0): 1, ("blend", 0): 1,
                    ("quantise x", 0): 1, ("blend", 1): 2, ("blend", 2): 2,
                }
            take_steps("steps", g, behind.get((place, t), 0))

        def combine(g, t):
            cols = columns(t)
            v = live[("v", g)]
            nc.vector.scalar_tensor_tensor(
                out=v[:, cols], in0=v[:, cols], scalar=live[("q", g)][:, t : t + 1],
                in1=live[("u1", g)][:, cols], op0=ALU.mult, op1=ALU.add,
            )

        def squash(g, t):
            if t == 0:
                live[("n", g)] = candidates.tile([P, GROUP_COLS], F32, name="n_sb")
            cols = columns(t)
            nc.scalar.activation(
                out=live[("n", g)][:, cols], in_=live[("v", g)][:, cols], func=ACT.Tanh,
                bias=live[("shift", g)][:, t : t + 1], scale=live[("rstd", g)][:, t : t + 1],
            )

        def gate_product(g):
            zh = live[("n", g - 2)] if g > 1 else candidates.tile([P, GROUP_COLS], F32, name="n_sb")
            live[("zh", g)] = zh
            if g == 1:
                nc.vector.memset(zh[:, 0:1], 0.0)
            nc.gpsimd.tensor_tensor(out=zh[:], in0=live[("z", g)][:], in1=live[("h", g)][:], op=ALU.mult)

        def weigh(g, tiles):
            z_sb = live[("z", g)]
            n_sb = live[("n", g)]
            for t in tiles:
                cols = columns(t)
                nc.vector.scalar_tensor_tensor(
                    out=n_sb[:, cols], in0=z_sb[:, cols], scalar=1.0, in1=n_sb[:, cols],
                    op0=ALU.subtract, op1=ALU.mult,
                )
                roots_behind(g + 1, "weigh", t)
                if on_tensor(g, t):
                    blend_on_tensor(g, t)

        def on_tensor(g, t):
            return g == LAST - 1 and t in TENSOR_BLENDS

        def store(g, source, cols):
            first_col = g * GROUP_COLS + cols.start
            nc.sync.dma_start(
                out=out_rows[:, first_col : first_col + cols.stop - cols.start], in_=source[:, cols]
            )

        def blend_on_tensor(g, t):
            cols = columns(t)
            bank = new_bank()
            nc.tensor.matmul(out=bank[:], lhsT=identity[:], rhs=live[("zh", g)][:, cols], start=True, stop=False)
            nc.tensor.matmul(out=bank[:], lhsT=minus_identity[:], rhs=live[("n", g)][:, cols], start=False, stop=True)
            live[("blend", g, t)] = bank

        def store_from_tensor(g, t):
            cols = columns(t)
            n_sb = live[("n", g)]
            nc.scalar.copy(out=n_sb[:, cols], in_=live[("blend", g, t)][:])
            store(g, n_sb, cols)

        def blend(g, tiles):
            n_sb = live[("n", g)]
            zh = live[("zh", g)]
            for t in tiles:
                if on_tensor(g, t):
                    continue
                cols = columns(t)
                nc.vector.tensor_tensor(out=zh[:, cols], in0=zh[:, cols], in1=n_sb[:, cols], op=ALU.subtract)
                if g >= LAST - 1:
                    store(g, zh, cols)
                elif t % 2 == 1:
                    store(g, zh, slice((t - 1) * H, (t + 1) * H))
                roots_behind(g + 1, "blend", t)

        on_vector = nc.vector.tensor_copy
        on_scalar = nc.scalar.copy
        bias_wide = {}
        transpose_weight("h", (on_vector, on_scalar))
        transpose_operand("h", 0, (on_vector, on_scalar))
        quantise_weight("h")
        quantise_operand("h", 0)
        bank = new_bank()
        nc.tensor.matmul(out=bank[:], lhsT=ones[:, 0:P], rhs=bias_rows[:, H : 2 * H], start=True, stop=True)
        bias_wide["h"] = const.tile([P, H], F32, name="bias2")
        bias_total = const.tile([P, 1], F32)
        mean_share = const.tile([P, 1], F32)
        nc.scalar.activation(
            out=bias_wide["h"][:], in_=bank[:], func=ACT.Copy, scale=1.0, accum_out=bias_total[:]
        )
        nc.scalar.mul(out=mean_share[:], in_=bias_total[:], mul=-1.0 / (H * P))
        transpose_weight("x", (on_scalar, on_vector))
        quantise_weight("x")
        transpose_operand("x", 0)
        new_moments(0)
        for t in range(GROUP_TILES):
            row_product("h", 0, t)
        bank = psum_sums.tile([P, H], F32, tag="s")
        nc.tensor.matmul(out=bank[:], lhsT=ones[:, 0:P], rhs=bias_rows[:, 0:H], start=True, stop=True)
        bias_wide["x"] = const.tile([P, H], F32, name="bias1")
        nc.scalar.copy(out=bias_wide["x"][:], in_=bank[:])
        for t in range(GROUP_TILES):
            row_moments("h", 0, t)
            if t == 1:
                quantise_operand("x", 0)
        bank = psum_sums.tile([P, H], F32, tag="s")
        for c in range(OUT_BLOCKS):
            nc.tensor.matmul(
                out=bank[:, c : c + 1], lhsT=bias_rows[:, H + c * P : H + (c + 1) * P], rhs=ones[:, 0:1],
                start=True, stop=True,
            )
        bias_cols = const.tile([P, OUT_BLOCKS], F32)
        nc.scalar.copy(out=bias_cols[:], in_=bank[:, 0:OUT_BLOCKS])
        for t in range(GROUP_TILES):
            row_product("x", 0, t)
        row_means(0)

        def row_window(g):
            new_moments(g)
            for t in range(GROUP_TILES):
                if t < TURNED_FROM[g]:
                    row_moments("h", g, t)
                if t + 2 < TURNED_FROM[g]:
                    row_product("h", g, t + 2)
                row_moments("x", g, t)
                if t < 2:
                    row_product("x", g, t + 2)
                if t + 1 == TURNED_FROM[g]:
                    row_means(g)
                if t >= TURNED_FROM[g]:
                    turned_moments(g, t)

        def window(g):
            new_moments(g)
            for t in range(GROUP_TILES):
                row_moments("x", g, t)
                turned_moments(g, t)
                if t == 0:
                    turn_back(g, 3)

        def load_step(s):
            if s + 2 < GROUPS:
                load_activations(s + 2)
            if s < GROUPS:
                load_gate("r", s)
                load_gate("z", s)

        load_step(1)
        gate_product(0)
        for t in range(GROUP_TILES):
            row_moments("x", 0, t)
        transpose_operand("h", 1, (on_vector, on_vector))
        transpose_operand("x", 1)
        variance(0)
        plan_roots(0)
        quantise_operand("h", 1)
        turned_product(1)
        for t in range(2):
            row_product("h", 1, t)
        for t in range(GROUP_TILES):
            reset_row(0, t)
            if t == 1:
                quantise_operand("x", 1)
            if t > 0:
                take_steps("steps", 0, 1)
        turned_sums(1)
        for t in range(2):
            row_product("x", 1, t)
        for t in range(TURNED_FROM[1], GROUP_TILES):
            turn_back(1, t)
        turned_means(1)
        transpose_operand("h", 2)
        transpose_operand("x", 2)
        for s in range(2, GROUPS + 2):
            a = s - 1
            b = s - 2
            load_step(s)
            if a < GROUPS:
                gate_product(a)
                if a == 1:
                    row_window(a)
                else:
                    window(a)
            if s == 2:
                quantise_operand("h", 2)
                quantise_operand("x", 2)
            if s < GROUPS:
                turned_sums(s)
            for t in range(GROUP_TILES):
                combine(b, t)
                squash(b, t)
                if a < GROUPS and t == (3 if a == LAST else 0):
                    variance(a)
                    plan_roots(a)
                elif t < 3:
                    take_steps("scalar steps", a, 1)
            if b == LAST:
                for t in TENSOR_BLENDS:
                    store_from_tensor(LAST - 1, t)
            if a == 1:
                for t in range(TURNED_FROM[1]):
                    reset_row(1, t)
            weigh(b, (0,))
            if s + 1 < GROUPS:
                transpose_operand("h", s + 1)
            early = (1,) if a == LAST - 1 else (1, 2)
            weigh(b, early)
            take_steps("scalar steps", a, 1)
            if s + 1 < GROUPS:
                transpose_operand("x", s + 1)
            weigh(b, range(1 + len(early), GROUP_TILES))
            if s + 1 < GROUPS:
                quantise_operand("h", s + 1)
            roots_behind(a, "quantise h")
            blend(b, (0,))
            if s + 1 < GROUPS:
                quantise_operand("x", s + 1)
            roots_behind(a, "quantise x")
            if s < GROUPS:
                turned_product(s)
                for t in range(GROUP_TILES):
                    row_product("x", s, t)
                for t in range(3):
                    turn_back(s, t)
                turned_means(s)
            blend(b, (1, 2, 3))
